import numpy as np
import ml_dtypes


def mxq(x, axis, fmt="e4m3"):
    dtype, down = {"e4m3": (ml_dtypes.float8_e4m3fn, 7), "e5m2": (ml_dtypes.float8_e5m2, 14)}[fmt]
    v = np.moveaxis(np.asarray(x, np.float32).astype(ml_dtypes.bfloat16).astype(np.float64), axis, -1)
    blocks = v.reshape(v.shape[:-1] + (-1, 32))
    amax = np.abs(blocks).max(-1, keepdims=True)
    byte = np.maximum(np.where(amax > 0, np.frexp(amax)[1] - 1 + 127, 0) - down, 1)
    scale = np.exp2(byte - 127.0)
    codes = (blocks / scale).astype(np.float32).astype(dtype).astype(np.float64)
    return np.moveaxis((codes * scale).reshape(v.shape), -1, axis)


WIDE = False


def mx_kscale(k):
    if not WIDE:
        return np.ones(k)
    levels = np.array([10, -10, 5, -5, 0])
    if k % 512:
        return np.exp2(np.random.permutation(np.resize(levels, k // 32))).repeat(32)
    a = np.empty((k // 512, 16))
    for p in range(k // 512):
        a[p, :8] = np.random.permutation(np.resize(levels, 8))
        for g in range(8):
            far = levels[np.abs(levels - a[p, g]) >= 10]
            a[p, g + 8] = far[np.random.randint(len(far))]
    return np.exp2(a.ravel()).repeat(32)


BF16 = ml_dtypes.bfloat16


def bf(x):
    return np.asarray(x, np.float32).astype(BF16)


def f64(x):
    return np.asarray(x).astype(np.float64)


E2M1 = np.array([0.0, 0.5, 1.0, 1.5, 2.0, 3.0, 4.0, 6.0, -0.0, -0.5, -1.0, -1.5, -2.0, -3.0, -4.0, -6.0])


def pack_weight(w, fmt):
    k, n = w.shape
    w = f64(bf(w)).reshape(k // 32, 32, n)
    amax = np.abs(w).max(1)
    if fmt == "e4m3":
        byte = np.frexp(amax)[1] - 1 + 127 - 7
    else:
        mant, ex = np.frexp(amax / 6.0)
        byte = np.where(mant > 0.5, ex, ex - 1) + 127
    byte = np.clip(np.where(amax > 0, byte, 1), 1, 254)
    scaled = (w * np.exp2(127.0 - byte)[:, None, :]).reshape(k, n).astype(np.float32)
    by_word = np.ascontiguousarray(scaled.reshape(k // 512, 128, 4, n).transpose(0, 1, 3, 2))
    if fmt == "e4m3":
        words = by_word.astype(ml_dtypes.float8_e4m3fn).view(np.uint8)
    else:
        c = by_word.astype(ml_dtypes.float4_e2m1fn).view(np.uint8) & 0xF
        words = c[..., 0::2] | (c[..., 1::2] << 4)
    return np.ascontiguousarray(words), np.ascontiguousarray(byte.astype(np.uint8).reshape(k // 512, 16, n))


def unpack_weight(words, scales, fmt):
    g, p, n, _ = words.shape
    if fmt == "e4m3":
        vals = np.ascontiguousarray(words).view(ml_dtypes.float8_e4m3fn).astype(np.float64)
    else:
        nib = np.empty((g, p, n, 4), np.uint8)
        nib[..., 0::2] = words & 0xF
        nib[..., 1::2] = words >> 4
        vals = E2M1[nib]
    vals = vals * np.repeat(np.exp2(scales.astype(np.float64) - 127.0), 8, axis=1)[..., None]
    return vals.transpose(0, 1, 3, 2).reshape(g * 512, n)
def pack4(w):
    words, scales = pack_weight(w, "e2m1")
    return words.reshape(words.shape[0], 128, -1), scales


def unpack4(words, scales):
    return unpack_weight(words.reshape(words.shape[0], 128, -1, 2), scales, "e2m1")


B_, S, D_IN, D_OUT, N, RANK, ALPHA = 4, 2048, 512, 256, 32, 16, 32
NR = N * RANK
SCALE = ALPHA / RANK


def draw0():
    s, t = mx_kscale(D_IN), mx_kscale(NR)
    tn = t.reshape(N, RANK)
    x = bf(np.random.standard_normal((B_, S, D_IN)) * s)
    lora_A = bf(np.random.standard_normal((N, RANK, D_IN)) / np.sqrt(D_IN) / s * tn[:, :, None])
    lora_B = bf(np.random.standard_normal((N, D_OUT, RANK)) / np.sqrt(RANK) / tn[:, None, :])
    W_words, W_scales = pack4((np.random.standard_normal((D_OUT, D_IN)) / np.sqrt(D_IN) / s).T)
    return {"x": x,
            "lora_A": lora_A,
            "lora_B": lora_B,
            "W_words": W_words,
            "W_scales": W_scales,
            "bias": bf(np.random.standard_normal(D_OUT) * 0.3),
            "lora_weights": bf((1.0 + 0.5 * np.random.standard_normal(N)) * 2.0 / N)}


def core(x, lora_A, lora_B, W_words, W_scales, bias, lora_weights):
    xq = mxq(f64(x), 2, "e4m3")
    h = xq @ mxq(f64(lora_A).reshape(NR, D_IN), 1, "e4m3").T
    coef = (SCALE * f64(lora_weights))[:, None, None]
    bc = (f64(lora_B) * coef).transpose(1, 0, 2).reshape(D_OUT, NR)
    lora_out = mxq(h, 2, "e4m3") @ mxq(bc, 1, "e4m3").T
    base = (xq @ unpack4(W_words, W_scales)) + f64(bias)
    return base + lora_out


def e4m3fn_bytes(y):
    return np.clip(np.asarray(y, np.float64), -448.0, 448.0).astype(np.float32).astype(ml_dtypes.float8_e4m3fn).view(np.uint8)


def e4m3fn_values(b):
    return np.asarray(b, np.uint8).view(ml_dtypes.float8_e4m3fn).astype(np.float64)


def setup_inputs():
    d = draw0()
    x0 = np.asarray(d['x']).astype(np.float64)
    s = (np.max(np.abs(x0), axis=(0, 1), keepdims=True) / 448.0).astype(np.float32)
    out = {}
    for k, v in d.items():
        if k == 'x':
            out['x_bytes'] = e4m3fn_bytes(x0 / s.astype(np.float64))
            out['x_scale'] = s
        else:
            out[k] = v
    return out


def reference(x_bytes, x_scale, lora_A, lora_B, W_words, W_scales, bias, lora_weights):
    return core(e4m3fn_values(x_bytes) * x_scale.astype(np.float64), lora_A, lora_B, W_words, W_scales, bias, lora_weights)

@@ -1,0 +1,243 @@
+from contextlib import ExitStack
+
+import concourse.mybir as mybir
+from concourse.masks import make_identity
+
+TOKENS, D, NR, D_OUT = 8192, 512, 512, 256
+FLOPS = 2 * TOKENS * (D * NR + D * D_OUT + NR * D_OUT)
+
+F32 = mybir.dt.float32
+BF16 = mybir.dt.bfloat16
+U32 = mybir.dt.uint32
+I32 = mybir.dt.int32
+U8 = mybir.dt.uint8
+FP8 = mybir.dt.float8_e4m3fn
+FP8X4 = mybir.dt.float8_e4m3fn_x4
+FP4X4 = mybir.dt.float4_e2m1fn_x4
+ALU = mybir.AluOpType
+ACT = mybir.ActivationFunctionType
+
+P = 128
+PER = 8
+CHUNKS = TOKENS // (P * PER)
+PAIRS = TOKENS // (2 * P)
+PPC = PER // 2
+
+
+def tile_replaced_compose_lora_pa_t_w4_kernel(
+    tc, x_bytes, x_scale, lora_A, lora_B, W_words, W_scales, bias, lora_weights, out
+):
+    nc = tc.nc
+    x_rows = x_bytes.rearrange("b s d -> (b s) d").rearrange("(c p n) d -> c p (n d)", p=P, n=PER)
+    out_rows = out.rearrange("b s o -> (b s) o").rearrange("(c p n) o -> c p n o", p=P, n=PER)
+
+    with ExitStack() as ctx:
+        keep = ctx.enter_context(tc.tile_pool(name="keep", bufs=1))
+        work = ctx.enter_context(tc.tile_pool(name="work", bufs=1))
+        psum = ctx.enter_context(tc.psum_pool(name="psum", bufs=1))
+        ctx.enter_context(tc.manual_schedule())
+
+        ident = keep.tile([P, P], F32, name="ident")
+        make_identity(nc, ident[:])
+
+        xb = [keep.tile([P, PER * D], U8, name="xb%d" % c, align_bytes=64) for c in range(CHUNKS)]
+        scale = keep.tile([P, 2 * D], F32, name="scale", align_bytes=64)
+        a_sb = keep.tile([P, 4 * D], BF16, name="a_sb", align_bytes=64)
+        b_sb = keep.tile([P, 2, 32, 16], BF16, name="b_sb", align_bytes=64)
+        w_sb = keep.tile([P, 2 * D_OUT], U8, name="w_sb", align_bytes=64)
+        w_sc = keep.tile([P, D_OUT], U8, name="w_sc", align_bytes=64)
+        bias_sb = keep.tile([P, D_OUT], BF16, name="bias_sb", align_bytes=64)
+        lw_sb = keep.tile([P, 32], BF16, name="lw_sb", align_bytes=64)
+        coef = keep.tile([P, 1], F32, name="coef")
+        junk = keep.tile([P, P], F32, name="junk")
+        warm = keep.tile([P, 1], F32, name="warm")
+
+        nc.vector.memset(w_sc[:].bitcast(I32), 0)
+        nc.vector.memset(warm[:], 0.0)
+        nc.scalar.dma_start(out=scale[:, 0:D], in_=x_scale.rearrange("a b k -> (a b k)").partition_broadcast(P))
+        nc.sync.dma_start(out=xb[0][:, 0 : 2 * D], in_=x_rows[0][:, 0 : 2 * D])
+        nc.sync.dma_start(out=a_sb[:], in_=lora_A.rearrange("n r d -> (n r) d").rearrange("(m t) d -> m (t d)", t=4))
+        nc.scalar.dma_start(out=lw_sb[:], in_=lora_weights.partition_broadcast(P))
+        for h in range(2):
+            nc.scalar.dma_start(out=b_sb[:, h], in_=lora_B[:, h * P : (h + 1) * P, :].rearrange("n o r -> o n r"))
+        nc.scalar.dma_start(out=bias_sb[:], in_=bias.partition_broadcast(P))
+        for q in range(1, PPC):
+            nc.sync.dma_start(out=xb[0][:, q * 2 * D : (q + 1) * 2 * D], in_=x_rows[0][:, q * 2 * D : (q + 1) * 2 * D])
+        nc.sync.dma_start(out=w_sb[:], in_=W_words[0])
+        for q in range(4):
+            nc.sync.dma_start(
+                out=w_sc[32 * q : 32 * q + 4, :].bitcast(I32), in_=W_scales[0, 4 * q : 4 * q + 4, :].bitcast(I32)
+            )
+        for c in range(1, CHUNKS):
+            nc.sync.dma_start(out=xb[c][:], in_=x_rows[c])
+
+        nc.scalar.activation(out=warm[:], in_=warm[:], func=ACT.Copy, scale=1.0)
+
+        a_codes = keep.tile([P, NR], U32, name="a_codes", align_bytes=64)
+        a_scales = keep.tile([P, NR], U8, name="a_scales", align_bytes=64)
+        b_codes = keep.tile([P, D_OUT], U32, name="b_codes", align_bytes=64)
+        b_scales = keep.tile([P, D_OUT], U8, name="b_scales", align_bytes=64)
+        a_grp = keep.tile([P, 4 * NR], BF16, name="a_grp", align_bytes=64)
+        b_grp = keep.tile([P, 4 * D_OUT], BF16, name="b_grp", align_bytes=64)
+
+        def turn(rows):
+            words = rows.bitcast(F32)
+            xt = psum.tile([P, 2, 2, P], F32, name="xt", tag="xt", bufs=2)
+            for j in range(2):
+                for u in range(2):
+                    nc.tensor.transpose(xt[:, j, u, :], words[:, 256 * j + u : 256 * (j + 1) : 2], ident[:])
+            return xt
+
+        def empty_turned(xt, dst):
+            nc.scalar.copy(
+                out=dst.bitcast(F32).rearrange("p (j r u) -> p j r u", j=2, u=2),
+                in_=xt[:].rearrange("p j u r -> p j r u"),
+            )
+
+        st = {}
+
+        def widen(i):
+            c, q = divmod(i, PPC)
+            xw = work.tile([P, 2 * D], BF16, name="xw", tag="xw", bufs=4, align_bytes=64)
+            nc.vector.tensor_tensor(
+                out=xw[:],
+                in0=xb[c][:, q * 2 * D : (q + 1) * 2 * D].bitcast(FP8),
+                in1=scale[:],
+                op=ALU.mult,
+            )
+            st["xw", i] = xw
+
+        def t_stage(i):
+            st["xt", i] = turn(st.pop(("xw", i))[:])
+
+        def e_stage(i):
+            xg = work.tile([P, 2 * D], BF16, name="xg", tag="xg", bufs=3, align_bytes=64)
+            empty_turned(st.pop(("xt", i)), xg[:])
+            st["xg", i] = xg
+
+        def qx_stage(i):
+            xg = st.pop(("xg", i))
+            xc = work.tile([P, 2 * P], U32, name="xc", tag="xc", bufs=6, align_bytes=64)
+            xs = work.tile([P, 2 * P], U8, name="xs", tag="xs", bufs=6, align_bytes=64)
+            nc.vector.quantize_mx(out=xc[:].bitcast(FP8X4), scales=xs[:], in_=xg[:])
+            st["xc", i] = (xc, xs)
+
+        def h_stage(i):
+            xc, xs = st["xc", i]
+            hp = []
+            for j in range(2):
+                h = psum.tile([P, 4, P], F32, name="hp", tag="hp", bufs=4)
+                cols = slice(j * P, (j + 1) * P)
+                for t in range(4):
+                    ch = slice(t * P, (t + 1) * P)
+                    nc.tensor.matmul_mx(
+                        out=h[:, t, :],
+                        lhsT=a_codes[:, ch].bitcast(FP8X4),
+                        lhsT_scale=a_scales[:, ch],
+                        rhs=xc[:, cols].bitcast(FP8X4),
+                        rhs_scale=xs[:, cols],
+                        start=True,
+                        stop=True,
+                    )
+                hp.append(h)
+            st["hp", i] = hp
+
+        def eh_stage(i):
+            hp = st.pop(("hp", i))
+            hg = work.tile([P, 2 * NR], BF16, name="hg", tag="hg", bufs=3, align_bytes=64)
+            for j in range(2):
+                nc.scalar.copy(
+                    out=hg[:, j * NR : (j + 1) * NR].rearrange("p (r t) -> p r t", t=4),
+                    in_=hp[j][:].rearrange("p t r -> p r t"),
+                )
+            st["hg", i] = hg
+
+        def qh_stage(i):
+            hg = st.pop(("hg", i))
+            hc = work.tile([P, 2 * P], U32, name="hc", tag="hc", bufs=3, align_bytes=64)
+            hs = work.tile([P, 2 * P], U8, name="hs", tag="hs", bufs=3, align_bytes=64)
+            nc.vector.quantize_mx(out=hc[:].bitcast(FP8X4), scales=hs[:], in_=hg[:])
+            st["hc", i] = (hc, hs)
+
+        def o_stage(i):
+            xc, xs = st.pop(("xc", i))
+            hc, hs = st.pop(("hc", i))
+            op = psum.tile([P, 2, D_OUT], F32, name="op", tag="op", bufs=2)
+            for j in range(2):
+                cols = slice(j * P, (j + 1) * P)
+                for half in range(2):
+                    oc = slice(half * P, (half + 1) * P)
+                    nc.tensor.matmul_mx(
+                        out=op[:, j, oc],
+                        lhsT=xc[:, cols].bitcast(FP8X4),
+                        lhsT_scale=xs[:, cols],
+                        rhs=w_sb[:, half * 256 : (half + 1) * 256].bitcast(FP4X4),
+                        rhs_scale=w_sc[:, oc],
+                        start=True,
+                        stop=False,
+                    )
+                    nc.tensor.matmul_mx(
+                        out=op[:, j, oc],
+                        lhsT=hc[:, cols].bitcast(FP8X4),
+                        lhsT_scale=hs[:, cols],
+                        rhs=b_codes[:, oc].bitcast(FP8X4),
+                        rhs_scale=b_scales[:, oc],
+                        start=False,
+                        stop=True,
+                    )
+            st["op", i] = op
+
+        def out_stage(i):
+            c, q = divmod(i, PPC)
+            op = st.pop(("op", i))
+            ob = work.tile([P, 2, D_OUT], F32, name="ob", tag="ob", bufs=4, align_bytes=64)
+            nc.vector.tensor_tensor(
+                out=ob[:], in0=op[:], in1=bias_sb[:].unsqueeze(1).to_broadcast([P, 2, D_OUT]), op=ALU.add
+            )
+            nc.sync.dma_start(out=out_rows[c][:, 2 * q : 2 * q + 2, :], in_=ob[:])
+
+        nc.scalar.copy(out=scale[:, D : 2 * D], in_=scale[:, 0:D])
+        widen(0)
+        a_t = [turn(a_sb[:, h * 2 * D : (h + 1) * 2 * D]) for h in range(2)]
+        for h in range(2):
+            empty_turned(a_t[h], a_grp[:, h * 2 * D : (h + 1) * 2 * D])
+        nc.vector.scalar_tensor_tensor(
+            out=junk[:].rearrange("p (n q) -> p n q", q=4),
+            in0=ident[:].rearrange("p (n q) -> p n q", q=4),
+            scalar=2.0,
+            in1=lw_sb[:].unsqueeze(2).to_broadcast([P, 32, 4]),
+            op0=ALU.mult,
+            op1=ALU.mult,
+            accum_out=coef[:],
+        )
+
+        for s in range(PAIRS + 5):
+            if s + 1 < PAIRS:
+                widen(s + 1)
+            if s == 0:
+                nc.vector.quantize_mx(out=a_codes[:].bitcast(FP8X4), scales=a_scales[:], in_=a_grp[:])
+            if 0 <= s - 1 < PAIRS:
+                qx_stage(s - 1)
+            if 0 <= s - 5 < PAIRS:
+                out_stage(s - 5)
+            if 0 <= s - 3 < PAIRS:
+                qh_stage(s - 3)
+            if s == 2:
+                nc.vector.quantize_mx(out=b_codes[:].bitcast(FP8X4), scales=b_scales[:], in_=b_grp[:])
+            if s < PAIRS:
+                t_stage(s)
+                e_stage(s)
+            if 0 <= s - 2 < PAIRS:
+                h_stage(s - 2)
+                eh_stage(s - 2)
+            if s == 1:
+                b_t = turn(b_sb[:].rearrange("p h n r -> p (h n r)"))
+                for h in range(2):
+                    nc.scalar.activation(
+                        out=b_grp[:, h * 2 * D_OUT : (h + 1) * 2 * D_OUT].rearrange("p (r u e) -> p r u e", u=2, e=2),
+                        in_=b_t[:, h].bitcast(BF16).rearrange("p u (r e) -> p r u e", e=2),
+                        func=ACT.Copy,
+                        scale=coef[:],
+                    )
+            if 0 <= s - 4 < PAIRS:
+                o_stage(s - 4)

@@ -22,6 +22,7 @@ PER = 8
 CHUNKS = TOKENS // (P * PER)
 PAIRS = TOKENS // (2 * P)
 PPC = PER // 2
+TURNED = ()
 
 
 def tile_replaced_compose_lora_pa_t_w4_kernel(
@@ -41,37 +42,42 @@ def tile_replaced_compose_lora_pa_t_w4_kernel(
         make_identity(nc, ident[:])
 
         xb = [keep.tile([P, PER * D], U8, name="xb%d" % c, align_bytes=64) for c in range(CHUNKS)]
+        scale_col = keep.tile([P, 4], F32, name="scale_col")
         scale = keep.tile([P, 2 * D], F32, name="scale", align_bytes=64)
         a_sb = keep.tile([P, 4 * D], BF16, name="a_sb", align_bytes=64)
-        b_sb = keep.tile([P, 2, 32, 16], BF16, name="b_sb", align_bytes=64)
+        b_sb = keep.tile([P, D_OUT, 16], BF16, name="b_sb", align_bytes=64)
         w_sb = keep.tile([P, 2 * D_OUT], U8, name="w_sb", align_bytes=64)
         w_sc = keep.tile([P, D_OUT], U8, name="w_sc", align_bytes=64)
         bias_sb = keep.tile([P, D_OUT], BF16, name="bias_sb", align_bytes=64)
+        bias_col = keep.tile([P, 2, 16], BF16, name="bias_col", align_bytes=64)
         lw_sb = keep.tile([P, 32], BF16, name="lw_sb", align_bytes=64)
         coef = keep.tile([P, 1], F32, name="coef")
-        junk = keep.tile([P, P], F32, name="junk")
-        warm = keep.tile([P, 1], F32, name="warm")
+        spread = keep.tile([P, P], F32, name="spread")
 
         nc.vector.memset(w_sc[:].bitcast(I32), 0)
-        nc.vector.memset(warm[:], 0.0)
-        nc.scalar.dma_start(out=scale[:, 0:D], in_=x_scale.rearrange("a b k -> (a b k)").partition_broadcast(P))
+        nc.sync.dma_start(out=scale_col[:], in_=x_scale.rearrange("a b (p t) -> p (a b t)", t=4))
+        nc.sync.dma_start(out=lw_sb[:], in_=lora_weights.partition_broadcast(P))
         nc.sync.dma_start(out=xb[0][:, 0 : 2 * D], in_=x_rows[0][:, 0 : 2 * D])
         nc.sync.dma_start(out=a_sb[:], in_=lora_A.rearrange("n r d -> (n r) d").rearrange("(m t) d -> m (t d)", t=4))
-        nc.scalar.dma_start(out=lw_sb[:], in_=lora_weights.partition_broadcast(P))
-        for h in range(2):
-            nc.scalar.dma_start(out=b_sb[:, h], in_=lora_B[:, h * P : (h + 1) * P, :].rearrange("n o r -> o n r"))
-        nc.scalar.dma_start(out=bias_sb[:], in_=bias.partition_broadcast(P))
-        for q in range(1, PPC):
-            nc.sync.dma_start(out=xb[0][:, q * 2 * D : (q + 1) * 2 * D], in_=x_rows[0][:, q * 2 * D : (q + 1) * 2 * D])
+        nc.sync.dma_start(out=xb[0][:, 2 * D :], in_=x_rows[0][:, 2 * D :])
+        b_rows = lora_B.rearrange("n o r -> n (o r)")
+        b_run = 16 * D_OUT - 12
+        for q in range(4):
+            nc.sync.dma_start(
+                out=b_sb[:].rearrange("p o r -> p (o r)")[q:P:4, 0:b_run], in_=b_rows[:, 4 * q : 4 * q + b_run]
+            )
+        nc.sync.dma_start(out=xb[1][:], in_=x_rows[1])
         nc.sync.dma_start(out=w_sb[:], in_=W_words[0])
         for q in range(4):
             nc.sync.dma_start(
                 out=w_sc[32 * q : 32 * q + 4, :].bitcast(I32), in_=W_scales[0, 4 * q : 4 * q + 4, :].bitcast(I32)
             )
-        for c in range(1, CHUNKS):
+        nc.sync.dma_start(out=bias_sb[:], in_=bias.partition_broadcast(P))
+        if TURNED:
+            for h in range(2):
+                nc.sync.dma_start(out=bias_col[:, h, 0:1], in_=bias[h * P : (h + 1) * P].unsqueeze(1))
+        for c in range(2, CHUNKS):
             nc.sync.dma_start(out=xb[c][:], in_=x_rows[c])
-
-        nc.scalar.activation(out=warm[:], in_=warm[:], func=ACT.Copy, scale=1.0)
 
         a_codes = keep.tile([P, NR], U32, name="a_codes", align_bytes=64)
         a_scales = keep.tile([P, NR], U8, name="a_scales", align_bytes=64)
@@ -82,7 +88,7 @@ def tile_replaced_compose_lora_pa_t_w4_kernel(
 
         def turn(rows):
             words = rows.bitcast(F32)
-            xt = psum.tile([P, 2, 2, P], F32, name="xt", tag="xt", bufs=2)
+            xt = psum.tile([P, 2, 2, P], F32, name="xt", tag="tr", bufs=2)
             for j in range(2):
                 for u in range(2):
                     nc.tensor.transpose(xt[:, j, u, :], words[:, 256 * j + u : 256 * (j + 1) : 2], ident[:])
@@ -96,34 +102,41 @@ def tile_replaced_compose_lora_pa_t_w4_kernel(
 
         st = {}
 
-        def widen(i):
+        def group(s):
+            if ("g", s) not in st:
+                st["g", s] = work.tile([P, 4 * D], BF16, name="grp", tag="grp", bufs=4, align_bytes=64)
+            return st["g", s]
+
+        def widen(i, parts=1):
             c, q = divmod(i, PPC)
             xw = work.tile([P, 2 * D], BF16, name="xw", tag="xw", bufs=4, align_bytes=64)
-            nc.vector.tensor_tensor(
-                out=xw[:],
-                in0=xb[c][:, q * 2 * D : (q + 1) * 2 * D].bitcast(FP8),
-                in1=scale[:],
-                op=ALU.mult,
-            )
+            width = 2 * D // parts
+            for k in range(parts):
+                nc.vector.tensor_tensor(
+                    out=xw[:, k * width : (k + 1) * width],
+                    in0=xb[c][:, q * 2 * D + k * width : q * 2 * D + (k + 1) * width].bitcast(FP8),
+                    in1=scale[:, 0:width],
+                    op=ALU.mult,
+                )
             st["xw", i] = xw
 
         def t_stage(i):
             st["xt", i] = turn(st.pop(("xw", i))[:])
 
         def e_stage(i):
-            xg = work.tile([P, 2 * D], BF16, name="xg", tag="xg", bufs=3, align_bytes=64)
-            empty_turned(st.pop(("xt", i)), xg[:])
-            st["xg", i] = xg
+            empty_turned(st.pop(("xt", i)), group(i)[:, 0 : 2 * D])
 
-        def qx_stage(i):
-            xg = st.pop(("xg", i))
-            xc = work.tile([P, 2 * P], U32, name="xc", tag="xc", bufs=6, align_bytes=64)
-            xs = work.tile([P, 2 * P], U8, name="xs", tag="xs", bufs=6, align_bytes=64)
-            nc.vector.quantize_mx(out=xc[:].bitcast(FP8X4), scales=xs[:], in_=xg[:])
-            st["xc", i] = (xc, xs)
+        def q_stage(s):
+            g = st.pop(("g", s))
+            cd = work.tile([P, 4 * P], U32, name="cd", tag="cd", bufs=5, align_bytes=64)
+            sc = work.tile([P, 4 * P], U8, name="sc", tag="sc", bufs=5, align_bytes=64)
+            lo = 0 if s < PAIRS else 2 * P
+            hi = 4 * P if s >= 2 else 2 * P
+            nc.vector.quantize_mx(out=cd[:, lo:hi].bitcast(FP8X4), scales=sc[:, lo:hi], in_=g[:, 4 * lo : 4 * hi])
+            st["cd", s] = (cd, sc)
 
         def h_stage(i):
-            xc, xs = st["xc", i]
+            cd, sc = st["cd", i]
             hp = []
             for j in range(2):
                 h = psum.tile([P, 4, P], F32, name="hp", tag="hp", bufs=4)
@@ -134,8 +147,8 @@ def tile_replaced_compose_lora_pa_t_w4_kernel(
                         out=h[:, t, :],
                         lhsT=a_codes[:, ch].bitcast(FP8X4),
                         lhsT_scale=a_scales[:, ch],
-                        rhs=xc[:, cols].bitcast(FP8X4),
-                        rhs_scale=xs[:, cols],
+                        rhs=cd[:, cols].bitcast(FP8X4),
+                        rhs_scale=sc[:, cols],
                         start=True,
                         stop=True,
                     )
@@ -144,65 +157,106 @@ def tile_replaced_compose_lora_pa_t_w4_kernel(
 
         def eh_stage(i):
             hp = st.pop(("hp", i))
-            hg = work.tile([P, 2 * NR], BF16, name="hg", tag="hg", bufs=3, align_bytes=64)
+            g = group(i + 2)
             for j in range(2):
                 nc.scalar.copy(
-                    out=hg[:, j * NR : (j + 1) * NR].rearrange("p (r t) -> p r t", t=4),
+                    out=g[:, (2 + j) * NR : (3 + j) * NR].rearrange("p (r t) -> p r t", t=4),
                     in_=hp[j][:].rearrange("p t r -> p r t"),
                 )
-            st["hg", i] = hg
-
-        def qh_stage(i):
-            hg = st.pop(("hg", i))
-            hc = work.tile([P, 2 * P], U32, name="hc", tag="hc", bufs=3, align_bytes=64)
-            hs = work.tile([P, 2 * P], U8, name="hs", tag="hs", bufs=3, align_bytes=64)
-            nc.vector.quantize_mx(out=hc[:].bitcast(FP8X4), scales=hs[:], in_=hg[:])
-            st["hc", i] = (hc, hs)
 
         def o_stage(i):
-            xc, xs = st.pop(("xc", i))
-            hc, hs = st.pop(("hc", i))
+            xc, xs = st.pop(("cd", i))
+            hc, hs = st["cd", i + 2]
             op = psum.tile([P, 2, D_OUT], F32, name="op", tag="op", bufs=2)
             for j in range(2):
                 cols = slice(j * P, (j + 1) * P)
-                for half in range(2):
-                    oc = slice(half * P, (half + 1) * P)
+                hcols = slice((2 + j) * P, (3 + j) * P)
+                if i in TURNED:
                     nc.tensor.matmul_mx(
-                        out=op[:, j, oc],
-                        lhsT=xc[:, cols].bitcast(FP8X4),
-                        lhsT_scale=xs[:, cols],
-                        rhs=w_sb[:, half * 256 : (half + 1) * 256].bitcast(FP4X4),
-                        rhs_scale=w_sc[:, oc],
+                        out=op[:, j, :],
+                        lhsT=b_codes[:, cols].bitcast(FP8X4),
+                        lhsT_scale=b_scales[:, cols],
+                        rhs=hc[:, 2 * P :].bitcast(FP8X4),
+                        rhs_scale=hs[:, 2 * P :],
                         start=True,
                         stop=False,
                     )
+                else:
                     nc.tensor.matmul_mx(
-                        out=op[:, j, oc],
-                        lhsT=hc[:, cols].bitcast(FP8X4),
-                        lhsT_scale=hs[:, cols],
-                        rhs=b_codes[:, oc].bitcast(FP8X4),
-                        rhs_scale=b_scales[:, oc],
-                        start=False,
-                        stop=True,
+                        out=op[:, j, :],
+                        lhsT=hc[:, hcols].bitcast(FP8X4),
+                        lhsT_scale=hs[:, hcols],
+                        rhs=b_codes[:].bitcast(FP8X4),
+                        rhs_scale=b_scales[:],
+                        start=True,
+                        stop=False,
                     )
+                for half in range(2):
+                    oc = slice(half * P, (half + 1) * P)
+                    if i in TURNED:
+                        nc.tensor.matmul_mx(
+                            out=op[:, j, oc],
+                            lhsT=w_sb[:, j * 256 : (j + 1) * 256].bitcast(FP4X4),
+                            lhsT_scale=w_sc[:, cols],
+                            rhs=xc[:, oc].bitcast(FP8X4),
+                            rhs_scale=xs[:, oc],
+                            start=False,
+                            stop=(half == 1),
+                        )
+                    else:
+                        nc.tensor.matmul_mx(
+                            out=op[:, j, oc],
+                            lhsT=xc[:, cols].bitcast(FP8X4),
+                            lhsT_scale=xs[:, cols],
+                            rhs=w_sb[:, half * 256 : (half + 1) * 256].bitcast(FP4X4),
+                            rhs_scale=w_sc[:, oc],
+                            start=False,
+                            stop=(half == 1),
+                        )
             st["op", i] = op
 
-        def out_stage(i):
+        def store(i, ob):
             c, q = divmod(i, PPC)
+            nc.sync.dma_start(out=out_rows[c][:, 2 * q : 2 * q + 2, :], in_=ob[:])
+
+        def out_stage(i):
             op = st.pop(("op", i))
             ob = work.tile([P, 2, D_OUT], F32, name="ob", tag="ob", bufs=4, align_bytes=64)
             nc.vector.tensor_tensor(
                 out=ob[:], in0=op[:], in1=bias_sb[:].unsqueeze(1).to_broadcast([P, 2, D_OUT]), op=ALU.add
             )
-            nc.sync.dma_start(out=out_rows[c][:, 2 * q : 2 * q + 2, :], in_=ob[:])
+            store(i, ob)
 
-        nc.scalar.copy(out=scale[:, D : 2 * D], in_=scale[:, 0:D])
-        widen(0)
-        a_t = [turn(a_sb[:, h * 2 * D : (h + 1) * 2 * D]) for h in range(2)]
-        for h in range(2):
-            empty_turned(a_t[h], a_grp[:, h * 2 * D : (h + 1) * 2 * D])
+        def bias_stage(i):
+            op = st.pop(("op", i))
+            ot = work.tile([P, 2, 2 * P], F32, name="ot", tag="ot", bufs=2, align_bytes=64)
+            for h in range(2):
+                nc.scalar.activation(out=ot[:, h, :], in_=op[:, h, :], func=ACT.Identity, bias=bias_col[:, h, 0:1], scale=1.0)
+            st["ot", i] = ot
+
+        def back_stage(i):
+            ot = st.pop(("ot", i))
+            bk = psum.tile([P, 2, D_OUT], F32, name="bk", tag="tr", bufs=2)
+            for j in range(2):
+                for h in range(2):
+                    nc.tensor.transpose(bk[:, j, h * P : (h + 1) * P], ot[:, h, j * P : (j + 1) * P], ident[:])
+            st["bk", i] = bk
+
+        def back_out_stage(i):
+            bk = st.pop(("bk", i))
+            ob = work.tile([P, 2, D_OUT], F32, name="ob", tag="ob", bufs=4, align_bytes=64)
+            nc.scalar.copy(out=ob[:], in_=bk[:])
+            store(i, ob)
+
+        sp = psum.tile([P, 4, P], F32, name="sp", tag="op", bufs=2)
+        for t in range(4):
+            nc.tensor.transpose(sp[:, t, :], scale_col[:, t : t + 1].to_broadcast([P, P]), ident[:])
+        for k in range(2):
+            nc.scalar.copy(
+                out=scale[:, k * D : (k + 1) * D].rearrange("p (n t) -> p n t", t=4), in_=sp[:].rearrange("p t n -> p n t")
+            )
         nc.vector.scalar_tensor_tensor(
-            out=junk[:].rearrange("p (n q) -> p n q", q=4),
+            out=spread[:].rearrange("p (n q) -> p n q", q=4),
             in0=ident[:].rearrange("p (n q) -> p n q", q=4),
             scalar=2.0,
             in1=lw_sb[:].unsqueeze(2).to_broadcast([P, 32, 4]),
@@ -210,34 +264,46 @@ def tile_replaced_compose_lora_pa_t_w4_kernel(
             op1=ALU.mult,
             accum_out=coef[:],
         )
+        widen(0, parts=2)
+        widen(1)
+        for h in range(2):
+            empty_turned(turn(a_sb[:, h * 2 * D : (h + 1) * 2 * D]), a_grp[:, h * 2 * D : (h + 1) * 2 * D])
+        for i in range(2):
+            t_stage(i)
+            e_stage(i)
+        nc.vector.quantize_mx(out=a_codes[:].bitcast(FP8X4), scales=a_scales[:], in_=a_grp[:])
+        nc.scalar.activation(
+            out=b_grp[:].rearrange("p (o t) -> p o t", t=4), in_=b_sb[:, :, 0:4], func=ACT.Copy, scale=coef[:]
+        )
 
-        for s in range(PAIRS + 5):
-            if s + 1 < PAIRS:
-                widen(s + 1)
-            if s == 0:
-                nc.vector.quantize_mx(out=a_codes[:].bitcast(FP8X4), scales=a_scales[:], in_=a_grp[:])
-            if 0 <= s - 1 < PAIRS:
-                qx_stage(s - 1)
-            if 0 <= s - 5 < PAIRS:
-                out_stage(s - 5)
-            if 0 <= s - 3 < PAIRS:
-                qh_stage(s - 3)
-            if s == 2:
-                nc.vector.quantize_mx(out=b_codes[:].bitcast(FP8X4), scales=b_scales[:], in_=b_grp[:])
-            if s < PAIRS:
-                t_stage(s)
-                e_stage(s)
-            if 0 <= s - 2 < PAIRS:
-                h_stage(s - 2)
-                eh_stage(s - 2)
+        def lead(s):
+            return 3 if s < 12 else 2
+
+        done = 2
+        for s in range(PAIRS + 4):
+            fresh = range(done, min(PAIRS, s + lead(s) + 1))
+            done = max(done, fresh.stop)
+            if s < PAIRS + 2:
+                q_stage(s)
+            for i in fresh:
+                widen(i)
             if s == 1:
-                b_t = turn(b_sb[:].rearrange("p h n r -> p (h n r)"))
-                for h in range(2):
-                    nc.scalar.activation(
-                        out=b_grp[:, h * 2 * D_OUT : (h + 1) * 2 * D_OUT].rearrange("p (r u e) -> p r u e", u=2, e=2),
-                        in_=b_t[:, h].bitcast(BF16).rearrange("p u (r e) -> p r u e", e=2),
-                        func=ACT.Copy,
-                        scale=coef[:],
-                    )
-            if 0 <= s - 4 < PAIRS:
-                o_stage(s - 4)
+                nc.vector.quantize_mx(out=b_codes[:].bitcast(FP8X4), scales=b_scales[:], in_=b_grp[:])
+            if 0 <= s - 3 < PAIRS and s - 3 not in TURNED:
+                out_stage(s - 3)
+            if s < PAIRS:
+                h_stage(s)
+                eh_stage(s)
+            if 0 <= s - 2 < PAIRS:
+                o_stage(s - 2)
+                if s - 2 in TURNED:
+                    bias_stage(s - 2)
+            for i in fresh:
+                t_stage(i)
+                if i + 1 == fresh.stop and s - 3 in TURNED:
+                    back_stage(s - 3)
+                e_stage(i)
+            if s - 3 in TURNED:
+                if not fresh:
+                    back_stage(s - 3)
+                back_out_stage(s - 3)

@@ -22,7 +22,7 @@ PER = 8
 CHUNKS = TOKENS // (P * PER)
 PAIRS = TOKENS // (2 * P)
 PPC = PER // 2
-TURNED = ()
+TURNED = range(0, 27, 4)
 
 
 def tile_replaced_compose_lora_pa_t_w4_kernel(
@@ -86,9 +86,9 @@ def tile_replaced_compose_lora_pa_t_w4_kernel(
         a_grp = keep.tile([P, 4 * NR], BF16, name="a_grp", align_bytes=64)
         b_grp = keep.tile([P, 4 * D_OUT], BF16, name="b_grp", align_bytes=64)
 
-        def turn(rows):
+        def turn(rows, tag="tr", bufs=2):
             words = rows.bitcast(F32)
-            xt = psum.tile([P, 2, 2, P], F32, name="xt", tag="tr", bufs=2)
+            xt = psum.tile([P, 2, 2, P], F32, name="xt", tag=tag, bufs=bufs)
             for j in range(2):
                 for u in range(2):
                     nc.tensor.transpose(xt[:, j, u, :], words[:, 256 * j + u : 256 * (j + 1) : 2], ident[:])
@@ -126,14 +126,14 @@ def tile_replaced_compose_lora_pa_t_w4_kernel(
         def e_stage(i):
             empty_turned(st.pop(("xt", i)), group(i)[:, 0 : 2 * D])
 
-        def q_stage(s):
-            g = st.pop(("g", s))
-            cd = work.tile([P, 4 * P], U32, name="cd", tag="cd", bufs=5, align_bytes=64)
-            sc = work.tile([P, 4 * P], U8, name="sc", tag="sc", bufs=5, align_bytes=64)
-            lo = 0 if s < PAIRS else 2 * P
-            hi = 4 * P if s >= 2 else 2 * P
+        def q_stage(s, lo, hi):
+            g = st["g", s]
+            if ("cd", s) not in st:
+                cd = work.tile([P, 4 * P], U32, name="cd", tag="cd", bufs=5, align_bytes=64)
+                sc = work.tile([P, 4 * P], U8, name="sc", tag="sc", bufs=5, align_bytes=64)
+                st["cd", s] = (cd, sc)
+            cd, sc = st["cd", s]
             nc.vector.quantize_mx(out=cd[:, lo:hi].bitcast(FP8X4), scales=sc[:, lo:hi], in_=g[:, 4 * lo : 4 * hi])
-            st["cd", s] = (cd, sc)
 
         def h_stage(i):
             cd, sc = st["cd", i]
@@ -221,7 +221,7 @@ def tile_replaced_compose_lora_pa_t_w4_kernel(
 
         def out_stage(i):
             op = st.pop(("op", i))
-            ob = work.tile([P, 2, D_OUT], F32, name="ob", tag="ob", bufs=4, align_bytes=64)
+            ob = work.tile([P, 2, D_OUT], F32, name="ob", tag="ob", bufs=PAIRS, align_bytes=64)
             nc.vector.tensor_tensor(
                 out=ob[:], in0=op[:], in1=bias_sb[:].unsqueeze(1).to_broadcast([P, 2, D_OUT]), op=ALU.add
             )
@@ -244,7 +244,7 @@ def tile_replaced_compose_lora_pa_t_w4_kernel(
 
         def back_out_stage(i):
             bk = st.pop(("bk", i))
-            ob = work.tile([P, 2, D_OUT], F32, name="ob", tag="ob", bufs=4, align_bytes=64)
+            ob = work.tile([P, 2, D_OUT], F32, name="ob", tag="ob", bufs=PAIRS, align_bytes=64)
             nc.scalar.copy(out=ob[:], in_=bk[:])
             store(i, ob)
 
@@ -267,7 +267,7 @@ def tile_replaced_compose_lora_pa_t_w4_kernel(
         widen(0, parts=2)
         widen(1)
         for h in range(2):
-            empty_turned(turn(a_sb[:, h * 2 * D : (h + 1) * 2 * D]), a_grp[:, h * 2 * D : (h + 1) * 2 * D])
+            empty_turned(turn(a_sb[:, h * 2 * D : (h + 1) * 2 * D], "hp", 4), a_grp[:, h * 2 * D : (h + 1) * 2 * D])
         for i in range(2):
             t_stage(i)
             e_stage(i)
@@ -277,14 +277,13 @@ def tile_replaced_compose_lora_pa_t_w4_kernel(
         )
 
         def lead(s):
-            return 3 if s < 12 else 2
+            return 3 if s < 26 else 2
 
         done = 2
-        for s in range(PAIRS + 4):
+        for s in range(PAIRS - 1):
             fresh = range(done, min(PAIRS, s + lead(s) + 1))
             done = max(done, fresh.stop)
-            if s < PAIRS + 2:
-                q_stage(s)
+            q_stage(s, 0, 4 * P if s >= 2 else 2 * P)
             for i in fresh:
                 widen(i)
             if s == 1:
@@ -307,3 +306,48 @@ def tile_replaced_compose_lora_pa_t_w4_kernel(
                 if not fresh:
                     back_stage(s - 3)
                 back_out_stage(s - 3)
+
+        last = PAIRS - 1
+        q_stage(last, 2 * P, 4 * P)
+        q_stage(last, 0, 2 * P)
+        out_stage(last - 3)
+        h_stage(last)
+        eh_stage(last)
+        o_stage(last - 2)
+        q_stage(last + 1, 2 * P, 4 * P)
+        o_stage(last - 1)
+        xc, xs = st.pop(("cd", last))
+        ob = work.tile([P, 2, D_OUT], F32, name="ob", tag="ob", bufs=PAIRS, align_bytes=64)
+        ops = []
+        for j in range(2):
+            cols = slice(j * P, (j + 1) * P)
+            hcols = slice((2 + j) * P, (3 + j) * P)
+            q_stage(last + 2, hcols.start, hcols.stop)
+            hc, hs = st["cd", last + 2]
+            bank = psum.tile([P, 2, D_OUT], F32, name="hp", tag="hp", bufs=4)
+            op = bank[:, 0, :]
+            nc.tensor.matmul_mx(
+                out=op,
+                lhsT=hc[:, hcols].bitcast(FP8X4),
+                lhsT_scale=hs[:, hcols],
+                rhs=b_codes[:].bitcast(FP8X4),
+                rhs_scale=b_scales[:],
+                start=True,
+                stop=False,
+            )
+            for half in range(2):
+                nc.tensor.matmul_mx(
+                    out=op[:, half * P : (half + 1) * P],
+                    lhsT=xc[:, cols].bitcast(FP8X4),
+                    lhsT_scale=xs[:, cols],
+                    rhs=w_sb[:, half * 256 : (half + 1) * 256].bitcast(FP4X4),
+                    rhs_scale=w_sc[:, half * P : (half + 1) * P],
+                    start=False,
+                    stop=(half == 1),
+                )
+            ops.append(op)
+            out_stage(last - 2 + j)
+        c, q = divmod(last, PPC)
+        for j in range(2):
+            nc.vector.tensor_tensor(out=ob[:, j, :], in0=ops[j], in1=bias_sb[:], op=ALU.add)
+            nc.sync.dma_start(out=out_rows[c][:, 2 * q + j, :], in_=ob[:, j, :])

@@ -22,7 +22,7 @@ PER = 8
 CHUNKS = TOKENS // (P * PER)
 PAIRS = TOKENS // (2 * P)
 PPC = PER // 2
-TURNED = range(0, 27, 4)
+TURNED = [i for i in range(22) if i % 7 in (0, 3)]
 
 
 def tile_replaced_compose_lora_pa_t_w4_kernel(
@@ -39,10 +39,11 @@ def tile_replaced_compose_lora_pa_t_w4_kernel(
         ctx.enter_context(tc.manual_schedule())
 
         ident = keep.tile([P, P], F32, name="ident")
-        make_identity(nc, ident[:])
+        nc.vector.memset(ident[:], 0.0)
+        make_identity(nc, ident[:], nomemset=True)
 
         xb = [keep.tile([P, PER * D], U8, name="xb%d" % c, align_bytes=64) for c in range(CHUNKS)]
-        scale_col = keep.tile([P, 4], F32, name="scale_col")
+        scale_col = keep.tile([P, 2, 2], F32, name="scale_col")
         scale = keep.tile([P, 2 * D], F32, name="scale", align_bytes=64)
         a_sb = keep.tile([P, 4 * D], BF16, name="a_sb", align_bytes=64)
         b_sb = keep.tile([P, D_OUT, 16], BF16, name="b_sb", align_bytes=64)
@@ -55,10 +56,12 @@ def tile_replaced_compose_lora_pa_t_w4_kernel(
         spread = keep.tile([P, P], F32, name="spread")
 
         nc.vector.memset(w_sc[:].bitcast(I32), 0)
-        nc.sync.dma_start(out=scale_col[:], in_=x_scale.rearrange("a b (p t) -> p (a b t)", t=4))
-        nc.sync.dma_start(out=lw_sb[:], in_=lora_weights.partition_broadcast(P))
+        a_rows = lora_A.rearrange("n r d -> (n r) d").rearrange("(m t) d -> m (t d)", t=4)
+        nc.sync.dma_start(out=scale_col[:], in_=x_scale.rearrange("a b (h p e) -> p (a b h) e", h=2, e=2))
         nc.sync.dma_start(out=xb[0][:, 0 : 2 * D], in_=x_rows[0][:, 0 : 2 * D])
-        nc.sync.dma_start(out=a_sb[:], in_=lora_A.rearrange("n r d -> (n r) d").rearrange("(m t) d -> m (t d)", t=4))
+        nc.scalar.dma_start(out=lw_sb[:], in_=lora_weights.partition_broadcast(P))
+        nc.sync.dma_start(out=a_sb[:, 0 : 2 * D], in_=a_rows[:, 0 : 2 * D])
+        nc.sync.dma_start(out=a_sb[:, 2 * D :], in_=a_rows[:, 2 * D :])
         nc.sync.dma_start(out=xb[0][:, 2 * D :], in_=x_rows[0][:, 2 * D :])
         b_rows = lora_B.rearrange("n o r -> n (o r)")
         b_run = 16 * D_OUT - 12
@@ -86,7 +89,7 @@ def tile_replaced_compose_lora_pa_t_w4_kernel(
         a_grp = keep.tile([P, 4 * NR], BF16, name="a_grp", align_bytes=64)
         b_grp = keep.tile([P, 4 * D_OUT], BF16, name="b_grp", align_bytes=64)
 
-        def turn(rows, tag="tr", bufs=2):
+        def turn(rows, tag="tr", bufs=3):
             words = rows.bitcast(F32)
             xt = psum.tile([P, 2, 2, P], F32, name="xt", tag=tag, bufs=bufs)
             for j in range(2):
@@ -107,15 +110,14 @@ def tile_replaced_compose_lora_pa_t_w4_kernel(
                 st["g", s] = work.tile([P, 4 * D], BF16, name="grp", tag="grp", bufs=4, align_bytes=64)
             return st["g", s]
 
-        def widen(i, parts=1):
+        def widen(i, parts=((0, 2 * D),)):
             c, q = divmod(i, PPC)
             xw = work.tile([P, 2 * D], BF16, name="xw", tag="xw", bufs=4, align_bytes=64)
-            width = 2 * D // parts
-            for k in range(parts):
+            for lo, hi in parts:
                 nc.vector.tensor_tensor(
-                    out=xw[:, k * width : (k + 1) * width],
-                    in0=xb[c][:, q * 2 * D + k * width : q * 2 * D + (k + 1) * width].bitcast(FP8),
-                    in1=scale[:, 0:width],
+                    out=xw[:, lo:hi],
+                    in0=xb[c][:, q * 2 * D + lo : q * 2 * D + hi].bitcast(FP8),
+                    in1=scale[:, lo % D : lo % D + hi - lo],
                     op=ALU.mult,
                 )
             st["xw", i] = xw
@@ -139,7 +141,7 @@ def tile_replaced_compose_lora_pa_t_w4_kernel(
             cd, sc = st["cd", i]
             hp = []
             for j in range(2):
-                h = psum.tile([P, 4, P], F32, name="hp", tag="hp", bufs=4)
+                h = psum.tile([P, 4, P], F32, name="hp", tag="hp", bufs=3)
                 cols = slice(j * P, (j + 1) * P)
                 for t in range(4):
                     ch = slice(t * P, (t + 1) * P)
@@ -236,7 +238,7 @@ def tile_replaced_compose_lora_pa_t_w4_kernel(
 
         def back_stage(i):
             ot = st.pop(("ot", i))
-            bk = psum.tile([P, 2, D_OUT], F32, name="bk", tag="tr", bufs=2)
+            bk = psum.tile([P, 2, D_OUT], F32, name="bk", tag="tr", bufs=3)
             for j in range(2):
                 for h in range(2):
                     nc.tensor.transpose(bk[:, j, h * P : (h + 1) * P], ot[:, h, j * P : (j + 1) * P], ident[:])
@@ -248,13 +250,18 @@ def tile_replaced_compose_lora_pa_t_w4_kernel(
             nc.scalar.copy(out=ob[:], in_=bk[:])
             store(i, ob)
 
-        sp = psum.tile([P, 4, P], F32, name="sp", tag="op", bufs=2)
-        for t in range(4):
-            nc.tensor.transpose(sp[:, t, :], scale_col[:, t : t + 1].to_broadcast([P, P]), ident[:])
-        for k in range(2):
-            nc.scalar.copy(
-                out=scale[:, k * D : (k + 1) * D].rearrange("p (n t) -> p n t", t=4), in_=sp[:].rearrange("p t n -> p n t")
-            )
+        halves = []
+        for h in range(2):
+            sp = psum.tile([P, 2, P], F32, name="sp", tag="op", bufs=2)
+            for e in range(2):
+                nc.tensor.transpose(sp[:, e, :], scale_col[:, h, e : e + 1].to_broadcast([P, P]), ident[:])
+            halves.append(sp)
+        for row in range(2):
+            for h in range(2):
+                lo = row * D + h * D // 2
+                nc.scalar.copy(
+                    out=scale[:, lo : lo + D // 2].rearrange("p (n e) -> p n e", e=2), in_=halves[h][:].rearrange("p e n -> p n e")
+                )
         nc.vector.scalar_tensor_tensor(
             out=spread[:].rearrange("p (n q) -> p n q", q=4),
             in0=ident[:].rearrange("p (n q) -> p n q", q=4),
@@ -264,10 +271,10 @@ def tile_replaced_compose_lora_pa_t_w4_kernel(
             op1=ALU.mult,
             accum_out=coef[:],
         )
-        widen(0, parts=2)
+        widen(0, parts=((0, D // 2), (D // 2, D), (D, 2 * D)))
         widen(1)
         for h in range(2):
-            empty_turned(turn(a_sb[:, h * 2 * D : (h + 1) * 2 * D], "hp", 4), a_grp[:, h * 2 * D : (h + 1) * 2 * D])
+            empty_turned(turn(a_sb[:, h * 2 * D : (h + 1) * 2 * D], "hp", 3), a_grp[:, h * 2 * D : (h + 1) * 2 * D])
         for i in range(2):
             t_stage(i)
             e_stage(i)
@@ -277,7 +284,7 @@ def tile_replaced_compose_lora_pa_t_w4_kernel(
         )
 
         def lead(s):
-            return 3 if s < 26 else 2
+            return 3 if s < 27 else 2
 
         done = 2
         for s in range(PAIRS - 1):
@@ -324,7 +331,7 @@ def tile_replaced_compose_lora_pa_t_w4_kernel(
             hcols = slice((2 + j) * P, (3 + j) * P)
             q_stage(last + 2, hcols.start, hcols.stop)
             hc, hs = st["cd", last + 2]
-            bank = psum.tile([P, 2, D_OUT], F32, name="hp", tag="hp", bufs=4)
+            bank = psum.tile([P, 2, D_OUT], F32, name="hp", tag="hp", bufs=3)
             op = bank[:, 0, :]
             nc.tensor.matmul_mx(
                 out=op,

@@ -3,7 +3,8 @@ from contextlib import ExitStack
 import concourse.mybir as mybir
 from concourse.masks import make_identity
 
-TOKENS, D, NR, D_OUT = 8192, 512, 512, 256
+TOKENS, D, NR, D_OUT, ADAPTERS, RANK = 8192, 512, 512, 256, 32, 16
+ALPHA_OVER_RANK = 2.0
 FLOPS = 2 * TOKENS * (D * NR + D * D_OUT + NR * D_OUT)
 
 F32 = mybir.dt.float32
@@ -18,19 +19,29 @@ ALU = mybir.AluOpType
 ACT = mybir.ActivationFunctionType
 
 P = 128
-PER = 8
-CHUNKS = TOKENS // (P * PER)
+PACK = 4
+CHUNK_PAIRS = 4
+CHUNKS = TOKENS // (P * 2 * CHUNK_PAIRS)
 PAIRS = TOKENS // (2 * P)
-PPC = PER // 2
-TURNED = [i for i in range(22) if i % 7 in (0, 3)]
+LAST = PAIRS - 1
+
+LEAD = 3
+H_LAG = 2
+OUT_LAG = H_LAG + 1
+CYCLE = 3
+TURNED = range(0, PAIRS - 10, CYCLE)
+
+X_WORDS = slice(0, 2 * P)
+H_WORDS = slice(2 * P, 4 * P)
+ALL_WORDS = slice(0, 4 * P)
 
 
 def tile_replaced_compose_lora_pa_t_w4_kernel(
     tc, x_bytes, x_scale, lora_A, lora_B, W_words, W_scales, bias, lora_weights, out
 ):
     nc = tc.nc
-    x_rows = x_bytes.rearrange("b s d -> (b s) d").rearrange("(c p n) d -> c p (n d)", p=P, n=PER)
-    out_rows = out.rearrange("b s o -> (b s) o").rearrange("(c p n) o -> c p n o", p=P, n=PER)
+    x_rows = x_bytes.rearrange("b s d -> (b s) d").rearrange("(c p n) d -> c p (n d)", p=P, n=2 * CHUNK_PAIRS)
+    out_rows = out.rearrange("b s o -> (b s) o").rearrange("(c p n) o -> c p n o", p=P, n=2 * CHUNK_PAIRS)
 
     with ExitStack() as ctx:
         keep = ctx.enter_context(tc.tile_pool(name="keep", bufs=1))
@@ -38,25 +49,28 @@ def tile_replaced_compose_lora_pa_t_w4_kernel(
         psum = ctx.enter_context(tc.psum_pool(name="psum", bufs=1))
         ctx.enter_context(tc.manual_schedule())
 
+        def bank(kind, shape):
+            return psum.tile(shape, F32, name=kind, tag=kind, bufs={"turn": 3, "h": 3, "out": 2}[kind])
+
         ident = keep.tile([P, P], F32, name="ident")
         nc.vector.memset(ident[:], 0.0)
         make_identity(nc, ident[:], nomemset=True)
 
-        xb = [keep.tile([P, PER * D], U8, name="xb%d" % c, align_bytes=64) for c in range(CHUNKS)]
+        xb = [keep.tile([P, 2 * CHUNK_PAIRS * D], U8, name="xb%d" % c, align_bytes=64) for c in range(CHUNKS)]
         scale_col = keep.tile([P, 2, 2], F32, name="scale_col")
         scale = keep.tile([P, 2 * D], F32, name="scale", align_bytes=64)
-        a_sb = keep.tile([P, 4 * D], BF16, name="a_sb", align_bytes=64)
-        b_sb = keep.tile([P, D_OUT, 16], BF16, name="b_sb", align_bytes=64)
+        a_sb = keep.tile([P, PACK * D], BF16, name="a_sb", align_bytes=64)
+        b_sb = keep.tile([P, D_OUT, RANK], BF16, name="b_sb", align_bytes=64)
         w_sb = keep.tile([P, 2 * D_OUT], U8, name="w_sb", align_bytes=64)
         w_sc = keep.tile([P, D_OUT], U8, name="w_sc", align_bytes=64)
         bias_sb = keep.tile([P, D_OUT], BF16, name="bias_sb", align_bytes=64)
         bias_col = keep.tile([P, 2, 16], BF16, name="bias_col", align_bytes=64)
-        lw_sb = keep.tile([P, 32], BF16, name="lw_sb", align_bytes=64)
+        lw_sb = keep.tile([P, ADAPTERS], BF16, name="lw_sb", align_bytes=64)
         coef = keep.tile([P, 1], F32, name="coef")
-        spread = keep.tile([P, P], F32, name="spread")
+        coef_terms = keep.tile([P, P], F32, name="coef_terms")
 
         nc.vector.memset(w_sc[:].bitcast(I32), 0)
-        a_rows = lora_A.rearrange("n r d -> (n r) d").rearrange("(m t) d -> m (t d)", t=4)
+        a_rows = lora_A.rearrange("n r d -> (n r) d").rearrange("(m t) d -> m (t d)", t=PACK)
         nc.sync.dma_start(out=scale_col[:], in_=x_scale.rearrange("a b (h p e) -> p (a b h) e", h=2, e=2))
         nc.sync.dma_start(out=xb[0][:, 0 : 2 * D], in_=x_rows[0][:, 0 : 2 * D])
         nc.scalar.dma_start(out=lw_sb[:], in_=lora_weights.partition_broadcast(P))
@@ -64,10 +78,11 @@ def tile_replaced_compose_lora_pa_t_w4_kernel(
         nc.sync.dma_start(out=a_sb[:, 2 * D :], in_=a_rows[:, 2 * D :])
         nc.sync.dma_start(out=xb[0][:, 2 * D :], in_=x_rows[0][:, 2 * D :])
         b_rows = lora_B.rearrange("n o r -> n (o r)")
-        b_run = 16 * D_OUT - 12
-        for q in range(4):
+        b_run = RANK * D_OUT - (RANK - PACK)
+        for q in range(PACK):
             nc.sync.dma_start(
-                out=b_sb[:].rearrange("p o r -> p (o r)")[q:P:4, 0:b_run], in_=b_rows[:, 4 * q : 4 * q + b_run]
+                out=b_sb[:].rearrange("p o r -> p (o r)")[q:P:PACK, 0:b_run],
+                in_=b_rows[:, PACK * q : PACK * q + b_run],
             )
         nc.sync.dma_start(out=xb[1][:], in_=x_rows[1])
         nc.sync.dma_start(out=w_sb[:], in_=W_words[0])
@@ -76,9 +91,8 @@ def tile_replaced_compose_lora_pa_t_w4_kernel(
                 out=w_sc[32 * q : 32 * q + 4, :].bitcast(I32), in_=W_scales[0, 4 * q : 4 * q + 4, :].bitcast(I32)
             )
         nc.sync.dma_start(out=bias_sb[:], in_=bias.partition_broadcast(P))
-        if TURNED:
-            for h in range(2):
-                nc.sync.dma_start(out=bias_col[:, h, 0:1], in_=bias[h * P : (h + 1) * P].unsqueeze(1))
+        for half in range(2):
+            nc.sync.dma_start(out=bias_col[:, half, 0:1], in_=bias[half * P : (half + 1) * P].unsqueeze(1))
         for c in range(2, CHUNKS):
             nc.sync.dma_start(out=xb[c][:], in_=x_rows[c])
 
@@ -86,33 +100,34 @@ def tile_replaced_compose_lora_pa_t_w4_kernel(
         a_scales = keep.tile([P, NR], U8, name="a_scales", align_bytes=64)
         b_codes = keep.tile([P, D_OUT], U32, name="b_codes", align_bytes=64)
         b_scales = keep.tile([P, D_OUT], U8, name="b_scales", align_bytes=64)
-        a_grp = keep.tile([P, 4 * NR], BF16, name="a_grp", align_bytes=64)
-        b_grp = keep.tile([P, 4 * D_OUT], BF16, name="b_grp", align_bytes=64)
+        a_values = keep.tile([P, PACK * NR], BF16, name="a_values", align_bytes=64)
+        b_values = keep.tile([P, PACK * D_OUT], BF16, name="b_values", align_bytes=64)
 
-        def turn(rows, tag="tr", bufs=3):
+        widened, x_banks, h_banks, out_banks, biased, back_banks = {}, {}, {}, {}, {}, {}
+        step_values, step_codes = {}, {}
+
+        def turn(rows, kind):
             words = rows.bitcast(F32)
-            xt = psum.tile([P, 2, 2, P], F32, name="xt", tag=tag, bufs=bufs)
+            turned = bank(kind, [P, 2, 2, P])
             for j in range(2):
                 for u in range(2):
-                    nc.tensor.transpose(xt[:, j, u, :], words[:, 256 * j + u : 256 * (j + 1) : 2], ident[:])
-            return xt
+                    nc.tensor.transpose(turned[:, j, u, :], words[:, 256 * j + u : 256 * (j + 1) : 2], ident[:])
+            return turned
 
-        def empty_turned(xt, dst):
+        def empty_turned(turned, values):
             nc.scalar.copy(
-                out=dst.bitcast(F32).rearrange("p (j r u) -> p j r u", j=2, u=2),
-                in_=xt[:].rearrange("p j u r -> p j r u"),
+                out=values.bitcast(F32).rearrange("p (j r u) -> p j r u", j=2, u=2),
+                in_=turned[:].rearrange("p j u r -> p j r u"),
             )
 
-        st = {}
-
-        def group(s):
-            if ("g", s) not in st:
-                st["g", s] = work.tile([P, 4 * D], BF16, name="grp", tag="grp", bufs=4, align_bytes=64)
-            return st["g", s]
+        def values_of(s):
+            if s not in step_values:
+                step_values[s] = work.tile([P, 4 * D], BF16, name="values", tag="values", bufs=LEAD + 1, align_bytes=64)
+            return step_values[s]
 
         def widen(i, parts=((0, 2 * D),)):
-            c, q = divmod(i, PPC)
-            xw = work.tile([P, 2 * D], BF16, name="xw", tag="xw", bufs=4, align_bytes=64)
+            c, q = divmod(i, CHUNK_PAIRS)
+            xw = work.tile([P, 2 * D], BF16, name="xw", tag="xw", bufs=LEAD + 1, align_bytes=64)
             for lo, hi in parts:
                 nc.vector.tensor_tensor(
                     out=xw[:, lo:hi],
@@ -120,241 +135,204 @@ def tile_replaced_compose_lora_pa_t_w4_kernel(
                     in1=scale[:, lo % D : lo % D + hi - lo],
                     op=ALU.mult,
                 )
-            st["xw", i] = xw
+            widened[i] = xw
 
-        def t_stage(i):
-            st["xt", i] = turn(st.pop(("xw", i))[:])
+        def turn_x(i):
+            x_banks[i] = turn(widened.pop(i)[:], "turn")
 
-        def e_stage(i):
-            empty_turned(st.pop(("xt", i)), group(i)[:, 0 : 2 * D])
+        def empty_x(i):
+            empty_turned(x_banks.pop(i), values_of(i)[:, 0 : 2 * D])
 
-        def q_stage(s, lo, hi):
-            g = st["g", s]
-            if ("cd", s) not in st:
-                cd = work.tile([P, 4 * P], U32, name="cd", tag="cd", bufs=5, align_bytes=64)
-                sc = work.tile([P, 4 * P], U8, name="sc", tag="sc", bufs=5, align_bytes=64)
-                st["cd", s] = (cd, sc)
-            cd, sc = st["cd", s]
-            nc.vector.quantize_mx(out=cd[:, lo:hi].bitcast(FP8X4), scales=sc[:, lo:hi], in_=g[:, 4 * lo : 4 * hi])
+        def quantise(s, words):
+            if s not in step_codes:
+                step_codes[s] = (
+                    work.tile([P, 4 * P], U32, name="codes", tag="codes", bufs=H_LAG + 3, align_bytes=64),
+                    work.tile([P, 4 * P], U8, name="scales", tag="scales", bufs=H_LAG + 3, align_bytes=64),
+                )
+            codes, scales = step_codes[s]
+            nc.vector.quantize_mx(
+                out=codes[:, words].bitcast(FP8X4),
+                scales=scales[:, words],
+                in_=step_values[s][:, PACK * words.start : PACK * words.stop],
+            )
 
-        def h_stage(i):
-            cd, sc = st["cd", i]
-            hp = []
+        def mx(acc, stationary, moving, start, stop):
+            nc.tensor.matmul_mx(
+                out=acc,
+                lhsT=stationary[0],
+                lhsT_scale=stationary[1],
+                rhs=moving[0],
+                rhs_scale=moving[1],
+                start=start,
+                stop=stop,
+            )
+
+        def e4m3(codes, scales, lo, width):
+            return codes[:, lo : lo + width].bitcast(FP8X4), scales[:, lo : lo + width]
+
+        def x_cols(i, j):
+            return e4m3(*step_codes[i], j * P, P)
+
+        def h_cols(i, j, tiles):
+            return e4m3(*step_codes[i + H_LAG], H_WORDS.start + j * P, tiles * P)
+
+        def w_cols(half):
+            return w_sb[:, half * 2 * P : (half + 1) * 2 * P].bitcast(FP4X4), w_sc[:, half * P : (half + 1) * P]
+
+        def make_h(i):
+            h_banks[i] = []
             for j in range(2):
-                h = psum.tile([P, 4, P], F32, name="hp", tag="hp", bufs=3)
-                cols = slice(j * P, (j + 1) * P)
-                for t in range(4):
-                    ch = slice(t * P, (t + 1) * P)
-                    nc.tensor.matmul_mx(
-                        out=h[:, t, :],
-                        lhsT=a_codes[:, ch].bitcast(FP8X4),
-                        lhsT_scale=a_scales[:, ch],
-                        rhs=cd[:, cols].bitcast(FP8X4),
-                        rhs_scale=sc[:, cols],
-                        start=True,
-                        stop=True,
-                    )
-                hp.append(h)
-            st["hp", i] = hp
+                acc = bank("h", [P, PACK, P])
+                for t in range(PACK):
+                    mx(acc[:, t, :], e4m3(a_codes, a_scales, t * P, P), x_cols(i, j), True, True)
+                h_banks[i].append(acc)
 
-        def eh_stage(i):
-            hp = st.pop(("hp", i))
-            g = group(i + 2)
-            for j in range(2):
+        def empty_h(i):
+            values = values_of(i + H_LAG)
+            for j, acc in enumerate(h_banks.pop(i)):
                 nc.scalar.copy(
-                    out=g[:, (2 + j) * NR : (3 + j) * NR].rearrange("p (r t) -> p r t", t=4),
-                    in_=hp[j][:].rearrange("p t r -> p r t"),
+                    out=values[:, (2 + j) * NR : (3 + j) * NR].rearrange("p (r t) -> p r t", t=PACK),
+                    in_=acc[:].rearrange("p t r -> p r t"),
                 )
 
-        def o_stage(i):
-            xc, xs = st.pop(("cd", i))
-            hc, hs = st["cd", i + 2]
-            op = psum.tile([P, 2, D_OUT], F32, name="op", tag="op", bufs=2)
+        def out_tile(i, j, acc):
+            mx(acc, h_cols(i, j, 1), e4m3(b_codes, b_scales, 0, D_OUT), True, False)
+            for half in range(2):
+                mx(acc[:, half * P : (half + 1) * P], x_cols(i, j), w_cols(half), False, half == 1)
+
+        def out_half_turned(i, half, acc):
+            mx(acc, e4m3(b_codes, b_scales, half * P, P), h_cols(i, 0, 2), True, False)
             for j in range(2):
-                cols = slice(j * P, (j + 1) * P)
-                hcols = slice((2 + j) * P, (3 + j) * P)
-                if i in TURNED:
-                    nc.tensor.matmul_mx(
-                        out=op[:, j, :],
-                        lhsT=b_codes[:, cols].bitcast(FP8X4),
-                        lhsT_scale=b_scales[:, cols],
-                        rhs=hc[:, 2 * P :].bitcast(FP8X4),
-                        rhs_scale=hs[:, 2 * P :],
-                        start=True,
-                        stop=False,
-                    )
-                else:
-                    nc.tensor.matmul_mx(
-                        out=op[:, j, :],
-                        lhsT=hc[:, hcols].bitcast(FP8X4),
-                        lhsT_scale=hs[:, hcols],
-                        rhs=b_codes[:].bitcast(FP8X4),
-                        rhs_scale=b_scales[:],
-                        start=True,
-                        stop=False,
-                    )
-                for half in range(2):
-                    oc = slice(half * P, (half + 1) * P)
-                    if i in TURNED:
-                        nc.tensor.matmul_mx(
-                            out=op[:, j, oc],
-                            lhsT=w_sb[:, j * 256 : (j + 1) * 256].bitcast(FP4X4),
-                            lhsT_scale=w_sc[:, cols],
-                            rhs=xc[:, oc].bitcast(FP8X4),
-                            rhs_scale=xs[:, oc],
-                            start=False,
-                            stop=(half == 1),
-                        )
-                    else:
-                        nc.tensor.matmul_mx(
-                            out=op[:, j, oc],
-                            lhsT=xc[:, cols].bitcast(FP8X4),
-                            lhsT_scale=xs[:, cols],
-                            rhs=w_sb[:, half * 256 : (half + 1) * 256].bitcast(FP4X4),
-                            rhs_scale=w_sc[:, oc],
-                            start=False,
-                            stop=(half == 1),
-                        )
-            st["op", i] = op
+                mx(acc[:, j * P : (j + 1) * P], w_cols(half), x_cols(i, j), False, j == 1)
 
-        def store(i, ob):
-            c, q = divmod(i, PPC)
-            nc.sync.dma_start(out=out_rows[c][:, 2 * q : 2 * q + 2, :], in_=ob[:])
+        def make_out(i):
+            out_banks[i] = bank("out", [P, 2, D_OUT])
+            for side in range(2):
+                (out_half_turned if i in TURNED else out_tile)(i, side, out_banks[i][:, side, :])
 
-        def out_stage(i):
-            op = st.pop(("op", i))
-            ob = work.tile([P, 2, D_OUT], F32, name="ob", tag="ob", bufs=PAIRS, align_bytes=64)
+        def result_tile():
+            return work.tile([P, 2, D_OUT], F32, name="result", tag="result", bufs=PAIRS, align_bytes=64)
+
+        def out_view(i):
+            c, q = divmod(i, CHUNK_PAIRS)
+            return out_rows[c][:, 2 * q : 2 * q + 2, :]
+
+        def finish(i):
+            result = result_tile()
             nc.vector.tensor_tensor(
-                out=ob[:], in0=op[:], in1=bias_sb[:].unsqueeze(1).to_broadcast([P, 2, D_OUT]), op=ALU.add
+                out=result[:],
+                in0=out_banks.pop(i)[:],
+                in1=bias_sb[:].unsqueeze(1).to_broadcast([P, 2, D_OUT]),
+                op=ALU.add,
             )
-            store(i, ob)
+            nc.sync.dma_start(out=out_view(i), in_=result[:])
 
-        def bias_stage(i):
-            op = st.pop(("op", i))
-            ot = work.tile([P, 2, 2 * P], F32, name="ot", tag="ot", bufs=2, align_bytes=64)
-            for h in range(2):
-                nc.scalar.activation(out=ot[:, h, :], in_=op[:, h, :], func=ACT.Identity, bias=bias_col[:, h, 0:1], scale=1.0)
-            st["ot", i] = ot
+        def add_bias_turned(i):
+            acc = out_banks.pop(i)
+            biased[i] = work.tile([P, 2, 2 * P], F32, name="biased", tag="biased", bufs=3, align_bytes=64)
+            for half in range(2):
+                nc.scalar.activation(
+                    out=biased[i][:, half, :],
+                    in_=acc[:, half, :],
+                    func=ACT.Identity,
+                    bias=bias_col[:, half, 0:1],
+                    scale=1.0,
+                )
 
-        def back_stage(i):
-            ot = st.pop(("ot", i))
-            bk = psum.tile([P, 2, D_OUT], F32, name="bk", tag="tr", bufs=3)
+        def turn_back(i):
+            sums = biased.pop(i)
+            back_banks[i] = bank("turn", [P, 2, D_OUT])
             for j in range(2):
-                for h in range(2):
-                    nc.tensor.transpose(bk[:, j, h * P : (h + 1) * P], ot[:, h, j * P : (j + 1) * P], ident[:])
-            st["bk", i] = bk
+                for half in range(2):
+                    nc.tensor.transpose(
+                        back_banks[i][:, j, half * P : (half + 1) * P], sums[:, half, j * P : (j + 1) * P], ident[:]
+                    )
 
-        def back_out_stage(i):
-            bk = st.pop(("bk", i))
-            ob = work.tile([P, 2, D_OUT], F32, name="ob", tag="ob", bufs=PAIRS, align_bytes=64)
-            nc.scalar.copy(out=ob[:], in_=bk[:])
-            store(i, ob)
+        def finish_turned(i):
+            result = result_tile()
+            nc.scalar.copy(out=result[:], in_=back_banks.pop(i)[:])
+            nc.sync.dma_start(out=out_view(i), in_=result[:])
 
-        halves = []
-        for h in range(2):
-            sp = psum.tile([P, 2, P], F32, name="sp", tag="op", bufs=2)
+        scale_banks = []
+        for half in range(2):
+            spread = bank("out", [P, 2, P])
             for e in range(2):
-                nc.tensor.transpose(sp[:, e, :], scale_col[:, h, e : e + 1].to_broadcast([P, P]), ident[:])
-            halves.append(sp)
-        for row in range(2):
-            for h in range(2):
-                lo = row * D + h * D // 2
+                nc.tensor.transpose(spread[:, e, :], scale_col[:, half, e : e + 1].to_broadcast([P, P]), ident[:])
+            scale_banks.append(spread)
+        for j in range(2):
+            for half in range(2):
+                lo = j * D + half * D // 2
                 nc.scalar.copy(
-                    out=scale[:, lo : lo + D // 2].rearrange("p (n e) -> p n e", e=2), in_=halves[h][:].rearrange("p e n -> p n e")
+                    out=scale[:, lo : lo + D // 2].rearrange("p (n e) -> p n e", e=2),
+                    in_=scale_banks[half][:].rearrange("p e n -> p n e"),
                 )
         nc.vector.scalar_tensor_tensor(
-            out=spread[:].rearrange("p (n q) -> p n q", q=4),
-            in0=ident[:].rearrange("p (n q) -> p n q", q=4),
-            scalar=2.0,
-            in1=lw_sb[:].unsqueeze(2).to_broadcast([P, 32, 4]),
+            out=coef_terms[:].rearrange("p (n q) -> p n q", q=PACK),
+            in0=ident[:].rearrange("p (n q) -> p n q", q=PACK),
+            scalar=ALPHA_OVER_RANK,
+            in1=lw_sb[:].unsqueeze(2).to_broadcast([P, ADAPTERS, PACK]),
             op0=ALU.mult,
             op1=ALU.mult,
             accum_out=coef[:],
         )
         widen(0, parts=((0, D // 2), (D // 2, D), (D, 2 * D)))
         widen(1)
-        for h in range(2):
-            empty_turned(turn(a_sb[:, h * 2 * D : (h + 1) * 2 * D], "hp", 3), a_grp[:, h * 2 * D : (h + 1) * 2 * D])
+        for half in range(2):
+            cols = slice(half * 2 * D, (half + 1) * 2 * D)
+            empty_turned(turn(a_sb[:, cols], "h"), a_values[:, cols])
         for i in range(2):
-            t_stage(i)
-            e_stage(i)
-        nc.vector.quantize_mx(out=a_codes[:].bitcast(FP8X4), scales=a_scales[:], in_=a_grp[:])
+            turn_x(i)
+            empty_x(i)
+        nc.vector.quantize_mx(out=a_codes[:].bitcast(FP8X4), scales=a_scales[:], in_=a_values[:])
         nc.scalar.activation(
-            out=b_grp[:].rearrange("p (o t) -> p o t", t=4), in_=b_sb[:, :, 0:4], func=ACT.Copy, scale=coef[:]
+            out=b_values[:].rearrange("p (o t) -> p o t", t=PACK), in_=b_sb[:, :, 0:PACK], func=ACT.Copy, scale=coef[:]
         )
 
-        def lead(s):
-            return 3 if s < 27 else 2
-
-        done = 2
-        for s in range(PAIRS - 1):
-            fresh = range(done, min(PAIRS, s + lead(s) + 1))
-            done = max(done, fresh.stop)
-            q_stage(s, 0, 4 * P if s >= 2 else 2 * P)
+        next_pair = 2
+        to_turn = []
+        for s in range(LAST):
+            quantise(s, ALL_WORDS if s >= H_LAG else X_WORDS)
+            if s + 1 == LAST:
+                quantise(LAST, X_WORDS)
+            fresh = range(next_pair, min(PAIRS, s + LEAD + 1))
+            next_pair = fresh.stop
             for i in fresh:
                 widen(i)
-            if s == 1:
-                nc.vector.quantize_mx(out=b_codes[:].bitcast(FP8X4), scales=b_scales[:], in_=b_grp[:])
-            if 0 <= s - 3 < PAIRS and s - 3 not in TURNED:
-                out_stage(s - 3)
-            if s < PAIRS:
-                h_stage(s)
-                eh_stage(s)
-            if 0 <= s - 2 < PAIRS:
-                o_stage(s - 2)
-                if s - 2 in TURNED:
-                    bias_stage(s - 2)
-            for i in fresh:
-                t_stage(i)
-                if i + 1 == fresh.stop and s - 3 in TURNED:
-                    back_stage(s - 3)
-                e_stage(i)
-            if s - 3 in TURNED:
-                if not fresh:
-                    back_stage(s - 3)
-                back_out_stage(s - 3)
+            if s + 1 == H_LAG:
+                nc.vector.quantize_mx(out=b_codes[:].bitcast(FP8X4), scales=b_scales[:], in_=b_values[:])
+            if s >= OUT_LAG and s - OUT_LAG not in TURNED:
+                finish(s - OUT_LAG)
+            make_h(s)
+            empty_h(s)
+            if s >= H_LAG:
+                make_out(s - H_LAG)
+            if s - H_LAG in TURNED:
+                add_bias_turned(s - H_LAG)
+            to_turn.extend(fresh)
+            if s % CYCLE != H_LAG:
+                for i in to_turn:
+                    turn_x(i)
+                    if i == to_turn[-1] and s - OUT_LAG in TURNED:
+                        turn_back(s - OUT_LAG)
+                    empty_x(i)
+                to_turn.clear()
+                if s - OUT_LAG in TURNED:
+                    finish_turned(s - OUT_LAG)
 
-        last = PAIRS - 1
-        q_stage(last, 2 * P, 4 * P)
-        q_stage(last, 0, 2 * P)
-        out_stage(last - 3)
-        h_stage(last)
-        eh_stage(last)
-        o_stage(last - 2)
-        q_stage(last + 1, 2 * P, 4 * P)
-        o_stage(last - 1)
-        xc, xs = st.pop(("cd", last))
-        ob = work.tile([P, 2, D_OUT], F32, name="ob", tag="ob", bufs=PAIRS, align_bytes=64)
-        ops = []
+        make_h(LAST)
+        empty_h(LAST)
+        quantise(LAST, H_WORDS)
+        finish(LAST - 3)
+        make_out(LAST - 2)
+        quantise(LAST + 1, H_WORDS)
+        make_out(LAST - 1)
+        last_result = result_tile()
+        last_banks = []
         for j in range(2):
-            cols = slice(j * P, (j + 1) * P)
-            hcols = slice((2 + j) * P, (3 + j) * P)
-            q_stage(last + 2, hcols.start, hcols.stop)
-            hc, hs = st["cd", last + 2]
-            bank = psum.tile([P, 2, D_OUT], F32, name="hp", tag="hp", bufs=3)
-            op = bank[:, 0, :]
-            nc.tensor.matmul_mx(
-                out=op,
-                lhsT=hc[:, hcols].bitcast(FP8X4),
-                lhsT_scale=hs[:, hcols],
-                rhs=b_codes[:].bitcast(FP8X4),
-                rhs_scale=b_scales[:],
-                start=True,
-                stop=False,
-            )
-            for half in range(2):
-                nc.tensor.matmul_mx(
-                    out=op[:, half * P : (half + 1) * P],
-                    lhsT=xc[:, cols].bitcast(FP8X4),
-                    lhsT_scale=xs[:, cols],
-                    rhs=w_sb[:, half * 256 : (half + 1) * 256].bitcast(FP4X4),
-                    rhs_scale=w_sc[:, half * P : (half + 1) * P],
-                    start=False,
-                    stop=(half == 1),
-                )
-            ops.append(op)
-            out_stage(last - 2 + j)
-        c, q = divmod(last, PPC)
+            quantise(LAST + H_LAG, slice(H_WORDS.start + j * P, H_WORDS.start + (j + 1) * P))
+            last_banks.append(bank("h", [P, D_OUT]))
+            out_tile(LAST, j, last_banks[j][:])
+            finish(LAST - 2 + j)
         for j in range(2):
-            nc.vector.tensor_tensor(out=ob[:, j, :], in0=ops[j], in1=bias_sb[:], op=ALU.add)
-            nc.sync.dma_start(out=out_rows[c][:, 2 * q + j, :], in_=ob[:, j, :])
+            nc.vector.tensor_tensor(out=last_result[:, j, :], in0=last_banks[j][:], in1=bias_sb[:], op=ALU.add)
+            nc.sync.dma_start(out=out_view(LAST)[:, j, :], in_=last_result[:, j, :])

@@ -3,7 +3,7 @@ from contextlib import ExitStack
 import concourse.mybir as mybir
 from concourse.masks import make_identity
 
-TOKENS, D, NR, D_OUT, ADAPTERS, RANK = 8192, 512, 512, 256, 32, 16
+TOKENS, D, NR, D_OUT, RANK = 8192, 512, 512, 256, 16
 ALPHA_OVER_RANK = 2.0
 FLOPS = 2 * TOKENS * (D * NR + D * D_OUT + NR * D_OUT)
 
@@ -65,18 +65,19 @@ def tile_replaced_compose_lora_pa_t_w4_kernel(
         w_sc = keep.tile([P, D_OUT], U8, name="w_sc", align_bytes=64)
         bias_sb = keep.tile([P, D_OUT], BF16, name="bias_sb", align_bytes=64)
         bias_col = keep.tile([P, 2, 16], BF16, name="bias_col", align_bytes=64)
-        lw_sb = keep.tile([P, ADAPTERS], BF16, name="lw_sb", align_bytes=64)
+        lw_col = keep.tile([P, 1], BF16, name="lw_col")
         coef = keep.tile([P, 1], F32, name="coef")
-        coef_terms = keep.tile([P, P], F32, name="coef_terms")
 
         nc.vector.memset(w_sc[:].bitcast(I32), 0)
         a_rows = lora_A.rearrange("n r d -> (n r) d").rearrange("(m t) d -> m (t d)", t=PACK)
         nc.sync.dma_start(out=scale_col[:], in_=x_scale.rearrange("a b (h p e) -> p (a b h) e", h=2, e=2))
         nc.sync.dma_start(out=xb[0][:, 0 : 2 * D], in_=x_rows[0][:, 0 : 2 * D])
-        nc.scalar.dma_start(out=lw_sb[:], in_=lora_weights.partition_broadcast(P))
         nc.sync.dma_start(out=a_sb[:, 0 : 2 * D], in_=a_rows[:, 0 : 2 * D])
         nc.sync.dma_start(out=a_sb[:, 2 * D :], in_=a_rows[:, 2 * D :])
         nc.sync.dma_start(out=xb[0][:, 2 * D :], in_=x_rows[0][:, 2 * D :])
+        nc.sync.dma_start(out=xb[1][:, 0 : 4 * D], in_=x_rows[1][:, 0 : 4 * D])
+        for q in range(PACK):
+            nc.sync.dma_start(out=lw_col[q:P:PACK, :], in_=lora_weights.unsqueeze(1))
         b_rows = lora_B.rearrange("n o r -> n (o r)")
         b_run = RANK * D_OUT - (RANK - PACK)
         for q in range(PACK):
@@ -84,7 +85,7 @@ def tile_replaced_compose_lora_pa_t_w4_kernel(
                 out=b_sb[:].rearrange("p o r -> p (o r)")[q:P:PACK, 0:b_run],
                 in_=b_rows[:, PACK * q : PACK * q + b_run],
             )
-        nc.sync.dma_start(out=xb[1][:], in_=x_rows[1])
+        nc.sync.dma_start(out=xb[1][:, 4 * D :], in_=x_rows[1][:, 4 * D :])
         nc.sync.dma_start(out=w_sb[:], in_=W_words[0])
         for q in range(4):
             nc.sync.dma_start(
@@ -266,23 +267,16 @@ def tile_replaced_compose_lora_pa_t_w4_kernel(
                     out=scale[:, lo : lo + D // 2].rearrange("p (n e) -> p n e", e=2),
                     in_=scale_banks[half][:].rearrange("p e n -> p n e"),
                 )
-        nc.vector.scalar_tensor_tensor(
-            out=coef_terms[:].rearrange("p (n q) -> p n q", q=PACK),
-            in0=ident[:].rearrange("p (n q) -> p n q", q=PACK),
-            scalar=ALPHA_OVER_RANK,
-            in1=lw_sb[:].unsqueeze(2).to_broadcast([P, ADAPTERS, PACK]),
-            op0=ALU.mult,
-            op1=ALU.mult,
-            accum_out=coef[:],
-        )
         widen(0, parts=((0, D // 2), (D // 2, D), (D, 2 * D)))
         widen(1)
         for half in range(2):
             cols = slice(half * 2 * D, (half + 1) * 2 * D)
             empty_turned(turn(a_sb[:, cols], "h"), a_values[:, cols])
-        for i in range(2):
-            turn_x(i)
-            empty_x(i)
+        turn_x(0)
+        empty_x(0)
+        nc.scalar.activation(out=coef[:], in_=lw_col[:], func=ACT.Copy, scale=ALPHA_OVER_RANK)
+        turn_x(1)
+        empty_x(1)
         nc.vector.quantize_mx(out=a_codes[:].bitcast(FP8X4), scales=a_scales[:], in_=a_values[:])
         nc.scalar.activation(
             out=b_values[:].rearrange("p (o t) -> p o t", t=PACK), in_=b_sb[:, :, 0:PACK], func=ACT.Copy, scale=coef[:]

@@ -74,8 +74,7 @@ def tile_replaced_compose_lora_pa_t_w4_kernel(
         nc.sync.dma_start(out=xb[0][:, 0 : 2 * D], in_=x_rows[0][:, 0 : 2 * D])
         nc.sync.dma_start(out=a_sb[:, 0 : 2 * D], in_=a_rows[:, 0 : 2 * D])
         nc.sync.dma_start(out=a_sb[:, 2 * D :], in_=a_rows[:, 2 * D :])
-        nc.sync.dma_start(out=xb[0][:, 2 * D :], in_=x_rows[0][:, 2 * D :])
-        nc.sync.dma_start(out=xb[1][:, 0 : 4 * D], in_=x_rows[1][:, 0 : 4 * D])
+        nc.sync.dma_start(out=xb[0][:, 2 * D : 6 * D], in_=x_rows[0][:, 2 * D : 6 * D])
         for q in range(PACK):
             nc.sync.dma_start(out=lw_col[q:P:PACK, :], in_=lora_weights.unsqueeze(1))
         b_rows = lora_B.rearrange("n o r -> n (o r)")
@@ -85,15 +84,16 @@ def tile_replaced_compose_lora_pa_t_w4_kernel(
                 out=b_sb[:].rearrange("p o r -> p (o r)")[q:P:PACK, 0:b_run],
                 in_=b_rows[:, PACK * q : PACK * q + b_run],
             )
-        nc.sync.dma_start(out=xb[1][:, 4 * D :], in_=x_rows[1][:, 4 * D :])
+        nc.sync.dma_start(out=xb[0][:, 6 * D :], in_=x_rows[0][:, 6 * D :])
+        nc.sync.dma_start(out=xb[1][:], in_=x_rows[1])
         nc.sync.dma_start(out=w_sb[:], in_=W_words[0])
         for q in range(4):
             nc.sync.dma_start(
                 out=w_sc[32 * q : 32 * q + 4, :].bitcast(I32), in_=W_scales[0, 4 * q : 4 * q + 4, :].bitcast(I32)
             )
-        nc.sync.dma_start(out=bias_sb[:], in_=bias.partition_broadcast(P))
         for half in range(2):
             nc.sync.dma_start(out=bias_col[:, half, 0:1], in_=bias[half * P : (half + 1) * P].unsqueeze(1))
+        nc.sync.dma_start(out=bias_sb[:], in_=bias.partition_broadcast(P))
         for c in range(2, CHUNKS):
             nc.sync.dma_start(out=xb[c][:], in_=x_rows[c])
 

@@ -25,11 +25,22 @@ CHUNKS = TOKENS // (P * 2 * CHUNK_PAIRS)
 PAIRS = TOKENS // (2 * P)
 LAST = PAIRS - 1
 
-LEAD = 3
+LEAD = 5
 H_LAG = 2
 OUT_LAG = H_LAG + 1
 CYCLE = 3
-TURNED = range(0, PAIRS - 10, CYCLE)
+TURNED = range(0, 24, 2)
+RUN = 2
+G_LEAD = 5
+G_DELAY = 0
+T_LEAD = 3
+PLAIN = range(9, 32, 2)
+TAIL = 40
+PHASE = (0,)
+EARLY = 0
+FIRST = 2
+NOW = 1
+BANKS = {"turn": 3, "h": 3, "out": 2}
 
 X_WORDS = slice(0, 2 * P)
 H_WORDS = slice(2 * P, 4 * P)
@@ -50,7 +61,7 @@ def tile_replaced_compose_lora_pa_t_w4_kernel(
         ctx.enter_context(tc.manual_schedule())
 
         def bank(kind, shape):
-            return psum.tile(shape, F32, name=kind, tag=kind, bufs={"turn": 3, "h": 3, "out": 2}[kind])
+            return psum.tile(shape, F32, name=kind, tag=kind, bufs=BANKS[kind])
 
         ident = keep.tile([P, P], F32, name="ident")
         nc.vector.memset(ident[:], 0.0)
@@ -58,6 +69,7 @@ def tile_replaced_compose_lora_pa_t_w4_kernel(
 
         xb = [keep.tile([P, 2 * CHUNK_PAIRS * D], U8, name="xb%d" % c, align_bytes=64) for c in range(CHUNKS)]
         scale_col = keep.tile([P, 2, 2], F32, name="scale_col")
+        scale4 = keep.tile([P, PACK], F32, name="scale4")
         scale = keep.tile([P, 2 * D], F32, name="scale", align_bytes=64)
         a_sb = keep.tile([P, PACK * D], BF16, name="a_sb", align_bytes=64)
         b_sb = keep.tile([P, D_OUT, RANK], BF16, name="b_sb", align_bytes=64)
@@ -86,6 +98,7 @@ def tile_replaced_compose_lora_pa_t_w4_kernel(
             )
         nc.sync.dma_start(out=xb[0][:, 6 * D :], in_=x_rows[0][:, 6 * D :])
         nc.sync.dma_start(out=xb[1][:], in_=x_rows[1])
+        nc.sync.dma_start(out=scale4[:], in_=x_scale.rearrange("a b (p t) -> p (a b t)", t=PACK))
         nc.sync.dma_start(out=w_sb[:], in_=W_words[0])
         for q in range(4):
             nc.sync.dma_start(
@@ -112,23 +125,23 @@ def tile_replaced_compose_lora_pa_t_w4_kernel(
             turned = bank(kind, [P, 2, 2, P])
             for j in range(2):
                 for u in range(2):
-                    nc.tensor.transpose(turned[:, j, u, :], words[:, 256 * j + u : 256 * (j + 1) : 2], ident[:])
+                    nc.tensor.transpose(turned[:, u, j, :], words[:, 256 * j + u : 256 * (j + 1) : 2], ident[:])
             return turned
 
         def empty_turned(turned, values):
             nc.scalar.copy(
-                out=values.bitcast(F32).rearrange("p (j r u) -> p j r u", j=2, u=2),
-                in_=turned[:].rearrange("p j u r -> p j r u"),
+                out=values.bitcast(F32).rearrange("p (n u) -> p n u", u=2),
+                in_=turned[:].rearrange("p u j r -> p (j r) u"),
             )
 
         def values_of(s):
             if s not in step_values:
-                step_values[s] = work.tile([P, 4 * D], BF16, name="values", tag="values", bufs=LEAD + 1, align_bytes=64)
+                step_values[s] = work.tile([P, 4 * D], BF16, name="values", tag="values", bufs=10, align_bytes=64)
             return step_values[s]
 
         def widen(i, parts=((0, 2 * D),)):
             c, q = divmod(i, CHUNK_PAIRS)
-            xw = work.tile([P, 2 * D], BF16, name="xw", tag="xw", bufs=LEAD + 1, align_bytes=64)
+            xw = work.tile([P, 2 * D], BF16, name="xw", tag="xw", bufs=LEAD + 2, align_bytes=64)
             for lo, hi in parts:
                 nc.vector.tensor_tensor(
                     out=xw[:, lo:hi],
@@ -137,6 +150,20 @@ def tile_replaced_compose_lora_pa_t_w4_kernel(
                     op=ALU.mult,
                 )
             widened[i] = xw
+
+        def widen_plain(i, s):
+            c, q = divmod(i, CHUNK_PAIRS)
+            xw = step_values[s][:, 0 : 2 * D]
+            nc.gpsimd.tensor_copy(out=xw, in_=xb[c][:, q * 2 * D : (q + 1) * 2 * D].bitcast(FP8))
+            widened[i] = xw
+
+        def scale_x(i):
+            nc.vector.tensor_tensor(
+                out=values_of(i)[:, 0 : 2 * D].rearrange("p (n u e) -> p n u e", u=2, e=2),
+                in0=x_banks.pop(i)[:].bitcast(BF16).rearrange("p u j (r e) -> p (j r) u e", e=2),
+                in1=scale4[:].rearrange("p (u e) -> p u e", e=2).unsqueeze(1).to_broadcast([P, 2 * P, 2, 2]),
+                op=ALU.mult,
+            )
 
         def turn_x(i):
             x_banks[i] = turn(widened.pop(i)[:], "turn")
@@ -283,50 +310,68 @@ def tile_replaced_compose_lora_pa_t_w4_kernel(
         )
 
         next_pair = 2
-        to_turn = []
-        for s in range(LAST):
-            quantise(s, ALL_WORDS if s >= H_LAG else X_WORDS)
+        to_turn, to_back, later = [], [], []
+        for s in range(LAST + H_LAG):
+            if s < LAST:
+                quantise(s, ALL_WORDS if s >= H_LAG else X_WORDS)
+            else:
+                quantise(s, H_WORDS)
             if s + 1 == LAST:
                 quantise(LAST, X_WORDS)
-            fresh = range(next_pair, min(PAIRS, s + LEAD + 1))
-            next_pair = fresh.stop
+            if s + G_LEAD in PLAIN:
+                widen_plain(s + G_LEAD, s)
+            if s - G_DELAY + G_LEAD in PLAIN:
+                to_turn[:0] = [s - G_DELAY + G_LEAD]
+            if s + T_LEAD in PLAIN:
+                scale_x(s + T_LEAD)
+            fresh = [i for i in range(next_pair, min(PAIRS, s + LEAD + 1, 2 * s + 4)) if i not in PLAIN]
+            next_pair = min(PAIRS, s + LEAD + 1, 2 * s + 4)
             for i in fresh:
                 widen(i)
             if s + 1 == H_LAG:
                 nc.vector.quantize_mx(out=b_codes[:].bitcast(FP8X4), scales=b_scales[:], in_=b_values[:])
             if s >= OUT_LAG and s - OUT_LAG not in TURNED:
                 finish(s - OUT_LAG)
-            make_h(s)
-            empty_h(s)
+            if s <= LAST:
+                make_h(s)
+            if EARLY:
+                for job, i in later[:EARLY]:
+                    job(i)
+                later[:] = later[EARLY:]
+            if s <= LAST:
+                empty_h(s)
             if s >= H_LAG:
                 make_out(s - H_LAG)
             if s - H_LAG in TURNED:
                 add_bias_turned(s - H_LAG)
+                to_back.append(s - H_LAG)
+            for job, i in later:
+                job(i)
+            later.clear()
             to_turn.extend(fresh)
-            if s % CYCLE != H_LAG:
+            if s % RUN in PHASE or s >= TAIL or s < FIRST:
+                jobs = []
                 for i in to_turn:
                     turn_x(i)
-                    if i == to_turn[-1] and s - OUT_LAG in TURNED:
-                        turn_back(s - OUT_LAG)
-                    empty_x(i)
+                    if i not in PLAIN:
+                        jobs.append((empty_x, i))
+                for i in to_back:
+                    if i < s - H_LAG:
+                        turn_back(i)
+                        jobs.append((finish_turned, i))
+                to_back[:] = [i for i in to_back if i == s - H_LAG]
                 to_turn.clear()
-                if s - OUT_LAG in TURNED:
-                    finish_turned(s - OUT_LAG)
+                for job, i in jobs[:NOW]:
+                    job(i)
+                later.extend(jobs[NOW:])
 
-        make_h(LAST)
-        empty_h(LAST)
-        quantise(LAST, H_WORDS)
-        finish(LAST - 3)
-        make_out(LAST - 2)
-        quantise(LAST + 1, H_WORDS)
-        make_out(LAST - 1)
         last_result = result_tile()
         last_banks = []
         for j in range(2):
             quantise(LAST + H_LAG, slice(H_WORDS.start + j * P, H_WORDS.start + (j + 1) * P))
             last_banks.append(bank("h", [P, D_OUT]))
             out_tile(LAST, j, last_banks[j][:])
-            finish(LAST - 2 + j)
+        finish(LAST - 1)
         for j in range(2):
             nc.vector.tensor_tensor(out=last_result[:, j, :], in0=last_banks[j][:], in1=bias_sb[:], op=ALU.add)
             nc.sync.dma_start(out=out_view(LAST)[:, j, :], in_=last_result[:, j, :])

@@ -25,26 +25,16 @@ CHUNKS = TOKENS // (P * 2 * CHUNK_PAIRS)
 PAIRS = TOKENS // (2 * P)
 LAST = PAIRS - 1
 
-LEAD = 5
-H_LAG = 2
-OUT_LAG = H_LAG + 1
-CYCLE = 3
-TURNED = range(0, 24, 2)
-RUN = 2
-G_LEAD = 5
-G_DELAY = 0
-T_LEAD = 3
-PLAIN = range(9, 32, 2)
-TAIL = 40
-PHASE = (0,)
-EARLY = 0
-FIRST = 2
-NOW = 1
-BANKS = {"turn": 3, "h": 3, "out": 2}
-
-X_WORDS = slice(0, 2 * P)
-H_WORDS = slice(2 * P, 4 * P)
-ALL_WORDS = slice(0, 4 * P)
+ROUNDS = PAIRS // 2
+LAG_A = 1
+LAG_B = 2
+TURNED = [i for i in range(25) if i % 2 == 0 or i % 6 == 3]
+BANKS = {"turn": 2, "h": 2, "out": 4}
+ORDER = "c"
+BPOS = 0
+FIN = 2
+SPARE = 384
+MID = 0
 
 
 def tile_replaced_compose_lora_pa_t_w4_kernel(
@@ -68,9 +58,8 @@ def tile_replaced_compose_lora_pa_t_w4_kernel(
         make_identity(nc, ident[:], nomemset=True)
 
         xb = [keep.tile([P, 2 * CHUNK_PAIRS * D], U8, name="xb%d" % c, align_bytes=64) for c in range(CHUNKS)]
-        scale_col = keep.tile([P, 2, 2], F32, name="scale_col")
-        scale4 = keep.tile([P, PACK], F32, name="scale4")
-        scale = keep.tile([P, 2 * D], F32, name="scale", align_bytes=64)
+        scale_col = keep.tile([P, PACK], F32, name="scale_col")
+        first = keep.tile([P, 8 * D], BF16, name="first", align_bytes=64)
         a_sb = keep.tile([P, PACK * D], BF16, name="a_sb", align_bytes=64)
         b_sb = keep.tile([P, D_OUT, RANK], BF16, name="b_sb", align_bytes=64)
         w_sb = keep.tile([P, 2 * D_OUT], U8, name="w_sb", align_bytes=64)
@@ -82,11 +71,13 @@ def tile_replaced_compose_lora_pa_t_w4_kernel(
 
         nc.vector.memset(w_sc[:].bitcast(I32), 0)
         a_rows = lora_A.rearrange("n r d -> (n r) d").rearrange("(m t) d -> m (t d)", t=PACK)
-        nc.sync.dma_start(out=scale_col[:], in_=x_scale.rearrange("a b (h p e) -> p (a b h) e", h=2, e=2))
         nc.sync.dma_start(out=xb[0][:, 0 : 2 * D], in_=x_rows[0][:, 0 : 2 * D])
+        nc.sync.dma_start(out=xb[0][:, 2 * D : 4 * D], in_=x_rows[0][:, 2 * D : 4 * D])
+        nc.sync.dma_start(out=scale_col[:], in_=x_scale.rearrange("a b (p t) -> p (a b t)", t=PACK))
+        nc.sync.dma_start(out=xb[0][:, 4 * D :], in_=x_rows[0][:, 4 * D :])
         nc.sync.dma_start(out=a_sb[:, 0 : 2 * D], in_=a_rows[:, 0 : 2 * D])
         nc.sync.dma_start(out=a_sb[:, 2 * D :], in_=a_rows[:, 2 * D :])
-        nc.sync.dma_start(out=xb[0][:, 2 * D : 6 * D], in_=x_rows[0][:, 2 * D : 6 * D])
+        nc.sync.dma_start(out=xb[1][:, 0 : 4 * D], in_=x_rows[1][:, 0 : 4 * D])
         for q in range(PACK):
             nc.sync.dma_start(out=lw_col[q:P:PACK, :], in_=lora_weights.unsqueeze(1))
         b_rows = lora_B.rearrange("n o r -> n (o r)")
@@ -96,9 +87,7 @@ def tile_replaced_compose_lora_pa_t_w4_kernel(
                 out=b_sb[:].rearrange("p o r -> p (o r)")[q:P:PACK, 0:b_run],
                 in_=b_rows[:, PACK * q : PACK * q + b_run],
             )
-        nc.sync.dma_start(out=xb[0][:, 6 * D :], in_=x_rows[0][:, 6 * D :])
-        nc.sync.dma_start(out=xb[1][:], in_=x_rows[1])
-        nc.sync.dma_start(out=scale4[:], in_=x_scale.rearrange("a b (p t) -> p (a b t)", t=PACK))
+        nc.sync.dma_start(out=xb[1][:, 4 * D :], in_=x_rows[1][:, 4 * D :])
         nc.sync.dma_start(out=w_sb[:], in_=W_words[0])
         for q in range(4):
             nc.sync.dma_start(
@@ -117,8 +106,14 @@ def tile_replaced_compose_lora_pa_t_w4_kernel(
         a_values = keep.tile([P, PACK * NR], BF16, name="a_values", align_bytes=64)
         b_values = keep.tile([P, PACK * D_OUT], BF16, name="b_values", align_bytes=64)
 
-        widened, x_banks, h_banks, out_banks, biased, back_banks = {}, {}, {}, {}, {}, {}
-        step_values, step_codes = {}, {}
+        plain, x_banks, h_banks, out_banks, biased, back_banks = {}, {}, {}, {}, {}, {}
+        round_values, round_codes = {}, {}
+
+        def x_place(i):
+            return i // 2 + 1, i % 2
+
+        def h_place(i):
+            return x_place(i)[0] + (LAG_B if i % 2 else LAG_A), 2 + i % 2
 
         def turn(rows, kind):
             words = rows.bitcast(F32)
@@ -134,54 +129,39 @@ def tile_replaced_compose_lora_pa_t_w4_kernel(
                 in_=turned[:].rearrange("p u j r -> p (j r) u"),
             )
 
-        def values_of(s):
-            if s not in step_values:
-                step_values[s] = work.tile([P, 4 * D], BF16, name="values", tag="values", bufs=10, align_bytes=64)
-            return step_values[s]
+        def values_at(place):
+            r, q = place
+            if r not in round_values:
+                round_values[r] = work.tile([P, 8 * D], BF16, name="values", tag="values", bufs=5, align_bytes=64)
+            return round_values[r][:, q * 2 * D : (q + 1) * 2 * D]
 
-        def widen(i, parts=((0, 2 * D),)):
-            c, q = divmod(i, CHUNK_PAIRS)
-            xw = work.tile([P, 2 * D], BF16, name="xw", tag="xw", bufs=LEAD + 2, align_bytes=64)
-            for lo, hi in parts:
-                nc.vector.tensor_tensor(
-                    out=xw[:, lo:hi],
-                    in0=xb[c][:, q * 2 * D + lo : q * 2 * D + hi].bitcast(FP8),
-                    in1=scale[:, lo % D : lo % D + hi - lo],
-                    op=ALU.mult,
-                )
-            widened[i] = xw
+        def widen(engine, first_pair, dst, lo, hi):
+            c, q = divmod(first_pair, CHUNK_PAIRS)
+            engine.tensor_copy(out=dst[:, lo:hi], in_=xb[c][:, q * 2 * D + lo : q * 2 * D + hi].bitcast(FP8))
+            plain[first_pair], plain[first_pair + 1] = dst[:, 0 : 2 * D], dst[:, 2 * D : 4 * D]
 
-        def widen_plain(i, s):
-            c, q = divmod(i, CHUNK_PAIRS)
-            xw = step_values[s][:, 0 : 2 * D]
-            nc.gpsimd.tensor_copy(out=xw, in_=xb[c][:, q * 2 * D : (q + 1) * 2 * D].bitcast(FP8))
-            widened[i] = xw
+        def turn_x(i):
+            x_banks[i] = turn(plain.pop(i), "turn")
 
-        def scale_x(i):
+        def scale_after(i):
             nc.vector.tensor_tensor(
-                out=values_of(i)[:, 0 : 2 * D].rearrange("p (n u e) -> p n u e", u=2, e=2),
+                out=values_at(x_place(i)).rearrange("p (n u e) -> p n u e", u=2, e=2),
                 in0=x_banks.pop(i)[:].bitcast(BF16).rearrange("p u j (r e) -> p (j r) u e", e=2),
-                in1=scale4[:].rearrange("p (u e) -> p u e", e=2).unsqueeze(1).to_broadcast([P, 2 * P, 2, 2]),
+                in1=scale_col[:].rearrange("p (u e) -> p u e", e=2).unsqueeze(1).to_broadcast([P, 2 * P, 2, 2]),
                 op=ALU.mult,
             )
 
-        def turn_x(i):
-            x_banks[i] = turn(widened.pop(i)[:], "turn")
-
-        def empty_x(i):
-            empty_turned(x_banks.pop(i), values_of(i)[:, 0 : 2 * D])
-
-        def quantise(s, words):
-            if s not in step_codes:
-                step_codes[s] = (
-                    work.tile([P, 4 * P], U32, name="codes", tag="codes", bufs=H_LAG + 3, align_bytes=64),
-                    work.tile([P, 4 * P], U8, name="scales", tag="scales", bufs=H_LAG + 3, align_bytes=64),
+        def quantise(r, lo, hi):
+            if r not in round_codes:
+                round_codes[r] = (
+                    work.tile([P, 8 * P], U32, name="codes", tag="codes", bufs=5, align_bytes=64),
+                    work.tile([P, 8 * P], U8, name="scales", tag="scales", bufs=5, align_bytes=64),
                 )
-            codes, scales = step_codes[s]
+            codes, scales = round_codes[r]
             nc.vector.quantize_mx(
-                out=codes[:, words].bitcast(FP8X4),
-                scales=scales[:, words],
-                in_=step_values[s][:, PACK * words.start : PACK * words.stop],
+                out=codes[:, lo:hi].bitcast(FP8X4),
+                scales=scales[:, lo:hi],
+                in_=round_values[r][:, PACK * lo : PACK * hi],
             )
 
         def mx(acc, stationary, moving, start, stop):
@@ -199,10 +179,12 @@ def tile_replaced_compose_lora_pa_t_w4_kernel(
             return codes[:, lo : lo + width].bitcast(FP8X4), scales[:, lo : lo + width]
 
         def x_cols(i, j):
-            return e4m3(*step_codes[i], j * P, P)
+            r, q = x_place(i)
+            return e4m3(*round_codes[r], (2 * q + j) * P, P)
 
         def h_cols(i, j, tiles):
-            return e4m3(*step_codes[i + H_LAG], H_WORDS.start + j * P, tiles * P)
+            r, q = h_place(i)
+            return e4m3(*round_codes[r], (2 * q + j) * P, tiles * P)
 
         def w_cols(half):
             return w_sb[:, half * 2 * P : (half + 1) * 2 * P].bitcast(FP4X4), w_sc[:, half * P : (half + 1) * P]
@@ -216,10 +198,10 @@ def tile_replaced_compose_lora_pa_t_w4_kernel(
                 h_banks[i].append(acc)
 
         def empty_h(i):
-            values = values_of(i + H_LAG)
+            values = values_at(h_place(i))
             for j, acc in enumerate(h_banks.pop(i)):
                 nc.scalar.copy(
-                    out=values[:, (2 + j) * NR : (3 + j) * NR].rearrange("p (r t) -> p r t", t=PACK),
+                    out=values[:, j * NR : (j + 1) * NR].rearrange("p (r t) -> p r t", t=PACK),
                     in_=acc[:].rearrange("p t r -> p r t"),
                 )
 
@@ -233,8 +215,8 @@ def tile_replaced_compose_lora_pa_t_w4_kernel(
             for j in range(2):
                 mx(acc[:, j * P : (j + 1) * P], w_cols(half), x_cols(i, j), False, j == 1)
 
-        def make_out(i):
-            out_banks[i] = bank("out", [P, 2, D_OUT])
+        def make_out(i, kind="out"):
+            out_banks[i] = bank(kind, [P, 2, D_OUT])
             for side in range(2):
                 (out_half_turned if i in TURNED else out_tile)(i, side, out_banks[i][:, side, :])
 
@@ -256,8 +238,8 @@ def tile_replaced_compose_lora_pa_t_w4_kernel(
             nc.sync.dma_start(out=out_view(i), in_=result[:])
 
         def add_bias_turned(i):
-            acc = out_banks.pop(i)
-            biased[i] = work.tile([P, 2, 2 * P], F32, name="biased", tag="biased", bufs=3, align_bytes=64)
+            acc = out_banks[i]
+            biased[i] = work.tile([P, 2, 2 * P], F32, name="biased", tag="biased", bufs=4, align_bytes=64)
             for half in range(2):
                 nc.scalar.activation(
                     out=biased[i][:, half, :],
@@ -269,7 +251,7 @@ def tile_replaced_compose_lora_pa_t_w4_kernel(
 
         def turn_back(i):
             sums = biased.pop(i)
-            back_banks[i] = bank("turn", [P, 2, D_OUT])
+            back_banks[i] = out_banks.pop(i)
             for j in range(2):
                 for half in range(2):
                     nc.tensor.transpose(
@@ -281,97 +263,158 @@ def tile_replaced_compose_lora_pa_t_w4_kernel(
             nc.scalar.copy(out=result[:], in_=back_banks.pop(i)[:])
             nc.sync.dma_start(out=out_view(i), in_=result[:])
 
-        scale_banks = []
-        for half in range(2):
-            spread = bank("out", [P, 2, P])
-            for e in range(2):
-                nc.tensor.transpose(spread[:, e, :], scale_col[:, half, e : e + 1].to_broadcast([P, P]), ident[:])
-            scale_banks.append(spread)
-        for j in range(2):
-            for half in range(2):
-                lo = j * D + half * D // 2
-                nc.scalar.copy(
-                    out=scale[:, lo : lo + D // 2].rearrange("p (n e) -> p n e", e=2),
-                    in_=scale_banks[half][:].rearrange("p e n -> p n e"),
-                )
-        widen(0, parts=((0, D // 2), (D // 2, D), (D, 2 * D)))
-        widen(1)
+        widen(nc.vector, 0, first[:, 0 : 4 * D], 0, 2 * D)
+        widen(nc.vector, 0, first[:, 0 : 4 * D], 2 * D, 4 * D)
+        widen(nc.gpsimd, 2, first[:, 4 * D :], 0, 4 * D)
+        turn_x(0)
+        turn_x(1)
         for half in range(2):
             cols = slice(half * 2 * D, (half + 1) * 2 * D)
             empty_turned(turn(a_sb[:, cols], "h"), a_values[:, cols])
-        turn_x(0)
-        empty_x(0)
-        nc.scalar.activation(out=coef[:], in_=lw_col[:], func=ACT.Copy, scale=ALPHA_OVER_RANK)
-        turn_x(1)
-        empty_x(1)
+        scale_after(0)
+        scale_after(1)
         nc.vector.quantize_mx(out=a_codes[:].bitcast(FP8X4), scales=a_scales[:], in_=a_values[:])
-        nc.scalar.activation(
-            out=b_values[:].rearrange("p (o t) -> p o t", t=PACK), in_=b_sb[:, :, 0:PACK], func=ACT.Copy, scale=coef[:]
-        )
 
-        next_pair = 2
-        to_turn, to_back, later = [], [], []
-        for s in range(LAST + H_LAG):
-            if s < LAST:
-                quantise(s, ALL_WORDS if s >= H_LAG else X_WORDS)
-            else:
-                quantise(s, H_WORDS)
-            if s + 1 == LAST:
-                quantise(LAST, X_WORDS)
-            if s + G_LEAD in PLAIN:
-                widen_plain(s + G_LEAD, s)
-            if s - G_DELAY + G_LEAD in PLAIN:
-                to_turn[:0] = [s - G_DELAY + G_LEAD]
-            if s + T_LEAD in PLAIN:
-                scale_x(s + T_LEAD)
-            fresh = [i for i in range(next_pair, min(PAIRS, s + LEAD + 1, 2 * s + 4)) if i not in PLAIN]
-            next_pair = min(PAIRS, s + LEAD + 1, 2 * s + 4)
-            for i in fresh:
-                widen(i)
-            if s + 1 == H_LAG:
+        def make_bc():
+            nc.scalar.activation(out=coef[:], in_=lw_col[:], func=ACT.Copy, scale=ALPHA_OVER_RANK)
+            nc.scalar.activation(
+                out=b_values[:].rearrange("p (o t) -> p o t", t=PACK),
+                in_=b_sb[:, :, 0:PACK],
+                func=ACT.Copy,
+                scale=coef[:],
+            )
+
+        if BPOS == 0:
+            make_bc()
+        x_at = {x_place(i): i for i in range(PAIRS)}
+        h_at = {h_place(i): i for i in range(PAIRS)}
+        to_finish, to_back = [], []
+        for r in range(1, ROUNDS):
+            filled = [q for q in range(4) if (r, q) in x_at or (r, q) in h_at]
+            if r == 2:
                 nc.vector.quantize_mx(out=b_codes[:].bitcast(FP8X4), scales=b_scales[:], in_=b_values[:])
-            if s >= OUT_LAG and s - OUT_LAG not in TURNED:
-                finish(s - OUT_LAG)
-            if s <= LAST:
-                make_h(s)
-            if EARLY:
-                for job, i in later[:EARLY]:
-                    job(i)
-                later[:] = later[EARLY:]
-            if s <= LAST:
-                empty_h(s)
-            if s >= H_LAG:
-                make_out(s - H_LAG)
-            if s - H_LAG in TURNED:
-                add_bias_turned(s - H_LAG)
-                to_back.append(s - H_LAG)
-            for job, i in later:
-                job(i)
-            later.clear()
-            to_turn.extend(fresh)
-            if s % RUN in PHASE or s >= TAIL or s < FIRST:
-                jobs = []
-                for i in to_turn:
-                    turn_x(i)
-                    if i not in PLAIN:
-                        jobs.append((empty_x, i))
-                for i in to_back:
-                    if i < s - H_LAG:
-                        turn_back(i)
-                        jobs.append((finish_turned, i))
-                to_back[:] = [i for i in to_back if i == s - H_LAG]
-                to_turn.clear()
-                for job, i in jobs[:NOW]:
-                    job(i)
-                later.extend(jobs[NOW:])
+            if len(filled) == 4:
+                quantise(r, 0, 8 * P)
+            else:
+                for q in filled[2:]:
+                    quantise(r, q * 2 * P, (q + 1) * 2 * P)
+                quantise(r, filled[0] * 2 * P, (filled[:2][-1] + 1) * 2 * P)
+            cut = 4 * D if to_finish else 4 * D - SPARE
+            if r + 1 < ROUNDS:
+                widen(nc.gpsimd, 2 * r + 2, round_values[r], 0, cut)
+            turn_x(2 * r)
+            turn_x(2 * r + 1)
+            if r + 1 == ROUNDS:
+                break
+            backs = list(to_back)
+            to_back.clear()
+            for i in backs[:1]:
+                turn_back(i)
+            if ORDER in "cd":
+                for i in backs[:1]:
+                    finish_turned(i)
+            for i in backs[1:]:
+                turn_back(i)
+            fins = list(to_finish)
+            to_finish.clear()
+            scal = [2 * r, 2 * r + 1] if r < ROUNDS else []
+            for i in scal[:FIN]:
+                scale_after(i)
+            for i in fins:
+                finish(i)
+            for i in scal[FIN:]:
+                scale_after(i)
+            if cut < 4 * D:
+                widen(nc.vector, 2 * r + 2, round_values[r], cut, 4 * D)
+            hs = [x_at[r, q] for q in range(2) if (r, q) in x_at]
+            outs = [h_at[r, q] for q in (2, 3) if (r, q) in h_at]
+            outs = [i for i in outs if i not in TURNED] + [i for i in outs if i in TURNED]
+            if ORDER in "bd":
+                outs = outs[::-1]
+            for i in hs[:1]:
+                make_h(i)
+                empty_h(i)
+            if r == 1 and BPOS == 1:
+                make_bc()
+            for i in backs[1 if ORDER in "cd" else 0 :]:
+                finish_turned(i)
+            for n, i in enumerate(outs):
+                make_out(i)
+                if i in TURNED:
+                    add_bias_turned(i)
+                    to_back.append(i)
+                else:
+                    to_finish.append(i)
+                if n == 0 and MID:
+                    for k in hs[1:]:
+                        make_h(k)
+                        empty_h(k)
+                    hs = []
+            for i in hs[1:]:
+                make_h(i)
+                empty_h(i)
+            if r == 1 and BPOS == 2:
+                make_bc()
 
+        def quantise_at(place):
+            quantise(place[0], place[1] * 2 * P, (place[1] + 1) * 2 * P)
+
+        def h_stage(i):
+            make_h(i)
+            empty_h(i)
+
+        def out_stage(i, kind="out"):
+            make_out(i, kind)
+            if i in TURNED:
+                add_bias_turned(i)
+
+        def back_stage(i):
+            if i in TURNED:
+                turn_back(i)
+                finish_turned(i)
+
+        def end_stage(i):
+            if i not in TURNED:
+                finish(i)
+
+        for i in to_back:
+            back_stage(i)
+        h_stage(LAST - 3)
+        scale_after(LAST - 1)
+        quantise_at(h_place(LAST - 4))
+        for i in to_finish:
+            finish(i)
+        out_stage(LAST - 6)
+        out_stage(LAST - 5)
+        quantise_at(x_place(LAST - 1))
+        h_stage(LAST - 2)
+        scale_after(LAST)
+        quantise_at(h_place(LAST - 3))
+        quantise_at(x_place(LAST))
+        end_stage(LAST - 6)
+        out_stage(LAST - 4)
+        h_stage(LAST - 1)
+        quantise_at(h_place(LAST - 2))
+        end_stage(LAST - 5)
+        out_stage(LAST - 3)
+        h_stage(LAST)
+        back_stage(LAST - 6)
+        back_stage(LAST - 5)
+        back_stage(LAST - 4)
+        end_stage(LAST - 4)
+        quantise_at(h_place(LAST - 1))
+        out_stage(LAST - 2)
+        end_stage(LAST - 3)
+        out_stage(LAST - 1)
+        back_stage(LAST - 3)
         last_result = result_tile()
         last_banks = []
+        r, q = h_place(LAST)
         for j in range(2):
-            quantise(LAST + H_LAG, slice(H_WORDS.start + j * P, H_WORDS.start + (j + 1) * P))
+            quantise(r, (2 * q + j) * P, (2 * q + j + 1) * P)
             last_banks.append(bank("h", [P, D_OUT]))
             out_tile(LAST, j, last_banks[j][:])
-        finish(LAST - 1)
+            finish(LAST - 2 + j)
         for j in range(2):
             nc.vector.tensor_tensor(out=last_result[:, j, :], in0=last_banks[j][:], in1=bias_sb[:], op=ALU.add)
             nc.sync.dma_start(out=out_view(LAST)[:, j, :], in_=last_result[:, j, :])

@@ -28,10 +28,16 @@ LAST = PAIRS - 1
 ROUNDS = PAIRS // 2
 LAG_A = 1
 LAG_B = 2
-TURNED = [i for i in range(25) if i % 2 == 0 or i % 6 == 3]
-BANKS = {"turn": 2, "h": 2, "out": 4}
-ORDER = "c"
+TURNED = range(0, 23, 2)
+BANKS = {"turn": 2, "h": 3, "out": 3}
+ORDER = "d"
+BQ = 2
+SD = 256
+LATE = (23, 24)
+TAIL = "h28 s30 s31 o25 o26 f25 x30 x31 q27 q28 h29 h30 f26 o27 q29 o28 h31 f27 q30 o29 f28 o30"
 BPOS = 0
+LOADS = "01s2aA4lb6"
+HEAD = "01aAsSq"
 FIN = 2
 SPARE = 384
 MID = 0
@@ -71,23 +77,40 @@ def tile_replaced_compose_lora_pa_t_w4_kernel(
 
         nc.vector.memset(w_sc[:].bitcast(I32), 0)
         a_rows = lora_A.rearrange("n r d -> (n r) d").rearrange("(m t) d -> m (t d)", t=PACK)
-        nc.sync.dma_start(out=xb[0][:, 0 : 2 * D], in_=x_rows[0][:, 0 : 2 * D])
-        nc.sync.dma_start(out=xb[0][:, 2 * D : 4 * D], in_=x_rows[0][:, 2 * D : 4 * D])
-        nc.sync.dma_start(out=scale_col[:], in_=x_scale.rearrange("a b (p t) -> p (a b t)", t=PACK))
-        nc.sync.dma_start(out=xb[0][:, 4 * D :], in_=x_rows[0][:, 4 * D :])
-        nc.sync.dma_start(out=a_sb[:, 0 : 2 * D], in_=a_rows[:, 0 : 2 * D])
-        nc.sync.dma_start(out=a_sb[:, 2 * D :], in_=a_rows[:, 2 * D :])
-        nc.sync.dma_start(out=xb[1][:, 0 : 4 * D], in_=x_rows[1][:, 0 : 4 * D])
-        for q in range(PACK):
-            nc.sync.dma_start(out=lw_col[q:P:PACK, :], in_=lora_weights.unsqueeze(1))
         b_rows = lora_B.rearrange("n o r -> n (o r)")
         b_run = RANK * D_OUT - (RANK - PACK)
-        for q in range(PACK):
-            nc.sync.dma_start(
-                out=b_sb[:].rearrange("p o r -> p (o r)")[q:P:PACK, 0:b_run],
-                in_=b_rows[:, PACK * q : PACK * q + b_run],
-            )
-        nc.sync.dma_start(out=xb[1][:, 4 * D :], in_=x_rows[1][:, 4 * D :])
+
+        def load_x(first_pair, pairs):
+            c, q = divmod(first_pair, CHUNK_PAIRS)
+            cols = slice(q * 2 * D, (q + pairs) * 2 * D)
+            nc.sync.dma_start(out=xb[c][:, cols], in_=x_rows[c][:, cols])
+
+        for what in LOADS:
+            if what == "0":
+                load_x(0, 1)
+            if what == "1":
+                load_x(1, 1)
+            if what == "2":
+                load_x(2, 2)
+            if what == "4":
+                load_x(4, 2)
+            if what == "6":
+                load_x(6, 2)
+            if what == "s":
+                nc.sync.dma_start(out=scale_col[:], in_=x_scale.rearrange("a b (p t) -> p (a b t)", t=PACK))
+            if what == "a":
+                nc.sync.dma_start(out=a_sb[:, 0 : 2 * D], in_=a_rows[:, 0 : 2 * D])
+            if what == "A":
+                nc.sync.dma_start(out=a_sb[:, 2 * D :], in_=a_rows[:, 2 * D :])
+            if what == "l":
+                for q in range(PACK):
+                    nc.sync.dma_start(out=lw_col[q:P:PACK, :], in_=lora_weights.unsqueeze(1))
+            if what == "b":
+                for q in range(PACK):
+                    nc.sync.dma_start(
+                        out=b_sb[:].rearrange("p o r -> p (o r)")[q:P:PACK, 0:b_run],
+                        in_=b_rows[:, PACK * q : PACK * q + b_run],
+                    )
         nc.sync.dma_start(out=w_sb[:], in_=W_words[0])
         for q in range(4):
             nc.sync.dma_start(
@@ -263,17 +286,36 @@ def tile_replaced_compose_lora_pa_t_w4_kernel(
             nc.scalar.copy(out=result[:], in_=back_banks.pop(i)[:])
             nc.sync.dma_start(out=out_view(i), in_=result[:])
 
-        widen(nc.vector, 0, first[:, 0 : 4 * D], 0, 2 * D)
-        widen(nc.vector, 0, first[:, 0 : 4 * D], 2 * D, 4 * D)
-        widen(nc.gpsimd, 2, first[:, 4 * D :], 0, 4 * D)
-        turn_x(0)
-        turn_x(1)
-        for half in range(2):
+        def quantise_at(place):
+            quantise(place[0], place[1] * 2 * P, (place[1] + 1) * 2 * P)
+
+        def turn_a(half):
             cols = slice(half * 2 * D, (half + 1) * 2 * D)
             empty_turned(turn(a_sb[:, cols], "h"), a_values[:, cols])
-        scale_after(0)
-        scale_after(1)
-        nc.vector.quantize_mx(out=a_codes[:].bitcast(FP8X4), scales=a_scales[:], in_=a_values[:])
+
+        widen(nc.vector, 0, first[:, 0 : 4 * D], 0, D)
+        nc.scalar.copy(out=first[:, D : 2 * D], in_=xb[0][:, D : 2 * D].bitcast(FP8))
+        widen(nc.vector, 0, first[:, 0 : 4 * D], 2 * D, 4 * D)
+        widen(nc.gpsimd, 2, first[:, 4 * D :], 0, 4 * D)
+        for what in HEAD:
+            if what == "0":
+                turn_x(0)
+            if what == "1":
+                turn_x(1)
+            if what == "a":
+                turn_a(0)
+            if what == "A":
+                turn_a(1)
+            if what == "s":
+                scale_after(0)
+            if what == "S":
+                scale_after(1)
+            if what == "q":
+                nc.vector.quantize_mx(out=a_codes[:].bitcast(FP8X4), scales=a_scales[:], in_=a_values[:])
+            if what == "x":
+                quantise_at(x_place(0))
+            if what == "h":
+                make_h(0)
 
         def make_bc():
             nc.scalar.activation(out=coef[:], in_=lw_col[:], func=ACT.Copy, scale=ALPHA_OVER_RANK)
@@ -286,20 +328,23 @@ def tile_replaced_compose_lora_pa_t_w4_kernel(
 
         if BPOS == 0:
             make_bc()
+        sums = keep.tile([P, len(LATE), 2, D_OUT], F32, name="sums", align_bytes=64)
         x_at = {x_place(i): i for i in range(PAIRS)}
         h_at = {h_place(i): i for i in range(PAIRS)}
-        to_finish, to_back = [], []
+        to_finish, to_back, waiting = [], [], []
         for r in range(1, ROUNDS):
             filled = [q for q in range(4) if (r, q) in x_at or (r, q) in h_at]
-            if r == 2:
+            if r == BQ:
                 nc.vector.quantize_mx(out=b_codes[:].bitcast(FP8X4), scales=b_scales[:], in_=b_values[:])
-            if len(filled) == 4:
+            if r == 1 and "x" in HEAD:
+                quantise_at(x_place(1))
+            elif len(filled) == 4:
                 quantise(r, 0, 8 * P)
             else:
                 for q in filled[2:]:
                     quantise(r, q * 2 * P, (q + 1) * 2 * P)
                 quantise(r, filled[0] * 2 * P, (filled[:2][-1] + 1) * 2 * P)
-            cut = 4 * D if to_finish else 4 * D - SPARE
+            cut = 4 * D - (SD if to_finish else SPARE)
             if r + 1 < ROUNDS:
                 widen(nc.gpsimd, 2 * r + 2, round_values[r], 0, cut)
             turn_x(2 * r)
@@ -324,16 +369,26 @@ def tile_replaced_compose_lora_pa_t_w4_kernel(
                 finish(i)
             for i in scal[FIN:]:
                 scale_after(i)
-            if cut < 4 * D:
+            if not fins:
                 widen(nc.vector, 2 * r + 2, round_values[r], cut, 4 * D)
             hs = [x_at[r, q] for q in range(2) if (r, q) in x_at]
             outs = [h_at[r, q] for q in (2, 3) if (r, q) in h_at]
+            if r < BQ:
+                waiting, outs = outs, []
+            elif r == BQ:
+                outs = waiting + outs
             outs = [i for i in outs if i not in TURNED] + [i for i in outs if i in TURNED]
             if ORDER in "bd":
                 outs = outs[::-1]
             for i in hs[:1]:
-                make_h(i)
+                if i > 0 or "h" not in HEAD:
+                    make_h(i)
                 empty_h(i)
+            if fins and SD:
+                c, q = divmod(2 * r + 2, CHUNK_PAIRS)
+                nc.scalar.copy(
+                    out=round_values[r][:, cut : 4 * D], in_=xb[c][:, q * 2 * D + cut : (q + 2) * 2 * D].bitcast(FP8)
+                )
             if r == 1 and BPOS == 1:
                 make_bc()
             for i in backs[1 if ORDER in "cd" else 0 :]:
@@ -343,6 +398,8 @@ def tile_replaced_compose_lora_pa_t_w4_kernel(
                 if i in TURNED:
                     add_bias_turned(i)
                     to_back.append(i)
+                elif i in LATE:
+                    nc.scalar.copy(out=sums[:, i - LATE[0]], in_=out_banks.pop(i)[:])
                 else:
                     to_finish.append(i)
                 if n == 0 and MID:
@@ -356,8 +413,15 @@ def tile_replaced_compose_lora_pa_t_w4_kernel(
             if r == 1 and BPOS == 2:
                 make_bc()
 
-        def quantise_at(place):
-            quantise(place[0], place[1] * 2 * P, (place[1] + 1) * 2 * P)
+        late = round_values[ROUNDS - 1][:, 0 : len(LATE) * 2 * D].bitcast(F32).rearrange("p (n o) -> p n o", o=D_OUT)
+        nc.gpsimd.tensor_tensor(
+            out=late,
+            in0=sums[:].rearrange("p i j o -> p (i j) o"),
+            in1=bias_sb[:].unsqueeze(1).to_broadcast([P, 2 * len(LATE), D_OUT]),
+            op=ALU.add,
+        )
+        for n, i in enumerate(LATE):
+            nc.sync.dma_start(out=out_view(i), in_=late[:, 2 * n : 2 * n + 2, :])
 
         def h_stage(i):
             make_h(i)
@@ -379,34 +443,28 @@ def tile_replaced_compose_lora_pa_t_w4_kernel(
 
         for i in to_back:
             back_stage(i)
-        h_stage(LAST - 3)
-        scale_after(LAST - 1)
-        quantise_at(h_place(LAST - 4))
-        for i in to_finish:
-            finish(i)
-        out_stage(LAST - 6)
-        out_stage(LAST - 5)
-        quantise_at(x_place(LAST - 1))
-        h_stage(LAST - 2)
-        scale_after(LAST)
-        quantise_at(h_place(LAST - 3))
-        quantise_at(x_place(LAST))
-        end_stage(LAST - 6)
-        out_stage(LAST - 4)
-        h_stage(LAST - 1)
-        quantise_at(h_place(LAST - 2))
-        end_stage(LAST - 5)
-        out_stage(LAST - 3)
-        h_stage(LAST)
-        back_stage(LAST - 6)
-        back_stage(LAST - 5)
-        back_stage(LAST - 4)
-        end_stage(LAST - 4)
-        quantise_at(h_place(LAST - 1))
-        out_stage(LAST - 2)
-        end_stage(LAST - 3)
-        out_stage(LAST - 1)
-        back_stage(LAST - 3)
+        for word in TAIL.split():
+            what, i = word[0], int(word[1:])
+            if what == "h":
+                h_stage(i)
+            if what == "s":
+                scale_after(i)
+            if what == "x":
+                quantise_at(x_place(i))
+            if what == "q":
+                quantise_at(h_place(i))
+            if what == "o":
+                make_out(i)
+            if what == "O":
+                make_out(i, "turn")
+            if what == "a":
+                add_bias_turned(i)
+            if what == "b":
+                turn_back(i)
+            if what == "r":
+                finish_turned(i)
+            if what == "f":
+                finish(i)
         last_result = result_tile()
         last_banks = []
         r, q = h_place(LAST)

@@ -28,18 +28,18 @@ LAST = PAIRS - 1
 ROUNDS = PAIRS // 2
 LAG_A = 1
 LAG_B = 2
-TURNED = range(0, 23, 2)
+TURNED = range(0, 25, 2)
 BANKS = {"turn": 2, "h": 3, "out": 3}
 ORDER = "d"
 BQ = 2
 SD = 256
-LATE = (23, 24)
-TAIL = "h28 s30 s31 o25 o26 f25 x30 x31 q27 q28 h29 h30 f26 o27 q29 o28 h31 f27 q30 o29 f28 o30"
+LATE = (23,)
+TAIL = "G15 h28 s30 s31 o25 o26 h29 q27 x30 f25 o27 q28 x31 h30 f26 o28 q29 h31 f27 q30 o29 f28 o30"
 BPOS = 0
-LOADS = "01s2aA4lb6"
-HEAD = "01aAsSq"
+LOADS = "01s2aAl4b6"
+HEAD = "01aAsScCq"
 FIN = 2
-SPARE = 384
+SPARE = 256
 MID = 0
 
 
@@ -72,7 +72,9 @@ def tile_replaced_compose_lora_pa_t_w4_kernel(
         w_sc = keep.tile([P, D_OUT], U8, name="w_sc", align_bytes=64)
         bias_sb = keep.tile([P, D_OUT], BF16, name="bias_sb", align_bytes=64)
         bias_col = keep.tile([P, 2, 16], BF16, name="bias_col", align_bytes=64)
-        lw_col = keep.tile([P, 1], BF16, name="lw_col")
+        lw_row = keep.tile([1, NR // RANK], BF16, name="lw_row")
+        coef_row = keep.tile([P, P], F32, name="coef_row")
+        nc.vector.memset(coef_row[:], 0.0)
         coef = keep.tile([P, 1], F32, name="coef")
 
         nc.vector.memset(w_sc[:].bitcast(I32), 0)
@@ -100,11 +102,14 @@ def tile_replaced_compose_lora_pa_t_w4_kernel(
                 nc.sync.dma_start(out=scale_col[:], in_=x_scale.rearrange("a b (p t) -> p (a b t)", t=PACK))
             if what == "a":
                 nc.sync.dma_start(out=a_sb[:, 0 : 2 * D], in_=a_rows[:, 0 : 2 * D])
+            if what == "M":
+                nc.sync.dma_start(out=a_sb[:], in_=a_rows)
+            if what == "X":
+                load_x(4, 4)
             if what == "A":
                 nc.sync.dma_start(out=a_sb[:, 2 * D :], in_=a_rows[:, 2 * D :])
             if what == "l":
-                for q in range(PACK):
-                    nc.sync.dma_start(out=lw_col[q:P:PACK, :], in_=lora_weights.unsqueeze(1))
+                nc.sync.dma_start(out=lw_row[:], in_=lora_weights.unsqueeze(0))
             if what == "b":
                 for q in range(PACK):
                     nc.sync.dma_start(
@@ -316,9 +321,19 @@ def tile_replaced_compose_lora_pa_t_w4_kernel(
                 quantise_at(x_place(0))
             if what == "h":
                 make_h(0)
+            if what == "c":
+                nc.scalar.activation(
+                    out=coef_row[0:1, :].rearrange("p (n q) -> p n q", q=PACK),
+                    in_=lw_row[:].unsqueeze(2).to_broadcast([1, NR // RANK, PACK]),
+                    func=ACT.Copy,
+                    scale=ALPHA_OVER_RANK,
+                )
+            if what == "C":
+                coef_bank = bank("out", [P, P])
+                nc.tensor.transpose(coef_bank[:], coef_row[:], ident[:])
+                nc.scalar.copy(out=coef[:], in_=coef_bank[:, 0:1])
 
         def make_bc():
-            nc.scalar.activation(out=coef[:], in_=lw_col[:], func=ACT.Copy, scale=ALPHA_OVER_RANK)
             nc.scalar.activation(
                 out=b_values[:].rearrange("p (o t) -> p o t", t=PACK),
                 in_=b_sb[:, :, 0:PACK],
@@ -338,6 +353,12 @@ def tile_replaced_compose_lora_pa_t_w4_kernel(
                 nc.vector.quantize_mx(out=b_codes[:].bitcast(FP8X4), scales=b_scales[:], in_=b_values[:])
             if r == 1 and "x" in HEAD:
                 quantise_at(x_place(1))
+            elif len(filled) == 4 and r == 3:
+                quantise(r, 4 * P, 8 * P)
+                quantise(r, 0, 4 * P)
+            elif len(filled) == 4 and r == 4:
+                quantise(r, 4 * P, 8 * P)
+                quantise(r, 0, 4 * P)
             elif len(filled) == 4:
                 quantise(r, 0, 8 * P)
             else:
@@ -369,8 +390,6 @@ def tile_replaced_compose_lora_pa_t_w4_kernel(
                 finish(i)
             for i in scal[FIN:]:
                 scale_after(i)
-            if not fins:
-                widen(nc.vector, 2 * r + 2, round_values[r], cut, 4 * D)
             hs = [x_at[r, q] for q in range(2) if (r, q) in x_at]
             outs = [h_at[r, q] for q in (2, 3) if (r, q) in h_at]
             if r < BQ:
@@ -384,7 +403,7 @@ def tile_replaced_compose_lora_pa_t_w4_kernel(
                 if i > 0 or "h" not in HEAD:
                     make_h(i)
                 empty_h(i)
-            if fins and SD:
+            if True:
                 c, q = divmod(2 * r + 2, CHUNK_PAIRS)
                 nc.scalar.copy(
                     out=round_values[r][:, cut : 4 * D], in_=xb[c][:, q * 2 * D + cut : (q + 2) * 2 * D].bitcast(FP8)
@@ -413,16 +432,6 @@ def tile_replaced_compose_lora_pa_t_w4_kernel(
             if r == 1 and BPOS == 2:
                 make_bc()
 
-        late = round_values[ROUNDS - 1][:, 0 : len(LATE) * 2 * D].bitcast(F32).rearrange("p (n o) -> p n o", o=D_OUT)
-        nc.gpsimd.tensor_tensor(
-            out=late,
-            in0=sums[:].rearrange("p i j o -> p (i j) o"),
-            in1=bias_sb[:].unsqueeze(1).to_broadcast([P, 2 * len(LATE), D_OUT]),
-            op=ALU.add,
-        )
-        for n, i in enumerate(LATE):
-            nc.sync.dma_start(out=out_view(i), in_=late[:, 2 * n : 2 * n + 2, :])
-
         def h_stage(i):
             make_h(i)
             empty_h(i)
@@ -450,9 +459,35 @@ def tile_replaced_compose_lora_pa_t_w4_kernel(
             if what == "s":
                 scale_after(i)
             if what == "x":
-                quantise_at(x_place(i))
+                last = x_place(i)
+                quantise_at(last)
             if what == "q":
-                quantise_at(h_place(i))
+                last = h_place(i)
+                quantise_at(last)
+            if what == "X":
+                quantise(ROUNDS, 0, 4 * P)
+            if what == "G":
+                late = round_values[i][:, 0 : len(LATE) * 2 * D].bitcast(F32).rearrange("p (n o) -> p n o", o=D_OUT)
+                nc.gpsimd.tensor_tensor(
+                    out=late,
+                    in0=sums[:].rearrange("p i j o -> p (i j) o"),
+                    in1=bias_sb[:].unsqueeze(1).to_broadcast([P, 2 * len(LATE), D_OUT]),
+                    op=ALU.add,
+                )
+                for n, k in enumerate(LATE):
+                    nc.sync.dma_start(out=out_view(k), in_=late[:, 2 * n : 2 * n + 2, :])
+            if what == "H":
+                quantise(i, 4 * P, 8 * P)
+            if what == "Q":
+                quantise(ROUNDS, 0, 8 * P)
+            if what == "c":
+                nc.scalar.copy(out=sums[:, 0], in_=out_banks.pop(i)[:])
+            if what == "g":
+                spot = values_at(last).bitcast(F32).rearrange("p (n o) -> p n o", o=D_OUT)
+                nc.gpsimd.tensor_tensor(
+                    out=spot, in0=sums[:, 0], in1=bias_sb[:].unsqueeze(1).to_broadcast([P, 2, D_OUT]), op=ALU.add
+                )
+                nc.sync.dma_start(out=out_view(i), in_=spot)
             if what == "o":
                 make_out(i)
             if what == "O":

@@ -4,6 +4,7 @@ import concourse.mybir as mybir
 from concourse.masks import make_identity
 
 TOKENS, D, NR, D_OUT, RANK = 8192, 512, 512, 256, 16
+ADAPTERS = NR // RANK
 ALPHA_OVER_RANK = 2.0
 FLOPS = 2 * TOKENS * (D * NR + D * D_OUT + NR * D_OUT)
 
@@ -25,22 +26,16 @@ CHUNKS = TOKENS // (P * 2 * CHUNK_PAIRS)
 PAIRS = TOKENS // (2 * P)
 LAST = PAIRS - 1
 
+PAIR_COLS = 2 * D
+PAIR_WORDS = PAIR_COLS // PACK
+
 ROUNDS = PAIRS // 2
-LAG_A = 1
-LAG_B = 2
-TURNED = range(0, 25, 2)
-BANKS = {"turn": 2, "h": 3, "out": 3}
-ORDER = "d"
-BQ = 2
-SD = 256
-LATE = (23,)
-TAIL = "G15 h28 s30 s31 o25 o26 h29 q27 x30 f25 o27 q28 x31 h30 f26 o28 q29 h31 f27 q30 o29 f28 o30"
-BPOS = 0
-LOADS = "01s2aAl4b6"
-HEAD = "01aAsScCq"
-FIN = 2
-SPARE = 256
-MID = 0
+X_HALF, H_HALF = slice(0, 2 * PAIR_WORDS), slice(2 * PAIR_WORDS, 4 * PAIR_WORDS)
+ROUND_TILES = 5
+SCALAR_COLS = 256
+BIASED_TILES = 4
+TURNED = range(0, 2 * ROUNDS - 7, 2)
+GPSIMD_PAIR = 2 * ROUNDS - 9
 
 
 def tile_replaced_compose_lora_pa_t_w4_kernel(
@@ -57,7 +52,7 @@ def tile_replaced_compose_lora_pa_t_w4_kernel(
         ctx.enter_context(tc.manual_schedule())
 
         def bank(kind, shape):
-            return psum.tile(shape, F32, name=kind, tag=kind, bufs=BANKS[kind])
+            return psum.tile(shape, F32, name=kind, tag=kind, bufs={"turn": 2, "h": 3, "out": 3}[kind])
 
         ident = keep.tile([P, P], F32, name="ident")
         nc.vector.memset(ident[:], 0.0)
@@ -65,57 +60,45 @@ def tile_replaced_compose_lora_pa_t_w4_kernel(
 
         xb = [keep.tile([P, 2 * CHUNK_PAIRS * D], U8, name="xb%d" % c, align_bytes=64) for c in range(CHUNKS)]
         scale_col = keep.tile([P, PACK], F32, name="scale_col")
-        first = keep.tile([P, 8 * D], BF16, name="first", align_bytes=64)
+        first = keep.tile([P, 4 * PAIR_COLS], BF16, name="first", align_bytes=64)
         a_sb = keep.tile([P, PACK * D], BF16, name="a_sb", align_bytes=64)
         b_sb = keep.tile([P, D_OUT, RANK], BF16, name="b_sb", align_bytes=64)
         w_sb = keep.tile([P, 2 * D_OUT], U8, name="w_sb", align_bytes=64)
         w_sc = keep.tile([P, D_OUT], U8, name="w_sc", align_bytes=64)
         bias_sb = keep.tile([P, D_OUT], BF16, name="bias_sb", align_bytes=64)
         bias_col = keep.tile([P, 2, 16], BF16, name="bias_col", align_bytes=64)
-        lw_row = keep.tile([1, NR // RANK], BF16, name="lw_row")
+        lw_row = keep.tile([1, ADAPTERS], BF16, name="lw_row")
         coef_row = keep.tile([P, P], F32, name="coef_row")
         nc.vector.memset(coef_row[:], 0.0)
         coef = keep.tile([P, 1], F32, name="coef")
 
         nc.vector.memset(w_sc[:].bitcast(I32), 0)
         a_rows = lora_A.rearrange("n r d -> (n r) d").rearrange("(m t) d -> m (t d)", t=PACK)
-        b_rows = lora_B.rearrange("n o r -> n (o r)")
-        b_run = RANK * D_OUT - (RANK - PACK)
+
+        def x_part(first_pair, lo, hi):
+            c, q = divmod(first_pair, CHUNK_PAIRS)
+            return c, slice(q * PAIR_COLS + lo, q * PAIR_COLS + hi)
 
         def load_x(first_pair, pairs):
-            c, q = divmod(first_pair, CHUNK_PAIRS)
-            cols = slice(q * 2 * D, (q + pairs) * 2 * D)
+            c, cols = x_part(first_pair, 0, pairs * PAIR_COLS)
             nc.sync.dma_start(out=xb[c][:, cols], in_=x_rows[c][:, cols])
 
-        for what in LOADS:
-            if what == "0":
-                load_x(0, 1)
-            if what == "1":
-                load_x(1, 1)
-            if what == "2":
-                load_x(2, 2)
-            if what == "4":
-                load_x(4, 2)
-            if what == "6":
-                load_x(6, 2)
-            if what == "s":
-                nc.sync.dma_start(out=scale_col[:], in_=x_scale.rearrange("a b (p t) -> p (a b t)", t=PACK))
-            if what == "a":
-                nc.sync.dma_start(out=a_sb[:, 0 : 2 * D], in_=a_rows[:, 0 : 2 * D])
-            if what == "M":
-                nc.sync.dma_start(out=a_sb[:], in_=a_rows)
-            if what == "X":
-                load_x(4, 4)
-            if what == "A":
-                nc.sync.dma_start(out=a_sb[:, 2 * D :], in_=a_rows[:, 2 * D :])
-            if what == "l":
-                nc.sync.dma_start(out=lw_row[:], in_=lora_weights.unsqueeze(0))
-            if what == "b":
-                for q in range(PACK):
-                    nc.sync.dma_start(
-                        out=b_sb[:].rearrange("p o r -> p (o r)")[q:P:PACK, 0:b_run],
-                        in_=b_rows[:, PACK * q : PACK * q + b_run],
-                    )
+        load_x(0, 1)
+        load_x(1, 1)
+        nc.sync.dma_start(out=scale_col[:], in_=x_scale.rearrange("a b (p t) -> p (a b t)", t=PACK))
+        load_x(2, 2)
+        nc.sync.dma_start(out=a_sb[:, 0 : 2 * D], in_=a_rows[:, 0 : 2 * D])
+        nc.sync.dma_start(out=a_sb[:, 2 * D :], in_=a_rows[:, 2 * D :])
+        nc.sync.dma_start(out=lw_row[:], in_=lora_weights.unsqueeze(0))
+        load_x(4, 2)
+        b_rows = lora_B.rearrange("n o r -> n (o r)")
+        b_run = RANK * D_OUT - (RANK - PACK)
+        for q in range(PACK):
+            nc.sync.dma_start(
+                out=b_sb[:].rearrange("p o r -> p (o r)")[q:P:PACK, 0:b_run],
+                in_=b_rows[:, PACK * q : PACK * q + b_run],
+            )
+        load_x(6, 2)
         nc.sync.dma_start(out=w_sb[:], in_=W_words[0])
         for q in range(4):
             nc.sync.dma_start(
@@ -123,8 +106,9 @@ def tile_replaced_compose_lora_pa_t_w4_kernel(
             )
         for half in range(2):
             nc.sync.dma_start(out=bias_col[:, half, 0:1], in_=bias[half * P : (half + 1) * P].unsqueeze(1))
+        nc.sync.dma_start(out=xb[2][:], in_=x_rows[2])
         nc.sync.dma_start(out=bias_sb[:], in_=bias.partition_broadcast(P))
-        for c in range(2, CHUNKS):
+        for c in range(3, CHUNKS):
             nc.sync.dma_start(out=xb[c][:], in_=x_rows[c])
 
         a_codes = keep.tile([P, NR], U32, name="a_codes", align_bytes=64)
@@ -134,14 +118,14 @@ def tile_replaced_compose_lora_pa_t_w4_kernel(
         a_values = keep.tile([P, PACK * NR], BF16, name="a_values", align_bytes=64)
         b_values = keep.tile([P, PACK * D_OUT], BF16, name="b_values", align_bytes=64)
 
-        plain, x_banks, h_banks, out_banks, biased, back_banks = {}, {}, {}, {}, {}, {}
+        cast, x_banks, out_banks, biased = {}, {}, {}, {}
         round_values, round_codes = {}, {}
 
         def x_place(i):
             return i // 2 + 1, i % 2
 
         def h_place(i):
-            return x_place(i)[0] + (LAG_B if i % 2 else LAG_A), 2 + i % 2
+            return i // 2 + 2 + i % 2, 2 + i % 2
 
         def turn(rows, kind):
             words = rows.bitcast(F32)
@@ -151,27 +135,24 @@ def tile_replaced_compose_lora_pa_t_w4_kernel(
                     nc.tensor.transpose(turned[:, u, j, :], words[:, 256 * j + u : 256 * (j + 1) : 2], ident[:])
             return turned
 
-        def empty_turned(turned, values):
-            nc.scalar.copy(
-                out=values.bitcast(F32).rearrange("p (n u) -> p n u", u=2),
-                in_=turned[:].rearrange("p u j r -> p (j r) u"),
-            )
-
         def values_at(place):
-            r, q = place
+            r, quarter = place
             if r not in round_values:
-                round_values[r] = work.tile([P, 8 * D], BF16, name="values", tag="values", bufs=5, align_bytes=64)
-            return round_values[r][:, q * 2 * D : (q + 1) * 2 * D]
+                round_values[r] = work.tile(
+                    [P, 4 * PAIR_COLS], BF16, name="values", tag="values", bufs=ROUND_TILES, align_bytes=64
+                )
+            return round_values[r][:, quarter * PAIR_COLS : (quarter + 1) * PAIR_COLS]
 
-        def widen(engine, first_pair, dst, lo, hi):
-            c, q = divmod(first_pair, CHUNK_PAIRS)
-            engine.tensor_copy(out=dst[:, lo:hi], in_=xb[c][:, q * 2 * D + lo : q * 2 * D + hi].bitcast(FP8))
-            plain[first_pair], plain[first_pair + 1] = dst[:, 0 : 2 * D], dst[:, 2 * D : 4 * D]
+        def cast_x(copy, first_pair, dst, lo, hi):
+            c, cols = x_part(first_pair, lo, hi)
+            copy(out=dst[:, lo:hi], in_=xb[c][:, cols].bitcast(FP8))
+            for n in range(2):
+                cast[first_pair + n] = dst[:, n * PAIR_COLS : (n + 1) * PAIR_COLS]
 
         def turn_x(i):
-            x_banks[i] = turn(plain.pop(i), "turn")
+            x_banks[i] = turn(cast[i], "turn")
 
-        def scale_after(i):
+        def scale_x(i):
             nc.vector.tensor_tensor(
                 out=values_at(x_place(i)).rearrange("p (n u e) -> p n u e", u=2, e=2),
                 in0=x_banks.pop(i)[:].bitcast(BF16).rearrange("p u j (r e) -> p (j r) u e", e=2),
@@ -179,18 +160,22 @@ def tile_replaced_compose_lora_pa_t_w4_kernel(
                 op=ALU.mult,
             )
 
-        def quantise(r, lo, hi):
+        def quantise(r, words):
             if r not in round_codes:
                 round_codes[r] = (
-                    work.tile([P, 8 * P], U32, name="codes", tag="codes", bufs=5, align_bytes=64),
-                    work.tile([P, 8 * P], U8, name="scales", tag="scales", bufs=5, align_bytes=64),
+                    work.tile([P, 4 * PAIR_WORDS], U32, name="codes", tag="codes", bufs=ROUND_TILES, align_bytes=64),
+                    work.tile([P, 4 * PAIR_WORDS], U8, name="scales", tag="scales", bufs=ROUND_TILES, align_bytes=64),
                 )
             codes, scales = round_codes[r]
             nc.vector.quantize_mx(
-                out=codes[:, lo:hi].bitcast(FP8X4),
-                scales=scales[:, lo:hi],
-                in_=round_values[r][:, PACK * lo : PACK * hi],
+                out=codes[:, words].bitcast(FP8X4),
+                scales=scales[:, words],
+                in_=round_values[r][:, PACK * words.start : PACK * words.stop],
             )
+
+        def quantise_quarter(place):
+            r, quarter = place
+            quantise(r, slice(quarter * PAIR_WORDS, (quarter + 1) * PAIR_WORDS))
 
         def mx(acc, stationary, moving, start, stop):
             nc.tensor.matmul_mx(
@@ -207,30 +192,27 @@ def tile_replaced_compose_lora_pa_t_w4_kernel(
             return codes[:, lo : lo + width].bitcast(FP8X4), scales[:, lo : lo + width]
 
         def x_cols(i, j):
-            r, q = x_place(i)
-            return e4m3(*round_codes[r], (2 * q + j) * P, P)
+            r, quarter = x_place(i)
+            return e4m3(*round_codes[r], quarter * PAIR_WORDS + j * P, P)
 
         def h_cols(i, j, tiles):
-            r, q = h_place(i)
-            return e4m3(*round_codes[r], (2 * q + j) * P, tiles * P)
+            r, quarter = h_place(i)
+            return e4m3(*round_codes[r], quarter * PAIR_WORDS + j * P, tiles * P)
 
         def w_cols(half):
             return w_sb[:, half * 2 * P : (half + 1) * 2 * P].bitcast(FP4X4), w_sc[:, half * P : (half + 1) * P]
 
         def make_h(i):
-            h_banks[i] = []
+            banks = []
             for j in range(2):
-                acc = bank("h", [P, PACK, P])
+                banks.append(bank("h", [P, PACK, P]))
                 for t in range(PACK):
-                    mx(acc[:, t, :], e4m3(a_codes, a_scales, t * P, P), x_cols(i, j), True, True)
-                h_banks[i].append(acc)
-
-        def empty_h(i):
+                    mx(banks[j][:, t, :], e4m3(a_codes, a_scales, t * P, P), x_cols(i, j), True, True)
             values = values_at(h_place(i))
-            for j, acc in enumerate(h_banks.pop(i)):
+            for j in range(2):
                 nc.scalar.copy(
                     out=values[:, j * NR : (j + 1) * NR].rearrange("p (r t) -> p r t", t=PACK),
-                    in_=acc[:].rearrange("p t r -> p r t"),
+                    in_=banks[j][:].rearrange("p t r -> p r t"),
                 )
 
         def out_tile(i, j, acc):
@@ -243,8 +225,8 @@ def tile_replaced_compose_lora_pa_t_w4_kernel(
             for j in range(2):
                 mx(acc[:, j * P : (j + 1) * P], w_cols(half), x_cols(i, j), False, j == 1)
 
-        def make_out(i, kind="out"):
-            out_banks[i] = bank(kind, [P, 2, D_OUT])
+        def make_out(i):
+            out_banks[i] = bank("out", [P, 2, D_OUT])
             for side in range(2):
                 (out_half_turned if i in TURNED else out_tile)(i, side, out_banks[i][:, side, :])
 
@@ -255,256 +237,139 @@ def tile_replaced_compose_lora_pa_t_w4_kernel(
             c, q = divmod(i, CHUNK_PAIRS)
             return out_rows[c][:, 2 * q : 2 * q + 2, :]
 
+        bias_rows = bias_sb[:].unsqueeze(1).to_broadcast([P, 2, D_OUT])
+
         def finish(i):
             result = result_tile()
-            nc.vector.tensor_tensor(
-                out=result[:],
-                in0=out_banks.pop(i)[:],
-                in1=bias_sb[:].unsqueeze(1).to_broadcast([P, 2, D_OUT]),
-                op=ALU.add,
-            )
+            nc.vector.tensor_tensor(out=result[:], in0=out_banks.pop(i)[:], in1=bias_rows, op=ALU.add)
             nc.sync.dma_start(out=out_view(i), in_=result[:])
 
         def add_bias_turned(i):
-            acc = out_banks[i]
-            biased[i] = work.tile([P, 2, 2 * P], F32, name="biased", tag="biased", bufs=4, align_bytes=64)
+            biased[i] = work.tile([P, 2, 2 * P], F32, name="biased", tag="biased", bufs=BIASED_TILES, align_bytes=64)
             for half in range(2):
                 nc.scalar.activation(
                     out=biased[i][:, half, :],
-                    in_=acc[:, half, :],
+                    in_=out_banks[i][:, half, :],
                     func=ACT.Identity,
                     bias=bias_col[:, half, 0:1],
                     scale=1.0,
                 )
 
-        def turn_back(i):
-            sums = biased.pop(i)
-            back_banks[i] = out_banks.pop(i)
+        def finish_turned(i):
+            sums, acc = biased.pop(i), out_banks.pop(i)
             for j in range(2):
                 for half in range(2):
                     nc.tensor.transpose(
-                        back_banks[i][:, j, half * P : (half + 1) * P], sums[:, half, j * P : (j + 1) * P], ident[:]
+                        acc[:, j, half * P : (half + 1) * P], sums[:, half, j * P : (j + 1) * P], ident[:]
                     )
-
-        def finish_turned(i):
             result = result_tile()
-            nc.scalar.copy(out=result[:], in_=back_banks.pop(i)[:])
+            nc.scalar.copy(out=result[:], in_=acc[:])
             nc.sync.dma_start(out=out_view(i), in_=result[:])
 
-        def quantise_at(place):
-            quantise(place[0], place[1] * 2 * P, (place[1] + 1) * 2 * P)
+        def warm_up(operand, count):
+            unread = bank("out", [P, P])
+            for n in range(count):
+                nc.tensor.matmul(out=unread[:], lhsT=operand[:], rhs=operand[:], start=True, stop=True)
 
-        def turn_a(half):
+        warm_up(coef_row, 4)
+        cast_x(nc.vector.tensor_copy, 0, first, 0, D)
+        cast_x(nc.scalar.copy, 0, first, D, PAIR_COLS)
+        cast_x(nc.vector.tensor_copy, 0, first, PAIR_COLS, 2 * PAIR_COLS)
+        cast_x(nc.gpsimd.tensor_copy, 2, first[:, 2 * PAIR_COLS :], 0, 2 * PAIR_COLS)
+        turn_x(0)
+        turn_x(1)
+        for half in range(2):
             cols = slice(half * 2 * D, (half + 1) * 2 * D)
-            empty_turned(turn(a_sb[:, cols], "h"), a_values[:, cols])
-
-        widen(nc.vector, 0, first[:, 0 : 4 * D], 0, D)
-        nc.scalar.copy(out=first[:, D : 2 * D], in_=xb[0][:, D : 2 * D].bitcast(FP8))
-        widen(nc.vector, 0, first[:, 0 : 4 * D], 2 * D, 4 * D)
-        widen(nc.gpsimd, 2, first[:, 4 * D :], 0, 4 * D)
-        for what in HEAD:
-            if what == "0":
-                turn_x(0)
-            if what == "1":
-                turn_x(1)
-            if what == "a":
-                turn_a(0)
-            if what == "A":
-                turn_a(1)
-            if what == "s":
-                scale_after(0)
-            if what == "S":
-                scale_after(1)
-            if what == "q":
-                nc.vector.quantize_mx(out=a_codes[:].bitcast(FP8X4), scales=a_scales[:], in_=a_values[:])
-            if what == "x":
-                quantise_at(x_place(0))
-            if what == "h":
-                make_h(0)
-            if what == "c":
-                nc.scalar.activation(
-                    out=coef_row[0:1, :].rearrange("p (n q) -> p n q", q=PACK),
-                    in_=lw_row[:].unsqueeze(2).to_broadcast([1, NR // RANK, PACK]),
-                    func=ACT.Copy,
-                    scale=ALPHA_OVER_RANK,
-                )
-            if what == "C":
-                coef_bank = bank("out", [P, P])
-                nc.tensor.transpose(coef_bank[:], coef_row[:], ident[:])
-                nc.scalar.copy(out=coef[:], in_=coef_bank[:, 0:1])
-
-        def make_bc():
-            nc.scalar.activation(
-                out=b_values[:].rearrange("p (o t) -> p o t", t=PACK),
-                in_=b_sb[:, :, 0:PACK],
-                func=ACT.Copy,
-                scale=coef[:],
+            nc.scalar.copy(
+                out=a_values[:, cols].bitcast(F32).rearrange("p (n u) -> p n u", u=2),
+                in_=turn(a_sb[:, cols], "h")[:].rearrange("p u j r -> p (j r) u"),
             )
+        warm_up(ident, 3)
+        scale_x(0)
+        scale_x(1)
+        nc.scalar.activation(
+            out=coef_row[0:1, :].rearrange("p (n q) -> p n q", q=PACK),
+            in_=lw_row[:].unsqueeze(2).to_broadcast([1, ADAPTERS, PACK]),
+            func=ACT.Copy,
+            scale=ALPHA_OVER_RANK,
+        )
+        coef_bank = bank("out", [P, P])
+        nc.tensor.transpose(coef_bank[:], coef_row[:], ident[:])
+        nc.scalar.copy(out=coef[:], in_=coef_bank[:, 0:1])
+        nc.vector.quantize_mx(out=a_codes[:].bitcast(FP8X4), scales=a_scales[:], in_=a_values[:])
+        nc.scalar.activation(
+            out=b_values[:].rearrange("p (o t) -> p o t", t=PACK), in_=b_sb[:, :, 0:PACK], func=ACT.Copy, scale=coef[:]
+        )
+        sums_late = keep.tile([P, 2, D_OUT], F32, name="sums_late", align_bytes=64)
 
-        if BPOS == 0:
-            make_bc()
-        sums = keep.tile([P, len(LATE), 2, D_OUT], F32, name="sums", align_bytes=64)
-        x_at = {x_place(i): i for i in range(PAIRS)}
-        h_at = {h_place(i): i for i in range(PAIRS)}
-        to_finish, to_back, waiting = [], [], []
-        for r in range(1, ROUNDS):
-            filled = [q for q in range(4) if (r, q) in x_at or (r, q) in h_at]
-            if r == BQ:
+        def begin_round(r):
+            if r == 2:
                 nc.vector.quantize_mx(out=b_codes[:].bitcast(FP8X4), scales=b_scales[:], in_=b_values[:])
-            if r == 1 and "x" in HEAD:
-                quantise_at(x_place(1))
-            elif len(filled) == 4 and r == 3:
-                quantise(r, 4 * P, 8 * P)
-                quantise(r, 0, 4 * P)
-            elif len(filled) == 4 and r == 4:
-                quantise(r, 4 * P, 8 * P)
-                quantise(r, 0, 4 * P)
-            elif len(filled) == 4:
-                quantise(r, 0, 8 * P)
+                quantise_quarter(h_place(0))
+            if 2 * r - 9 >= 0:
+                quantise(r, slice(X_HALF.start, H_HALF.stop))
             else:
-                for q in filled[2:]:
-                    quantise(r, q * 2 * P, (q + 1) * 2 * P)
-                quantise(r, filled[0] * 2 * P, (filled[:2][-1] + 1) * 2 * P)
-            cut = 4 * D - (SD if to_finish else SPARE)
-            if r + 1 < ROUNDS:
-                widen(nc.gpsimd, 2 * r + 2, round_values[r], 0, cut)
-            turn_x(2 * r)
-            turn_x(2 * r + 1)
-            if r + 1 == ROUNDS:
-                break
-            backs = list(to_back)
-            to_back.clear()
-            for i in backs[:1]:
-                turn_back(i)
-            if ORDER in "cd":
-                for i in backs[:1]:
-                    finish_turned(i)
-            for i in backs[1:]:
-                turn_back(i)
-            fins = list(to_finish)
-            to_finish.clear()
-            scal = [2 * r, 2 * r + 1] if r < ROUNDS else []
-            for i in scal[:FIN]:
-                scale_after(i)
-            for i in fins:
-                finish(i)
-            for i in scal[FIN:]:
-                scale_after(i)
-            hs = [x_at[r, q] for q in range(2) if (r, q) in x_at]
-            outs = [h_at[r, q] for q in (2, 3) if (r, q) in h_at]
-            if r < BQ:
-                waiting, outs = outs, []
-            elif r == BQ:
-                outs = waiting + outs
-            outs = [i for i in outs if i not in TURNED] + [i for i in outs if i in TURNED]
-            if ORDER in "bd":
-                outs = outs[::-1]
-            for i in hs[:1]:
-                if i > 0 or "h" not in HEAD:
-                    make_h(i)
-                empty_h(i)
-            if True:
-                c, q = divmod(2 * r + 2, CHUNK_PAIRS)
-                nc.scalar.copy(
-                    out=round_values[r][:, cut : 4 * D], in_=xb[c][:, q * 2 * D + cut : (q + 2) * 2 * D].bitcast(FP8)
-                )
-            if r == 1 and BPOS == 1:
-                make_bc()
-            for i in backs[1 if ORDER in "cd" else 0 :]:
-                finish_turned(i)
-            for n, i in enumerate(outs):
-                make_out(i)
-                if i in TURNED:
-                    add_bias_turned(i)
-                    to_back.append(i)
-                elif i in LATE:
-                    nc.scalar.copy(out=sums[:, i - LATE[0]], in_=out_banks.pop(i)[:])
-                else:
-                    to_finish.append(i)
-                if n == 0 and MID:
-                    for k in hs[1:]:
-                        make_h(k)
-                        empty_h(k)
-                    hs = []
-            for i in hs[1:]:
-                make_h(i)
-                empty_h(i)
-            if r == 1 and BPOS == 2:
-                make_bc()
+                if r > 2:
+                    quantise(r, H_HALF)
+                quantise(r, X_HALF)
 
-        def h_stage(i):
-            make_h(i)
-            empty_h(i)
+        for r in range(1, ROUNDS - 1):
+            even_x, odd_x = 2 * r, 2 * r + 1
+            even_out, odd_out = 2 * r - 4, 2 * r - 5
+            begin_round(r)
+            cut = 2 * PAIR_COLS - SCALAR_COLS
+            cast_x(nc.gpsimd.tensor_copy, even_x + 2, round_values[r], 0, cut)
+            turn_x(even_x)
+            turn_x(odd_x)
+            if even_out - 2 in TURNED:
+                finish_turned(even_out - 2)
+            scale_x(even_x)
+            scale_x(odd_x)
+            if odd_out - 2 >= 0:
+                finish(odd_out - 2)
+            make_h(even_x - 2)
+            cast_x(nc.scalar.copy, even_x + 2, round_values[r], cut, 2 * PAIR_COLS)
+            if even_out >= 0:
+                make_out(even_out)
+                add_bias_turned(even_out)
+            if odd_out >= 0:
+                make_out(odd_out)
+            if odd_out == GPSIMD_PAIR:
+                nc.scalar.copy(out=sums_late[:], in_=out_banks.pop(odd_out)[:])
+            make_h(odd_x - 2)
 
-        def out_stage(i, kind="out"):
-            make_out(i, kind)
-            if i in TURNED:
-                add_bias_turned(i)
-
-        def back_stage(i):
-            if i in TURNED:
-                turn_back(i)
-                finish_turned(i)
-
-        def end_stage(i):
-            if i not in TURNED:
-                finish(i)
-
-        for i in to_back:
-            back_stage(i)
-        for word in TAIL.split():
-            what, i = word[0], int(word[1:])
-            if what == "h":
-                h_stage(i)
-            if what == "s":
-                scale_after(i)
-            if what == "x":
-                last = x_place(i)
-                quantise_at(last)
-            if what == "q":
-                last = h_place(i)
-                quantise_at(last)
-            if what == "X":
-                quantise(ROUNDS, 0, 4 * P)
-            if what == "G":
-                late = round_values[i][:, 0 : len(LATE) * 2 * D].bitcast(F32).rearrange("p (n o) -> p n o", o=D_OUT)
-                nc.gpsimd.tensor_tensor(
-                    out=late,
-                    in0=sums[:].rearrange("p i j o -> p (i j) o"),
-                    in1=bias_sb[:].unsqueeze(1).to_broadcast([P, 2 * len(LATE), D_OUT]),
-                    op=ALU.add,
-                )
-                for n, k in enumerate(LATE):
-                    nc.sync.dma_start(out=out_view(k), in_=late[:, 2 * n : 2 * n + 2, :])
-            if what == "H":
-                quantise(i, 4 * P, 8 * P)
-            if what == "Q":
-                quantise(ROUNDS, 0, 8 * P)
-            if what == "c":
-                nc.scalar.copy(out=sums[:, 0], in_=out_banks.pop(i)[:])
-            if what == "g":
-                spot = values_at(last).bitcast(F32).rearrange("p (n o) -> p n o", o=D_OUT)
-                nc.gpsimd.tensor_tensor(
-                    out=spot, in0=sums[:, 0], in1=bias_sb[:].unsqueeze(1).to_broadcast([P, 2, D_OUT]), op=ALU.add
-                )
-                nc.sync.dma_start(out=out_view(i), in_=spot)
-            if what == "o":
-                make_out(i)
-            if what == "O":
-                make_out(i, "turn")
-            if what == "a":
-                add_bias_turned(i)
-            if what == "b":
-                turn_back(i)
-            if what == "r":
-                finish_turned(i)
-            if what == "f":
-                finish(i)
+        begin_round(ROUNDS - 1)
+        turn_x(LAST - 1)
+        turn_x(LAST)
+        finish_turned(TURNED[-1])
+        late = round_values[ROUNDS - 1][:, 0:PAIR_COLS].bitcast(F32).rearrange("p (n o) -> p n o", o=D_OUT)
+        nc.gpsimd.tensor_tensor(out=late, in0=sums_late[:], in1=bias_rows, op=ALU.add)
+        nc.sync.dma_start(out=out_view(GPSIMD_PAIR), in_=late)
+        make_h(LAST - 3)
+        scale_x(LAST - 1)
+        scale_x(LAST)
+        make_out(LAST - 6)
+        make_out(LAST - 5)
+        make_h(LAST - 2)
+        for i in range(LAST - 4, LAST - 2):
+            quantise_quarter(h_place(i))
+            quantise_quarter(x_place(i + 3))
+            if i == LAST - 3:
+                make_h(LAST - 1)
+            finish(i - 2)
+            make_out(i)
+        quantise_quarter(h_place(LAST - 2))
+        make_h(LAST)
+        finish(LAST - 4)
+        quantise_quarter(h_place(LAST - 1))
+        make_out(LAST - 2)
+        finish(LAST - 3)
+        make_out(LAST - 1)
         last_result = result_tile()
         last_banks = []
-        r, q = h_place(LAST)
+        r, quarter = h_place(LAST)
         for j in range(2):
-            quantise(r, (2 * q + j) * P, (2 * q + j + 1) * P)
+            quantise(r, slice(quarter * PAIR_WORDS + j * P, quarter * PAIR_WORDS + (j + 1) * P))
             last_banks.append(bank("h", [P, D_OUT]))
             out_tile(LAST, j, last_banks[j][:])
             finish(LAST - 2 + j)

@@ -34,7 +34,9 @@ X_HALF, H_HALF = slice(0, 2 * PAIR_WORDS), slice(2 * PAIR_WORDS, 4 * PAIR_WORDS)
 ROUND_TILES = 5
 SCALAR_COLS = 256
 BIASED_TILES = 4
-TURNED = range(0, 2 * ROUNDS - 7, 2)
+TURNED_EVEN = range(0, 2 * ROUNDS - 7, 2)
+TURNED_ODD = range(11, 2 * ROUNDS - 9, 8)
+TURNED = list(TURNED_EVEN) + list(TURNED_ODD)
 GPSIMD_PAIR = 2 * ROUNDS - 9
 
 
@@ -256,14 +258,20 @@ def tile_replaced_compose_lora_pa_t_w4_kernel(
                 )
 
         def finish_turned(i):
-            sums, acc = biased.pop(i), out_banks.pop(i)
+            turn_back(i)
+            store_turned(i)
+
+        def turn_back(i):
+            sums, acc = biased.pop(i), out_banks[i]
             for j in range(2):
                 for half in range(2):
                     nc.tensor.transpose(
                         acc[:, j, half * P : (half + 1) * P], sums[:, half, j * P : (j + 1) * P], ident[:]
                     )
+
+        def store_turned(i):
             result = result_tile()
-            nc.scalar.copy(out=result[:], in_=acc[:])
+            nc.scalar.copy(out=result[:], in_=out_banks.pop(i)[:])
             nc.sync.dma_start(out=out_view(i), in_=result[:])
 
         def warm_up(operand, count):
@@ -302,11 +310,14 @@ def tile_replaced_compose_lora_pa_t_w4_kernel(
         )
         sums_late = keep.tile([P, 2, D_OUT], F32, name="sums_late", align_bytes=64)
 
+        def plain_odd(i):
+            return i >= 0 and i not in TURNED
+
         def begin_round(r):
             if r == 2:
                 nc.vector.quantize_mx(out=b_codes[:].bitcast(FP8X4), scales=b_scales[:], in_=b_values[:])
                 quantise_quarter(h_place(0))
-            if 2 * r - 9 >= 0:
+            if plain_odd(2 * r - 9):
                 quantise(r, slice(X_HALF.start, H_HALF.stop))
             else:
                 if r > 2:
@@ -323,17 +334,23 @@ def tile_replaced_compose_lora_pa_t_w4_kernel(
             turn_x(odd_x)
             if even_out - 2 in TURNED:
                 finish_turned(even_out - 2)
+            if odd_out - 2 in TURNED:
+                turn_back(odd_out - 2)
             scale_x(even_x)
             scale_x(odd_x)
-            if odd_out - 2 >= 0:
+            if plain_odd(odd_out - 2):
                 finish(odd_out - 2)
             make_h(even_x - 2)
+            if odd_out - 2 in TURNED:
+                store_turned(odd_out - 2)
             cast_x(nc.scalar.copy, even_x + 2, round_values[r], cut, 2 * PAIR_COLS)
             if even_out >= 0:
                 make_out(even_out)
                 add_bias_turned(even_out)
             if odd_out >= 0:
                 make_out(odd_out)
+            if odd_out in TURNED:
+                add_bias_turned(odd_out)
             if odd_out == GPSIMD_PAIR:
                 nc.scalar.copy(out=sums_late[:], in_=out_banks.pop(odd_out)[:])
             make_h(odd_x - 2)
@@ -341,7 +358,7 @@ def tile_replaced_compose_lora_pa_t_w4_kernel(
         begin_round(ROUNDS - 1)
         turn_x(LAST - 1)
         turn_x(LAST)
-        finish_turned(TURNED[-1])
+        finish_turned(TURNED_EVEN[-1])
         late = round_values[ROUNDS - 1][:, 0:PAIR_COLS].bitcast(F32).rearrange("p (n o) -> p n o", o=D_OUT)
         nc.gpsimd.tensor_tensor(out=late, in0=sums_late[:], in1=bias_rows, op=ALU.add)
         nc.sync.dma_start(out=out_view(GPSIMD_PAIR), in_=late)

@@ -193,9 +193,9 @@ def tile_replaced_compose_lora_pa_t_w4_kernel(
         def e4m3(codes, scales, lo, width):
             return codes[:, lo : lo + width].bitcast(FP8X4), scales[:, lo : lo + width]
 
-        def x_cols(i, j):
+        def x_cols(i, j, tiles):
             r, quarter = x_place(i)
-            return e4m3(*round_codes[r], quarter * PAIR_WORDS + j * P, P)
+            return e4m3(*round_codes[r], quarter * PAIR_WORDS + j * P, tiles * P)
 
         def h_cols(i, j, tiles):
             r, quarter = h_place(i)
@@ -209,7 +209,7 @@ def tile_replaced_compose_lora_pa_t_w4_kernel(
             for j in range(2):
                 banks.append(bank("h", [P, PACK, P]))
                 for t in range(PACK):
-                    mx(banks[j][:, t, :], e4m3(a_codes, a_scales, t * P, P), x_cols(i, j), True, True)
+                    mx(banks[j][:, t, :], e4m3(a_codes, a_scales, t * P, P), x_cols(i, j, 1), True, True)
             values = values_at(h_place(i))
             for j in range(2):
                 nc.scalar.copy(
@@ -219,13 +219,11 @@ def tile_replaced_compose_lora_pa_t_w4_kernel(
 
         def out_tile(i, j, acc):
             mx(acc, h_cols(i, j, 1), e4m3(b_codes, b_scales, 0, D_OUT), True, False)
-            for half in range(2):
-                mx(acc[:, half * P : (half + 1) * P], x_cols(i, j), w_cols(half), False, half == 1)
+            mx(acc, x_cols(i, j, 1), (w_sb[:].bitcast(FP4X4), w_sc[:]), False, True)
 
         def out_half_turned(i, half, acc):
             mx(acc, e4m3(b_codes, b_scales, half * P, P), h_cols(i, 0, 2), True, False)
-            for j in range(2):
-                mx(acc[:, j * P : (j + 1) * P], w_cols(half), x_cols(i, j), False, j == 1)
+            mx(acc, w_cols(half), x_cols(i, 0, 2), False, True)
 
         def make_out(i):
             out_banks[i] = bank("out", [P, 2, D_OUT])

@@ -33,11 +33,10 @@ ROUNDS = PAIRS // 2
 X_HALF, H_HALF = slice(0, 2 * PAIR_WORDS), slice(2 * PAIR_WORDS, 4 * PAIR_WORDS)
 ROUND_TILES = 5
 SCALAR_COLS = 256
-BIASED_TILES = 4
-TURNED_EVEN = range(0, 2 * ROUNDS - 7, 2)
-TURNED_ODD = range(11, 2 * ROUNDS - 9, 8)
-TURNED = list(TURNED_EVEN) + list(TURNED_ODD)
+BIASED_TILES = 2
+TURNED = range(0, 2 * ROUNDS - 7, 2)
 GPSIMD_PAIR = 2 * ROUNDS - 9
+FIRST_PAIRS = 5
 
 
 def tile_replaced_compose_lora_pa_t_w4_kernel(
@@ -62,7 +61,7 @@ def tile_replaced_compose_lora_pa_t_w4_kernel(
 
         xb = [keep.tile([P, 2 * CHUNK_PAIRS * D], U8, name="xb%d" % c, align_bytes=64) for c in range(CHUNKS)]
         scale_col = keep.tile([P, PACK], F32, name="scale_col")
-        first = keep.tile([P, 4 * PAIR_COLS], BF16, name="first", align_bytes=64)
+        first = keep.tile([P, FIRST_PAIRS * PAIR_COLS], BF16, name="first", align_bytes=64)
         a_sb = keep.tile([P, PACK * D], BF16, name="a_sb", align_bytes=64)
         b_sb = keep.tile([P, D_OUT, RANK], BF16, name="b_sb", align_bytes=64)
         w_sb = keep.tile([P, 2 * D_OUT], U8, name="w_sb", align_bytes=64)
@@ -90,9 +89,9 @@ def tile_replaced_compose_lora_pa_t_w4_kernel(
         nc.sync.dma_start(out=scale_col[:], in_=x_scale.rearrange("a b (p t) -> p (a b t)", t=PACK))
         load_x(2, 2)
         nc.sync.dma_start(out=a_sb[:, 0 : 2 * D], in_=a_rows[:, 0 : 2 * D])
+        load_x(4, 2)
         nc.sync.dma_start(out=a_sb[:, 2 * D :], in_=a_rows[:, 2 * D :])
         nc.sync.dma_start(out=lw_row[:], in_=lora_weights.unsqueeze(0))
-        load_x(4, 2)
         b_rows = lora_B.rearrange("n o r -> n (o r)")
         b_run = RANK * D_OUT - (RANK - PACK)
         for q in range(PACK):
@@ -129,10 +128,10 @@ def tile_replaced_compose_lora_pa_t_w4_kernel(
         def h_place(i):
             return i // 2 + 2 + i % 2, 2 + i % 2
 
-        def turn(rows, kind):
+        def turn(rows, tiles, kind):
             words = rows.bitcast(F32)
-            turned = bank(kind, [P, 2, 2, P])
-            for j in range(2):
+            turned = bank(kind, [P, 2, tiles, P])
+            for j in range(tiles):
                 for u in range(2):
                     nc.tensor.transpose(turned[:, u, j, :], words[:, 256 * j + u : 256 * (j + 1) : 2], ident[:])
             return turned
@@ -145,22 +144,26 @@ def tile_replaced_compose_lora_pa_t_w4_kernel(
                 )
             return round_values[r][:, quarter * PAIR_COLS : (quarter + 1) * PAIR_COLS]
 
-        def cast_x(copy, first_pair, dst, lo, hi):
+        def cast_x(copy, first_pair, pairs, dst, lo, hi):
             c, cols = x_part(first_pair, lo, hi)
             copy(out=dst[:, lo:hi], in_=xb[c][:, cols].bitcast(FP8))
-            for n in range(2):
+            for n in range(pairs):
                 cast[first_pair + n] = dst[:, n * PAIR_COLS : (n + 1) * PAIR_COLS]
 
-        def turn_x(i):
-            x_banks[i] = turn(cast[i], "turn")
+        def turn_x(i, kind="turn"):
+            x_banks[i] = turn(cast[i], 2, kind)
 
-        def scale_x(i):
+        def scale_into(values, turned):
+            tokens = values.shape[1] // PACK
             nc.vector.tensor_tensor(
-                out=values_at(x_place(i)).rearrange("p (n u e) -> p n u e", u=2, e=2),
-                in0=x_banks.pop(i)[:].bitcast(BF16).rearrange("p u j (r e) -> p (j r) u e", e=2),
-                in1=scale_col[:].rearrange("p (u e) -> p u e", e=2).unsqueeze(1).to_broadcast([P, 2 * P, 2, 2]),
+                out=values.rearrange("p (n u e) -> p n u e", u=2, e=2),
+                in0=turned[:].bitcast(BF16).rearrange("p u j (r e) -> p (j r) u e", e=2),
+                in1=scale_col[:].rearrange("p (u e) -> p u e", e=2).unsqueeze(1).to_broadcast([P, tokens, 2, 2]),
                 op=ALU.mult,
             )
+
+        def scale_x(i):
+            scale_into(values_at(x_place(i)), x_banks.pop(i))
 
         def quantise(r, words):
             if r not in round_codes:
@@ -272,83 +275,95 @@ def tile_replaced_compose_lora_pa_t_w4_kernel(
             nc.scalar.copy(out=result[:], in_=out_banks.pop(i)[:])
             nc.sync.dma_start(out=out_view(i), in_=result[:])
 
-        def warm_up(operand, count):
-            unread = bank("out", [P, P])
-            for n in range(count):
-                nc.tensor.matmul(out=unread[:], lhsT=operand[:], rhs=operand[:], start=True, stop=True)
-
-        warm_up(coef_row, 4)
-        cast_x(nc.vector.tensor_copy, 0, first, 0, D)
-        cast_x(nc.scalar.copy, 0, first, D, PAIR_COLS)
-        cast_x(nc.vector.tensor_copy, 0, first, PAIR_COLS, 2 * PAIR_COLS)
-        cast_x(nc.gpsimd.tensor_copy, 2, first[:, 2 * PAIR_COLS :], 0, 2 * PAIR_COLS)
-        turn_x(0)
-        turn_x(1)
-        for half in range(2):
+        def turn_a(half):
             cols = slice(half * 2 * D, (half + 1) * 2 * D)
             nc.scalar.copy(
                 out=a_values[:, cols].bitcast(F32).rearrange("p (n u) -> p n u", u=2),
-                in_=turn(a_sb[:, cols], "h")[:].rearrange("p u j r -> p (j r) u"),
+                in_=turn(a_sb[:, cols], 2, "h")[:].rearrange("p u j r -> p (j r) u"),
             )
-        warm_up(ident, 3)
-        scale_x(0)
-        scale_x(1)
+
+        def quantise_a(half):
+            words = slice(half * 2 * P, (half + 1) * 2 * P)
+            nc.vector.quantize_mx(
+                out=a_codes[:, words].bitcast(FP8X4),
+                scales=a_scales[:, words],
+                in_=a_values[:, half * 2 * D : (half + 1) * 2 * D],
+            )
+
+        def first_cast(copy, i, lo, hi):
+            cast_x(copy, i, 1, first[:, i * PAIR_COLS : (i + 1) * PAIR_COLS], lo, hi)
+
+        first_cast(nc.vector.tensor_copy, 0, 0, D)
+        first_cast(nc.scalar.copy, 0, D, PAIR_COLS)
+        first_cast(nc.vector.tensor_copy, 1, 0, PAIR_COLS)
+        first_cast(nc.gpsimd.tensor_copy, 2, 0, PAIR_COLS)
+        first_cast(nc.scalar.copy, 3, 0, PAIR_COLS)
+        first_cast(nc.gpsimd.tensor_copy, 4, 0, PAIR_COLS)
         nc.scalar.activation(
             out=coef_row[0:1, :].rearrange("p (n q) -> p n q", q=PACK),
             in_=lw_row[:].unsqueeze(2).to_broadcast([1, ADAPTERS, PACK]),
             func=ACT.Copy,
             scale=ALPHA_OVER_RANK,
         )
-        coef_bank = bank("out", [P, P])
+        first_tiles = [turn(cast[0][:, j * D : (j + 1) * D], 1, "out") for j in range(2)]
+        turn_x(1)
+        turn_a(0)
+        turn_a(1)
+        coef_bank = bank("h", [P, P])
         nc.tensor.transpose(coef_bank[:], coef_row[:], ident[:])
         nc.scalar.copy(out=coef[:], in_=coef_bank[:, 0:1])
-        nc.vector.quantize_mx(out=a_codes[:].bitcast(FP8X4), scales=a_scales[:], in_=a_values[:])
         nc.scalar.activation(
             out=b_values[:].rearrange("p (o t) -> p o t", t=PACK), in_=b_sb[:, :, 0:PACK], func=ACT.Copy, scale=coef[:]
         )
+        turn_x(2)
+        turn_x(3, "out")
+        for j in range(2):
+            scale_into(values_at(x_place(0))[:, j * D : (j + 1) * D], first_tiles[j])
+        scale_x(1)
+        for i in range(2):
+            quantise_a(i)
+            quantise_quarter(x_place(i))
+        cast_x(nc.gpsimd.tensor_copy, FIRST_PAIRS, 1, values_at(x_place(1)), 0, PAIR_COLS)
+        make_h(0)
+        make_h(1)
+        scale_x(2)
+        scale_x(3)
         sums_late = keep.tile([P, 2, D_OUT], F32, name="sums_late", align_bytes=64)
-
-        def plain_odd(i):
-            return i >= 0 and i not in TURNED
 
         def begin_round(r):
             if r == 2:
                 nc.vector.quantize_mx(out=b_codes[:].bitcast(FP8X4), scales=b_scales[:], in_=b_values[:])
                 quantise_quarter(h_place(0))
-            if plain_odd(2 * r - 9):
+            if 2 * r - 9 > 0:
                 quantise(r, slice(X_HALF.start, H_HALF.stop))
             else:
                 if r > 2:
                     quantise(r, H_HALF)
                 quantise(r, X_HALF)
 
-        for r in range(1, ROUNDS - 1):
+        def scale_both(even_x):
+            scale_x(even_x + 1)
+            scale_x(even_x)
+
+        for r in range(2, ROUNDS - 1):
             even_x, odd_x = 2 * r, 2 * r + 1
             even_out, odd_out = 2 * r - 4, 2 * r - 5
             begin_round(r)
             cut = 2 * PAIR_COLS - SCALAR_COLS
-            cast_x(nc.gpsimd.tensor_copy, even_x + 2, round_values[r], 0, cut)
+            cast_x(nc.gpsimd.tensor_copy, even_x + 2, 2, round_values[r], 0, cut)
             turn_x(even_x)
             turn_x(odd_x)
             if even_out - 2 in TURNED:
                 finish_turned(even_out - 2)
-            if odd_out - 2 in TURNED:
-                turn_back(odd_out - 2)
-            scale_x(even_x)
-            scale_x(odd_x)
-            if plain_odd(odd_out - 2):
+            scale_both(even_x)
+            if odd_out - 2 > 0:
                 finish(odd_out - 2)
             make_h(even_x - 2)
-            if odd_out - 2 in TURNED:
-                store_turned(odd_out - 2)
-            cast_x(nc.scalar.copy, even_x + 2, round_values[r], cut, 2 * PAIR_COLS)
-            if even_out >= 0:
-                make_out(even_out)
-                add_bias_turned(even_out)
-            if odd_out >= 0:
+            cast_x(nc.scalar.copy, even_x + 2, 2, round_values[r], cut, 2 * PAIR_COLS)
+            make_out(even_out)
+            add_bias_turned(even_out)
+            if odd_out > 0:
                 make_out(odd_out)
-            if odd_out in TURNED:
-                add_bias_turned(odd_out)
             if odd_out == GPSIMD_PAIR:
                 nc.scalar.copy(out=sums_late[:], in_=out_banks.pop(odd_out)[:])
             make_h(odd_x - 2)
@@ -356,29 +371,28 @@ def tile_replaced_compose_lora_pa_t_w4_kernel(
         begin_round(ROUNDS - 1)
         turn_x(LAST - 1)
         turn_x(LAST)
-        finish_turned(TURNED_EVEN[-1])
-        late = round_values[ROUNDS - 1][:, 0:PAIR_COLS].bitcast(F32).rearrange("p (n o) -> p n o", o=D_OUT)
+        finish_turned(TURNED[-1])
+        late = values_at(h_place(LAST - 5)).bitcast(F32).rearrange("p (n o) -> p n o", o=D_OUT)
         nc.gpsimd.tensor_tensor(out=late, in0=sums_late[:], in1=bias_rows, op=ALU.add)
         nc.sync.dma_start(out=out_view(GPSIMD_PAIR), in_=late)
+        scale_both(LAST - 1)
         make_h(LAST - 3)
-        scale_x(LAST - 1)
-        scale_x(LAST)
-        make_out(LAST - 6)
         make_out(LAST - 5)
+        make_out(LAST - 6)
         make_h(LAST - 2)
-        for i in range(LAST - 4, LAST - 2):
-            quantise_quarter(h_place(i))
-            quantise_quarter(x_place(i + 3))
-            if i == LAST - 3:
-                make_h(LAST - 1)
-            finish(i - 2)
-            make_out(i)
-        quantise_quarter(h_place(LAST - 2))
+        quantise_quarter(h_place(LAST - 4))
+        quantise_quarter(x_place(LAST - 1))
+        finish(LAST - 6)
+        quantise_quarter(x_place(LAST))
+        quantise_quarter(h_place(LAST - 3))
+        make_h(LAST - 1)
+        make_out(LAST - 4)
         make_h(LAST)
-        finish(LAST - 4)
-        quantise_quarter(h_place(LAST - 1))
-        make_out(LAST - 2)
-        finish(LAST - 3)
+        finish(LAST - 5)
+        for i in range(LAST - 3, LAST - 1):
+            quantise_quarter(h_place(i + 1))
+            make_out(i)
+            finish(i - 1)
         make_out(LAST - 1)
         last_result = result_tile()
         last_banks = []

@@ -33,8 +33,10 @@ ROUNDS = PAIRS // 2
 X_HALF, H_HALF = slice(0, 2 * PAIR_WORDS), slice(2 * PAIR_WORDS, 4 * PAIR_WORDS)
 ROUND_TILES = 5
 SCALAR_COLS = 256
-BIASED_TILES = 2
-TURNED = range(0, 2 * ROUNDS - 7, 2)
+BIASED_TILES = 4
+TURNED_EVEN = range(0, 2 * ROUNDS - 7, 2)
+TURNED_ODD = range(7, 2 * ROUNDS - 9, 6)
+TURNED = list(TURNED_EVEN) + list(TURNED_ODD)
 GPSIMD_PAIR = 2 * ROUNDS - 9
 FIRST_PAIRS = 5
 
@@ -320,9 +322,9 @@ def tile_replaced_compose_lora_pa_t_w4_kernel(
         for j in range(2):
             scale_into(values_at(x_place(0))[:, j * D : (j + 1) * D], first_tiles[j])
         scale_x(1)
-        for i in range(2):
-            quantise_a(i)
-            quantise_quarter(x_place(i))
+        quantise_a(0)
+        quantise(1, X_HALF)
+        quantise_a(1)
         cast_x(nc.gpsimd.tensor_copy, FIRST_PAIRS, 1, values_at(x_place(1)), 0, PAIR_COLS)
         make_h(0)
         make_h(1)
@@ -330,40 +332,47 @@ def tile_replaced_compose_lora_pa_t_w4_kernel(
         scale_x(3)
         sums_late = keep.tile([P, 2, D_OUT], F32, name="sums_late", align_bytes=64)
 
+        def vector_adds(i):
+            return i >= 0 and i not in TURNED
+
         def begin_round(r):
             if r == 2:
                 nc.vector.quantize_mx(out=b_codes[:].bitcast(FP8X4), scales=b_scales[:], in_=b_values[:])
                 quantise_quarter(h_place(0))
-            if 2 * r - 9 > 0:
+            if vector_adds(2 * r - 9):
                 quantise(r, slice(X_HALF.start, H_HALF.stop))
             else:
                 if r > 2:
                     quantise(r, H_HALF)
                 quantise(r, X_HALF)
 
-        def scale_both(even_x):
-            scale_x(even_x + 1)
-            scale_x(even_x)
-
         for r in range(2, ROUNDS - 1):
             even_x, odd_x = 2 * r, 2 * r + 1
             even_out, odd_out = 2 * r - 4, 2 * r - 5
             begin_round(r)
-            cut = 2 * PAIR_COLS - SCALAR_COLS
+            cut = 2 * PAIR_COLS - (0 if vector_adds(odd_out - 2) else SCALAR_COLS)
             cast_x(nc.gpsimd.tensor_copy, even_x + 2, 2, round_values[r], 0, cut)
             turn_x(even_x)
             turn_x(odd_x)
             if even_out - 2 in TURNED:
                 finish_turned(even_out - 2)
-            scale_both(even_x)
-            if odd_out - 2 > 0:
+            if odd_out - 2 in TURNED:
+                turn_back(odd_out - 2)
+            scale_x(even_x)
+            scale_x(odd_x)
+            if vector_adds(odd_out - 2):
                 finish(odd_out - 2)
             make_h(even_x - 2)
-            cast_x(nc.scalar.copy, even_x + 2, 2, round_values[r], cut, 2 * PAIR_COLS)
+            if odd_out - 2 in TURNED:
+                store_turned(odd_out - 2)
+            if cut < 2 * PAIR_COLS:
+                cast_x(nc.scalar.copy, even_x + 2, 2, round_values[r], cut, 2 * PAIR_COLS)
             make_out(even_out)
             add_bias_turned(even_out)
-            if odd_out > 0:
+            if odd_out >= 0:
                 make_out(odd_out)
+            if odd_out in TURNED:
+                add_bias_turned(odd_out)
             if odd_out == GPSIMD_PAIR:
                 nc.scalar.copy(out=sums_late[:], in_=out_banks.pop(odd_out)[:])
             make_h(odd_x - 2)
@@ -371,11 +380,12 @@ def tile_replaced_compose_lora_pa_t_w4_kernel(
         begin_round(ROUNDS - 1)
         turn_x(LAST - 1)
         turn_x(LAST)
-        finish_turned(TURNED[-1])
+        finish_turned(TURNED_EVEN[-1])
         late = values_at(h_place(LAST - 5)).bitcast(F32).rearrange("p (n o) -> p n o", o=D_OUT)
         nc.gpsimd.tensor_tensor(out=late, in0=sums_late[:], in1=bias_rows, op=ALU.add)
         nc.sync.dma_start(out=out_view(GPSIMD_PAIR), in_=late)
-        scale_both(LAST - 1)
+        scale_x(LAST - 1)
+        scale_x(LAST)
         make_h(LAST - 3)
         make_out(LAST - 5)
         make_out(LAST - 6)

@@ -32,7 +32,7 @@ PAIR_WORDS = PAIR_COLS // PACK
 ROUNDS = PAIRS // 2
 X_HALF, H_HALF = slice(0, 2 * PAIR_WORDS), slice(2 * PAIR_WORDS, 4 * PAIR_WORDS)
 ROUND_TILES = 5
-SCALAR_COLS = 256
+SCALAR_COLS = 384
 BIASED_TILES = 4
 TURNED_EVEN = range(0, 2 * ROUNDS - 7, 2)
 TURNED_ODD = range(7, 2 * ROUNDS - 9, 6)
@@ -89,10 +89,10 @@ def tile_replaced_compose_lora_pa_t_w4_kernel(
         load_x(0, 1)
         load_x(1, 1)
         nc.sync.dma_start(out=scale_col[:], in_=x_scale.rearrange("a b (p t) -> p (a b t)", t=PACK))
-        load_x(2, 2)
         nc.sync.dma_start(out=a_sb[:, 0 : 2 * D], in_=a_rows[:, 0 : 2 * D])
-        load_x(4, 2)
+        load_x(2, 2)
         nc.sync.dma_start(out=a_sb[:, 2 * D :], in_=a_rows[:, 2 * D :])
+        load_x(4, 2)
         nc.sync.dma_start(out=lw_row[:], in_=lora_weights.unsqueeze(0))
         b_rows = lora_B.rearrange("n o r -> n (o r)")
         b_run = RANK * D_OUT - (RANK - PACK)
@@ -119,9 +119,8 @@ def tile_replaced_compose_lora_pa_t_w4_kernel(
         b_codes = keep.tile([P, D_OUT], U32, name="b_codes", align_bytes=64)
         b_scales = keep.tile([P, D_OUT], U8, name="b_scales", align_bytes=64)
         a_values = keep.tile([P, PACK * NR], BF16, name="a_values", align_bytes=64)
-        b_values = keep.tile([P, PACK * D_OUT], BF16, name="b_values", align_bytes=64)
 
-        cast, x_banks, out_banks, biased = {}, {}, {}, {}
+        cast, ahead, x_banks, out_banks, biased = {}, {}, {}, {}, {}
         round_values, round_codes = {}, {}
 
         def x_place(i):
@@ -130,13 +129,15 @@ def tile_replaced_compose_lora_pa_t_w4_kernel(
         def h_place(i):
             return i // 2 + 2 + i % 2, 2 + i % 2
 
-        def turn(rows, tiles, kind):
-            words = rows.bitcast(F32)
-            turned = bank(kind, [P, 2, tiles, P])
-            for j in range(tiles):
+        def turn(rows, kind):
+            turned = bank(kind, [P, 2, len(rows), P])
+            for j, row in enumerate(rows):
                 for u in range(2):
-                    nc.tensor.transpose(turned[:, u, j, :], words[:, 256 * j + u : 256 * (j + 1) : 2], ident[:])
+                    nc.tensor.transpose(turned[:, u, j, :], row.bitcast(F32)[:, u::2], ident[:])
             return turned
+
+        def two_rows(cols):
+            return [cols[:, 0:D], cols[:, D : 2 * D]]
 
         def values_at(place):
             r, quarter = place
@@ -150,10 +151,10 @@ def tile_replaced_compose_lora_pa_t_w4_kernel(
             c, cols = x_part(first_pair, lo, hi)
             copy(out=dst[:, lo:hi], in_=xb[c][:, cols].bitcast(FP8))
             for n in range(pairs):
-                cast[first_pair + n] = dst[:, n * PAIR_COLS : (n + 1) * PAIR_COLS]
+                cast[first_pair + n] = two_rows(dst[:, n * PAIR_COLS : (n + 1) * PAIR_COLS])
 
         def turn_x(i, kind="turn"):
-            x_banks[i] = turn(cast[i], 2, kind)
+            x_banks[i] = turn(cast[i], kind)
 
         def scale_into(values, turned):
             tokens = values.shape[1] // PACK
@@ -281,7 +282,7 @@ def tile_replaced_compose_lora_pa_t_w4_kernel(
             cols = slice(half * 2 * D, (half + 1) * 2 * D)
             nc.scalar.copy(
                 out=a_values[:, cols].bitcast(F32).rearrange("p (n u) -> p n u", u=2),
-                in_=turn(a_sb[:, cols], 2, "h")[:].rearrange("p u j r -> p (j r) u"),
+                in_=turn(two_rows(a_sb[:, cols]), "h")[:].rearrange("p u j r -> p (j r) u"),
             )
 
         def quantise_a(half):
@@ -300,33 +301,34 @@ def tile_replaced_compose_lora_pa_t_w4_kernel(
         first_cast(nc.vector.tensor_copy, 1, 0, PAIR_COLS)
         first_cast(nc.gpsimd.tensor_copy, 2, 0, PAIR_COLS)
         first_cast(nc.scalar.copy, 3, 0, PAIR_COLS)
-        first_cast(nc.gpsimd.tensor_copy, 4, 0, PAIR_COLS)
+        first_tiles = [turn([row], "out") for row in cast[0]]
+        turn_x(1)
+        turn_a(0)
+        turn_a(1)
+        turn_x(2)
+        turn_x(3, "out")
         nc.scalar.activation(
             out=coef_row[0:1, :].rearrange("p (n q) -> p n q", q=PACK),
             in_=lw_row[:].unsqueeze(2).to_broadcast([1, ADAPTERS, PACK]),
             func=ACT.Copy,
             scale=ALPHA_OVER_RANK,
         )
-        first_tiles = [turn(cast[0][:, j * D : (j + 1) * D], 1, "out") for j in range(2)]
-        turn_x(1)
-        turn_a(0)
-        turn_a(1)
         coef_bank = bank("h", [P, P])
         nc.tensor.transpose(coef_bank[:], coef_row[:], ident[:])
         nc.scalar.copy(out=coef[:], in_=coef_bank[:, 0:1])
-        nc.scalar.activation(
-            out=b_values[:].rearrange("p (o t) -> p o t", t=PACK), in_=b_sb[:, :, 0:PACK], func=ACT.Copy, scale=coef[:]
-        )
-        turn_x(2)
-        turn_x(3, "out")
+        first_cast(nc.scalar.copy, 4, 0, PAIR_COLS)
         for j in range(2):
             scale_into(values_at(x_place(0))[:, j * D : (j + 1) * D], first_tiles[j])
         scale_x(1)
         quantise_a(0)
         quantise(1, X_HALF)
         quantise_a(1)
-        cast_x(nc.gpsimd.tensor_copy, FIRST_PAIRS, 1, values_at(x_place(1)), 0, PAIR_COLS)
+        cast_x(nc.gpsimd.tensor_copy, FIRST_PAIRS, 1, a_values[:, 2 * D :], 0, PAIR_COLS)
         make_h(0)
+        b_values = values_at((2, 3))
+        nc.scalar.activation(
+            out=b_values.rearrange("p (o t) -> p o t", t=PACK), in_=b_sb[:, :, 0:PACK], func=ACT.Copy, scale=coef[:]
+        )
         make_h(1)
         scale_x(2)
         scale_x(3)
@@ -335,9 +337,11 @@ def tile_replaced_compose_lora_pa_t_w4_kernel(
         def vector_adds(i):
             return i >= 0 and i not in TURNED
 
+        def cast_into(r):
+            return round_values[r][:, 2 * PAIR_COLS :] if r == 2 else round_values[r][:, 0 : 2 * PAIR_COLS]
+
         def begin_round(r):
             if r == 2:
-                nc.vector.quantize_mx(out=b_codes[:].bitcast(FP8X4), scales=b_scales[:], in_=b_values[:])
                 quantise_quarter(h_place(0))
             if vector_adds(2 * r - 9):
                 quantise(r, slice(X_HALF.start, H_HALF.stop))
@@ -345,13 +349,19 @@ def tile_replaced_compose_lora_pa_t_w4_kernel(
                 if r > 2:
                     quantise(r, H_HALF)
                 quantise(r, X_HALF)
+            if r == 2:
+                nc.vector.quantize_mx(out=b_codes[:].bitcast(FP8X4), scales=b_scales[:], in_=b_values)
 
         for r in range(2, ROUNDS - 1):
             even_x, odd_x = 2 * r, 2 * r + 1
             even_out, odd_out = 2 * r - 4, 2 * r - 5
             begin_round(r)
-            cut = 2 * PAIR_COLS - (0 if vector_adds(odd_out - 2) else SCALAR_COLS)
-            cast_x(nc.gpsimd.tensor_copy, even_x + 2, 2, round_values[r], 0, cut)
+            cut = 2 * PAIR_COLS - (SCALAR_COLS if odd_out - 2 < 0 else 0)
+            if odd_out - 2 in TURNED:
+                cast_x(nc.gpsimd.tensor_copy, even_x + 2, 2, cast_into(r), 0, cut - D)
+                cast[odd_x + 2][1] = ahead.pop(r)[:]
+            else:
+                cast_x(nc.gpsimd.tensor_copy, even_x + 2, 2, cast_into(r), 0, cut)
             turn_x(even_x)
             turn_x(odd_x)
             if even_out - 2 in TURNED:
@@ -366,7 +376,11 @@ def tile_replaced_compose_lora_pa_t_w4_kernel(
             if odd_out - 2 in TURNED:
                 store_turned(odd_out - 2)
             if cut < 2 * PAIR_COLS:
-                cast_x(nc.scalar.copy, even_x + 2, 2, round_values[r], cut, 2 * PAIR_COLS)
+                cast_x(nc.scalar.copy, even_x + 2, 2, cast_into(r), cut, 2 * PAIR_COLS)
+            if odd_out + 2 in TURNED:
+                ahead[r + 2] = work.tile([P, D], BF16, name="ahead", tag="ahead", bufs=2, align_bytes=64)
+                c, cols = x_part(odd_x + 6, D, 2 * D)
+                nc.scalar.copy(out=ahead[r + 2][:], in_=xb[c][:, cols].bitcast(FP8))
             make_out(even_out)
             add_bias_turned(even_out)
             if odd_out >= 0:

@@ -21,23 +21,21 @@ ACT = mybir.ActivationFunctionType
 
 P = 128
 PACK = 4
-CHUNK_PAIRS = 4
-CHUNKS = TOKENS // (P * 2 * CHUNK_PAIRS)
-PAIRS = TOKENS // (2 * P)
+CHUNK_ROWS = 8
+ROWS = TOKENS // P
+CHUNKS = ROWS // CHUNK_ROWS
+PAIRS = ROWS // 2
 LAST = PAIRS - 1
+ROUNDS = PAIRS // 2
 
 PAIR_COLS = 2 * D
 PAIR_WORDS = PAIR_COLS // PACK
-
-ROUNDS = PAIRS // 2
-X_HALF, H_HALF = slice(0, 2 * PAIR_WORDS), slice(2 * PAIR_WORDS, 4 * PAIR_WORDS)
 ROUND_TILES = 5
-SCALAR_COLS = 384
-BIASED_TILES = 4
-TURNED_EVEN = range(0, 2 * ROUNDS - 7, 2)
-TURNED_ODD = range(7, 2 * ROUNDS - 9, 6)
-TURNED = list(TURNED_EVEN) + list(TURNED_ODD)
-GPSIMD_PAIR = 2 * ROUNDS - 9
+RAW_TILES = 4
+SHARED_ROUNDS = range(3, ROUNDS)
+HANDED_ROUNDS = ()
+VECTOR_ROWS = 1
+HANDED = [2 * r - 6 + n for r in HANDED_ROUNDS for n in range(2)]
 FIRST_PAIRS = 5
 
 
@@ -45,8 +43,8 @@ def tile_replaced_compose_lora_pa_t_w4_kernel(
     tc, x_bytes, x_scale, lora_A, lora_B, W_words, W_scales, bias, lora_weights, out
 ):
     nc = tc.nc
-    x_rows = x_bytes.rearrange("b s d -> (b s) d").rearrange("(c p n) d -> c p (n d)", p=P, n=2 * CHUNK_PAIRS)
-    out_rows = out.rearrange("b s o -> (b s) o").rearrange("(c p n) o -> c p n o", p=P, n=2 * CHUNK_PAIRS)
+    x_rows = x_bytes.rearrange("b s d -> (b s) d").rearrange("(c p n) d -> c p (n d)", p=P, n=CHUNK_ROWS)
+    out_rows = out.rearrange("b s o -> (b s) o").rearrange("(c p n) o -> c p n o", p=P, n=CHUNK_ROWS)
 
     with ExitStack() as ctx:
         keep = ctx.enter_context(tc.tile_pool(name="keep", bufs=1))
@@ -61,7 +59,7 @@ def tile_replaced_compose_lora_pa_t_w4_kernel(
         nc.vector.memset(ident[:], 0.0)
         make_identity(nc, ident[:], nomemset=True)
 
-        xb = [keep.tile([P, 2 * CHUNK_PAIRS * D], U8, name="xb%d" % c, align_bytes=64) for c in range(CHUNKS)]
+        xb = keep.tile([P, ROWS * D], U8, name="xb", align_bytes=64)
         scale_col = keep.tile([P, PACK], F32, name="scale_col")
         first = keep.tile([P, FIRST_PAIRS * PAIR_COLS], BF16, name="first", align_bytes=64)
         a_sb = keep.tile([P, PACK * D], BF16, name="a_sb", align_bytes=64)
@@ -69,31 +67,26 @@ def tile_replaced_compose_lora_pa_t_w4_kernel(
         w_sb = keep.tile([P, 2 * D_OUT], U8, name="w_sb", align_bytes=64)
         w_sc = keep.tile([P, D_OUT], U8, name="w_sc", align_bytes=64)
         bias_sb = keep.tile([P, D_OUT], BF16, name="bias_sb", align_bytes=64)
-        bias_col = keep.tile([P, 2, 16], BF16, name="bias_col", align_bytes=64)
         lw_row = keep.tile([1, ADAPTERS], BF16, name="lw_row")
         coef_row = keep.tile([P, P], F32, name="coef_row")
         nc.vector.memset(coef_row[:], 0.0)
         coef = keep.tile([P, 1], F32, name="coef")
-
         nc.vector.memset(w_sc[:].bitcast(I32), 0)
         a_rows = lora_A.rearrange("n r d -> (n r) d").rearrange("(m t) d -> m (t d)", t=PACK)
 
-        def x_part(first_pair, lo, hi):
-            c, q = divmod(first_pair, CHUNK_PAIRS)
-            return c, slice(q * PAIR_COLS + lo, q * PAIR_COLS + hi)
+        def load_x(row, rows):
+            c, n = divmod(row, CHUNK_ROWS)
+            nc.sync.dma_start(out=xb[:, row * D : (row + rows) * D], in_=x_rows[c][:, n * D : (n + rows) * D])
 
-        def load_x(first_pair, pairs):
-            c, cols = x_part(first_pair, 0, pairs * PAIR_COLS)
-            nc.sync.dma_start(out=xb[c][:, cols], in_=x_rows[c][:, cols])
-
-        load_x(0, 1)
-        load_x(1, 1)
+        load_x(0, 2)
+        load_x(2, 2)
         nc.sync.dma_start(out=scale_col[:], in_=x_scale.rearrange("a b (p t) -> p (a b t)", t=PACK))
         nc.sync.dma_start(out=a_sb[:, 0 : 2 * D], in_=a_rows[:, 0 : 2 * D])
-        load_x(2, 2)
+        load_x(4, 4)
         nc.sync.dma_start(out=a_sb[:, 2 * D :], in_=a_rows[:, 2 * D :])
-        load_x(4, 2)
+        load_x(8, 4)
         nc.sync.dma_start(out=lw_row[:], in_=lora_weights.unsqueeze(0))
+        load_x(12, 4)
         b_rows = lora_B.rearrange("n o r -> n (o r)")
         b_run = RANK * D_OUT - (RANK - PACK)
         for q in range(PACK):
@@ -101,33 +94,34 @@ def tile_replaced_compose_lora_pa_t_w4_kernel(
                 out=b_sb[:].rearrange("p o r -> p (o r)")[q:P:PACK, 0:b_run],
                 in_=b_rows[:, PACK * q : PACK * q + b_run],
             )
-        load_x(6, 2)
+        load_x(16, 4)
         nc.sync.dma_start(out=w_sb[:], in_=W_words[0])
         for q in range(4):
             nc.sync.dma_start(
                 out=w_sc[32 * q : 32 * q + 4, :].bitcast(I32), in_=W_scales[0, 4 * q : 4 * q + 4, :].bitcast(I32)
             )
-        for half in range(2):
-            nc.sync.dma_start(out=bias_col[:, half, 0:1], in_=bias[half * P : (half + 1) * P].unsqueeze(1))
-        nc.sync.dma_start(out=xb[2][:], in_=x_rows[2])
+        load_x(20, 4)
         nc.sync.dma_start(out=bias_sb[:], in_=bias.partition_broadcast(P))
-        for c in range(3, CHUNKS):
-            nc.sync.dma_start(out=xb[c][:], in_=x_rows[c])
+        load_x(3 * CHUNK_ROWS, CHUNK_ROWS)
+        for c in range(4, CHUNKS):
+            load_x(c * CHUNK_ROWS, CHUNK_ROWS)
 
         a_codes = keep.tile([P, NR], U32, name="a_codes", align_bytes=64)
         a_scales = keep.tile([P, NR], U8, name="a_scales", align_bytes=64)
         b_codes = keep.tile([P, D_OUT], U32, name="b_codes", align_bytes=64)
         b_scales = keep.tile([P, D_OUT], U8, name="b_scales", align_bytes=64)
         a_values = keep.tile([P, PACK * NR], BF16, name="a_values", align_bytes=64)
+        b_values = keep.tile([P, PACK * D_OUT], BF16, name="b_values", align_bytes=64)
 
-        cast, ahead, x_banks, out_banks, biased = {}, {}, {}, {}, {}
+        scale_rows = keep.tile([P, D], F32, name="scale_rows", align_bytes=64)
+        cast, x_banks, h_banks, out_banks, sums = {}, {}, {}, {}, {}
         round_values, round_codes = {}, {}
 
         def x_place(i):
-            return i // 2 + 1, i % 2
+            return i // 2 + 1, 2 + i % 2
 
         def h_place(i):
-            return i // 2 + 2 + i % 2, 2 + i % 2
+            return i // 2 + 2 + i % 2, i % 2
 
         def turn(rows, kind):
             turned = bank(kind, [P, 2, len(rows), P])
@@ -135,9 +129,6 @@ def tile_replaced_compose_lora_pa_t_w4_kernel(
                 for u in range(2):
                     nc.tensor.transpose(turned[:, u, j, :], row.bitcast(F32)[:, u::2], ident[:])
             return turned
-
-        def two_rows(cols):
-            return [cols[:, 0:D], cols[:, D : 2 * D]]
 
         def values_at(place):
             r, quarter = place
@@ -147,14 +138,46 @@ def tile_replaced_compose_lora_pa_t_w4_kernel(
                 )
             return round_values[r][:, quarter * PAIR_COLS : (quarter + 1) * PAIR_COLS]
 
-        def cast_x(copy, first_pair, pairs, dst, lo, hi):
-            c, cols = x_part(first_pair, lo, hi)
-            copy(out=dst[:, lo:hi], in_=xb[c][:, cols].bitcast(FP8))
-            for n in range(pairs):
-                cast[first_pair + n] = two_rows(dst[:, n * PAIR_COLS : (n + 1) * PAIR_COLS])
+        def cast_x(copy, i, dst, lo=0):
+            cols = dst.shape[1]
+            copy(out=dst[:, lo:], in_=xb[:, i * PAIR_COLS + lo : i * PAIR_COLS + cols].bitcast(FP8))
+            for n in range(cols // PAIR_COLS):
+                cast[i + n] = dst[:, n * PAIR_COLS : (n + 1) * PAIR_COLS]
+
+        def cast_first(copy, i, pairs=1):
+            cast_x(copy, i, first[:, i * PAIR_COLS : (i + pairs) * PAIR_COLS])
+
+        def raw_tile():
+            return work.tile([P, PAIR_COLS], BF16, name="raw", tag="raw", bufs=RAW_TILES, align_bytes=64)
+
+        def cast_raw(i):
+            cast_x(nc.scalar.copy, i, raw_tile()[:])
+
+        def cast_row(copy, i, j):
+            if i not in cast:
+                cast[i] = raw_tile()[:]
+            copy(out=cast[i][:, j * D : (j + 1) * D], in_=xb[:, (2 * i + j) * D : (2 * i + j + 1) * D].bitcast(FP8))
+
+        def scale_before(i, dst):
+            nc.gpsimd.tensor_tensor(
+                out=dst.rearrange("p (j d) -> p j d", j=2),
+                in0=cast[i].rearrange("p (j d) -> p j d", j=2),
+                in1=scale_rows[:].unsqueeze(1).to_broadcast([P, 2, D]),
+                op=ALU.mult,
+            )
+            cast[i] = dst
+
+        def h_half(r):
+            return round_values[r][:, 0 : 2 * PAIR_COLS]
 
         def turn_x(i, kind="turn"):
-            x_banks[i] = turn(cast[i], kind)
+            x_banks[i] = turn([cast[i][:, 0:D], cast[i][:, D:]], kind)
+
+        def copy_words(values, turned):
+            nc.scalar.copy(
+                out=values.bitcast(F32).rearrange("p (n u) -> p n u", u=2),
+                in_=turned[:].rearrange("p u j r -> p (j r) u"),
+            )
 
         def scale_into(values, turned):
             tokens = values.shape[1] // PACK
@@ -168,7 +191,7 @@ def tile_replaced_compose_lora_pa_t_w4_kernel(
         def scale_x(i):
             scale_into(values_at(x_place(i)), x_banks.pop(i))
 
-        def quantise(r, words):
+        def quantise(r, lo, width):
             if r not in round_codes:
                 round_codes[r] = (
                     work.tile([P, 4 * PAIR_WORDS], U32, name="codes", tag="codes", bufs=ROUND_TILES, align_bytes=64),
@@ -176,14 +199,13 @@ def tile_replaced_compose_lora_pa_t_w4_kernel(
                 )
             codes, scales = round_codes[r]
             nc.vector.quantize_mx(
-                out=codes[:, words].bitcast(FP8X4),
-                scales=scales[:, words],
-                in_=round_values[r][:, PACK * words.start : PACK * words.stop],
+                out=codes[:, lo : lo + width].bitcast(FP8X4),
+                scales=scales[:, lo : lo + width],
+                in_=round_values[r][:, PACK * lo : PACK * (lo + width)],
             )
 
-        def quantise_quarter(place):
-            r, quarter = place
-            quantise(r, slice(quarter * PAIR_WORDS, (quarter + 1) * PAIR_WORDS))
+        def quantise_quarters(r, quarter, count):
+            quantise(r, quarter * PAIR_WORDS, count * PAIR_WORDS)
 
         def mx(acc, stationary, moving, start, stop):
             nc.tensor.matmul_mx(
@@ -207,83 +229,56 @@ def tile_replaced_compose_lora_pa_t_w4_kernel(
             r, quarter = h_place(i)
             return e4m3(*round_codes[r], quarter * PAIR_WORDS + j * P, tiles * P)
 
-        def w_cols(half):
-            return w_sb[:, half * 2 * P : (half + 1) * 2 * P].bitcast(FP4X4), w_sc[:, half * P : (half + 1) * P]
+        def make_h(i, j):
+            h_banks[i, j] = bank("h", [P, PACK, P])
+            for t in range(PACK):
+                mx(h_banks[i, j][:, t, :], e4m3(a_codes, a_scales, t * P, P), x_cols(i, j, 1), True, True)
 
-        def make_h(i):
-            banks = []
-            for j in range(2):
-                banks.append(bank("h", [P, PACK, P]))
-                for t in range(PACK):
-                    mx(banks[j][:, t, :], e4m3(a_codes, a_scales, t * P, P), x_cols(i, j, 1), True, True)
-            values = values_at(h_place(i))
-            for j in range(2):
-                nc.scalar.copy(
-                    out=values[:, j * NR : (j + 1) * NR].rearrange("p (r t) -> p r t", t=PACK),
-                    in_=banks[j][:].rearrange("p t r -> p r t"),
-                )
+        def round_h(i, j):
+            nc.scalar.copy(
+                out=values_at(h_place(i))[:, j * NR : (j + 1) * NR].rearrange("p (r t) -> p r t", t=PACK),
+                in_=h_banks.pop((i, j))[:].rearrange("p t r -> p r t"),
+            )
 
         def out_tile(i, j, acc):
             mx(acc, h_cols(i, j, 1), e4m3(b_codes, b_scales, 0, D_OUT), True, False)
             mx(acc, x_cols(i, j, 1), (w_sb[:].bitcast(FP4X4), w_sc[:]), False, True)
 
-        def out_half_turned(i, half, acc):
-            mx(acc, e4m3(b_codes, b_scales, half * P, P), h_cols(i, 0, 2), True, False)
-            mx(acc, w_cols(half), x_cols(i, 0, 2), False, True)
-
         def make_out(i):
             out_banks[i] = bank("out", [P, 2, D_OUT])
-            for side in range(2):
-                (out_half_turned if i in TURNED else out_tile)(i, side, out_banks[i][:, side, :])
+            for j in range(2):
+                out_tile(i, j, out_banks[i][:, j, :])
 
         def result_tile():
-            return work.tile([P, 2, D_OUT], F32, name="result", tag="result", bufs=PAIRS, align_bytes=64)
+            return work.tile([P, 2, D_OUT], F32, name="result", tag="result", bufs=PAIRS - len(HANDED), align_bytes=64)
 
         def out_view(i):
-            c, q = divmod(i, CHUNK_PAIRS)
+            c, q = divmod(i, CHUNK_ROWS // 2)
             return out_rows[c][:, 2 * q : 2 * q + 2, :]
 
-        bias_rows = bias_sb[:].unsqueeze(1).to_broadcast([P, 2, D_OUT])
+        def bias_rows(rows):
+            return bias_sb[:].unsqueeze(1).to_broadcast([P, rows, D_OUT])
 
         def finish(i):
             result = result_tile()
-            nc.vector.tensor_tensor(out=result[:], in0=out_banks.pop(i)[:], in1=bias_rows, op=ALU.add)
+            nc.vector.tensor_tensor(out=result[:], in0=out_banks.pop(i)[:], in1=bias_rows(2), op=ALU.add)
             nc.sync.dma_start(out=out_view(i), in_=result[:])
 
-        def add_bias_turned(i):
-            biased[i] = work.tile([P, 2, 2 * P], F32, name="biased", tag="biased", bufs=BIASED_TILES, align_bytes=64)
-            for half in range(2):
-                nc.scalar.activation(
-                    out=biased[i][:, half, :],
-                    in_=out_banks[i][:, half, :],
-                    func=ACT.Identity,
-                    bias=bias_col[:, half, 0:1],
-                    scale=1.0,
-                )
+        def hand_over(i):
+            r, n = divmod(i + 6, 2)
+            if n == 0:
+                sums[r] = work.tile([P, 4, D_OUT], F32, name="sums", tag="sums", bufs=2, align_bytes=64)
+            nc.scalar.copy(out=sums[r][:, 2 * n : 2 * n + 2, :], in_=out_banks.pop(i)[:])
 
-        def finish_turned(i):
-            turn_back(i)
-            store_turned(i)
-
-        def turn_back(i):
-            sums, acc = biased.pop(i), out_banks[i]
-            for j in range(2):
-                for half in range(2):
-                    nc.tensor.transpose(
-                        acc[:, j, half * P : (half + 1) * P], sums[:, half, j * P : (j + 1) * P], ident[:]
-                    )
-
-        def store_turned(i):
-            result = result_tile()
-            nc.scalar.copy(out=result[:], in_=out_banks.pop(i)[:])
-            nc.sync.dma_start(out=out_view(i), in_=result[:])
+        def finish_handed(r):
+            result = h_half(r + 1).bitcast(F32).rearrange("p (n o) -> p n o", o=D_OUT)
+            nc.gpsimd.tensor_tensor(out=result, in0=sums.pop(r)[:], in1=bias_rows(4), op=ALU.add)
+            for n in range(2):
+                nc.sync.dma_start(out=out_view(2 * r - 6 + n), in_=result[:, 2 * n : 2 * n + 2, :])
 
         def turn_a(half):
-            cols = slice(half * 2 * D, (half + 1) * 2 * D)
-            nc.scalar.copy(
-                out=a_values[:, cols].bitcast(F32).rearrange("p (n u) -> p n u", u=2),
-                in_=turn(two_rows(a_sb[:, cols]), "h")[:].rearrange("p u j r -> p (j r) u"),
-            )
+            rows = [a_sb[:, (2 * half + n) * D : (2 * half + n + 1) * D] for n in range(2)]
+            copy_words(a_values[:, half * 2 * D : (half + 1) * 2 * D], turn(rows, "h"))
 
         def quantise_a(half):
             words = slice(half * 2 * P, (half + 1) * 2 * P)
@@ -293,15 +288,12 @@ def tile_replaced_compose_lora_pa_t_w4_kernel(
                 in_=a_values[:, half * 2 * D : (half + 1) * 2 * D],
             )
 
-        def first_cast(copy, i, lo, hi):
-            cast_x(copy, i, 1, first[:, i * PAIR_COLS : (i + 1) * PAIR_COLS], lo, hi)
-
-        first_cast(nc.vector.tensor_copy, 0, 0, D)
-        first_cast(nc.scalar.copy, 0, D, PAIR_COLS)
-        first_cast(nc.vector.tensor_copy, 1, 0, PAIR_COLS)
-        first_cast(nc.gpsimd.tensor_copy, 2, 0, PAIR_COLS)
-        first_cast(nc.scalar.copy, 3, 0, PAIR_COLS)
-        first_tiles = [turn([row], "out") for row in cast[0]]
+        nc.vector.tensor_copy(out=first[:, 0:D], in_=xb[:, 0:D].bitcast(FP8))
+        cast_x(nc.scalar.copy, 0, first[:, 0:PAIR_COLS], D)
+        cast_first(nc.vector.tensor_copy, 1)
+        cast_first(nc.gpsimd.tensor_copy, 2)
+        cast_first(nc.scalar.copy, 3)
+        first_tiles = [turn([cast[0][:, j * D : (j + 1) * D]], "out") for j in range(2)]
         turn_x(1)
         turn_a(0)
         turn_a(1)
@@ -316,116 +308,104 @@ def tile_replaced_compose_lora_pa_t_w4_kernel(
         coef_bank = bank("h", [P, P])
         nc.tensor.transpose(coef_bank[:], coef_row[:], ident[:])
         nc.scalar.copy(out=coef[:], in_=coef_bank[:, 0:1])
-        first_cast(nc.scalar.copy, 4, 0, PAIR_COLS)
+        cast_first(nc.scalar.copy, 4)
         for j in range(2):
             scale_into(values_at(x_place(0))[:, j * D : (j + 1) * D], first_tiles[j])
         scale_x(1)
         quantise_a(0)
-        quantise(1, X_HALF)
+        quantise_quarters(1, 2, 2)
         quantise_a(1)
-        cast_x(nc.gpsimd.tensor_copy, FIRST_PAIRS, 1, a_values[:, 2 * D :], 0, PAIR_COLS)
-        make_h(0)
-        b_values = values_at((2, 3))
-        nc.scalar.activation(
-            out=b_values.rearrange("p (o t) -> p o t", t=PACK), in_=b_sb[:, :, 0:PACK], func=ACT.Copy, scale=coef[:]
-        )
-        make_h(1)
-        scale_x(2)
-        scale_x(3)
-        sums_late = keep.tile([P, 2, D_OUT], F32, name="sums_late", align_bytes=64)
 
-        def vector_adds(i):
-            return i >= 0 and i not in TURNED
-
-        def cast_into(r):
-            return round_values[r][:, 2 * PAIR_COLS :] if r == 2 else round_values[r][:, 0 : 2 * PAIR_COLS]
-
-        def begin_round(r):
+        for r in range(1, ROUNDS):
+            even_h, odd_h = 2 * r - 2, 2 * r - 1
+            outs = [i for i in (2 * r - 5, 2 * r - 4) if i >= 0]
             if r == 2:
-                quantise_quarter(h_place(0))
-            if vector_adds(2 * r - 9):
-                quantise(r, slice(X_HALF.start, H_HALF.stop))
+                quantise_quarters(r, 0, 1)
+            elif r > 2:
+                if r + 1 < ROUNDS:
+                    cast_row(nc.vector.tensor_copy, 2 * r + 2, 1)
+                quantise_quarters(r, 0, 2)
+            if r > 1:
+                quantise_quarters(r, 2, 2)
+            if r == 1:
+                cast_x(nc.gpsimd.tensor_copy, 5, a_values[:])
+            elif r == 2:
+                nc.vector.quantize_mx(out=b_codes[:].bitcast(FP8X4), scales=b_scales[:], in_=b_values[:])
+                scale_before(2 * r + 3, b_values[:])
+            elif r + 1 < ROUNDS:
+                scale_before(2 * r + 3, h_half(r)[:, 0:PAIR_COLS])
+            scale_x(2 * r)
+            if r in SHARED_ROUNDS:
+                copy_words(values_at(x_place(2 * r + 1)), x_banks.pop(2 * r + 1))
             else:
-                if r > 2:
-                    quantise(r, H_HALF)
-                quantise(r, X_HALF)
-            if r == 2:
-                nc.vector.quantize_mx(out=b_codes[:].bitcast(FP8X4), scales=b_scales[:], in_=b_values)
+                scale_x(2 * r + 1)
+            if r > 2 and r + 1 < ROUNDS:
+                cast_row(nc.scalar.copy, 2 * r + 2, 0)
+            if len(outs) == 2:
+                make_out(outs[0])
+            make_h(even_h, 0)
+            make_h(even_h, 1)
+            round_h(even_h, 0)
+            round_h(even_h, 1)
+            if r == 1:
+                nc.scalar.activation(
+                    out=b_values[:].rearrange("p (o t) -> p o t", t=PACK),
+                    in_=b_sb[:, :, 0:PACK],
+                    func=ACT.Copy,
+                    scale=coef[:],
+                )
+            if outs:
+                make_out(outs[-1])
+            if r + 2 < ROUNDS:
+                cast_raw(2 * r + 5)
+            for i in (2 * r - 6, 2 * r - 5):
+                if i >= 0:
+                    (hand_over if i in HANDED else finish)(i)
+            make_h(odd_h, 0)
+            make_h(odd_h, 1)
+            if r == 1:
+                spread = bank("out", [P, PACK, P])
+                for t in range(PACK):
+                    nc.tensor.transpose(spread[:, t, :], scale_col[:, t : t + 1].to_broadcast([P, P]), ident[:])
+                nc.scalar.copy(
+                    out=scale_rows[:].rearrange("p (m t) -> p m t", t=PACK), in_=spread[:].rearrange("p t m -> p m t")
+                )
+            round_h(odd_h, 0)
+            round_h(odd_h, 1)
+            if r + 1 < ROUNDS:
+                turn_x(2 * r + 2)
+                turn_x(2 * r + 3)
 
-        for r in range(2, ROUNDS - 1):
-            even_x, odd_x = 2 * r, 2 * r + 1
-            even_out, odd_out = 2 * r - 4, 2 * r - 5
-            begin_round(r)
-            cut = 2 * PAIR_COLS - (SCALAR_COLS if odd_out - 2 < 0 else 0)
-            if odd_out - 2 in TURNED:
-                cast_x(nc.gpsimd.tensor_copy, even_x + 2, 2, cast_into(r), 0, cut - D)
-                cast[odd_x + 2][1] = ahead.pop(r)[:]
-            else:
-                cast_x(nc.gpsimd.tensor_copy, even_x + 2, 2, cast_into(r), 0, cut)
-            turn_x(even_x)
-            turn_x(odd_x)
-            if even_out - 2 in TURNED:
-                finish_turned(even_out - 2)
-            if odd_out - 2 in TURNED:
-                turn_back(odd_out - 2)
-            scale_x(even_x)
-            scale_x(odd_x)
-            if vector_adds(odd_out - 2):
-                finish(odd_out - 2)
-            make_h(even_x - 2)
-            if odd_out - 2 in TURNED:
-                store_turned(odd_out - 2)
-            if cut < 2 * PAIR_COLS:
-                cast_x(nc.scalar.copy, even_x + 2, 2, cast_into(r), cut, 2 * PAIR_COLS)
-            if odd_out + 2 in TURNED:
-                ahead[r + 2] = work.tile([P, D], BF16, name="ahead", tag="ahead", bufs=2, align_bytes=64)
-                c, cols = x_part(odd_x + 6, D, 2 * D)
-                nc.scalar.copy(out=ahead[r + 2][:], in_=xb[c][:, cols].bitcast(FP8))
-            make_out(even_out)
-            add_bias_turned(even_out)
-            if odd_out >= 0:
-                make_out(odd_out)
-            if odd_out in TURNED:
-                add_bias_turned(odd_out)
-            if odd_out == GPSIMD_PAIR:
-                nc.scalar.copy(out=sums_late[:], in_=out_banks.pop(odd_out)[:])
-            make_h(odd_x - 2)
-
-        begin_round(ROUNDS - 1)
-        turn_x(LAST - 1)
-        turn_x(LAST)
-        finish_turned(TURNED_EVEN[-1])
-        late = values_at(h_place(LAST - 5)).bitcast(F32).rearrange("p (n o) -> p n o", o=D_OUT)
-        nc.gpsimd.tensor_tensor(out=late, in0=sums_late[:], in1=bias_rows, op=ALU.add)
-        nc.sync.dma_start(out=out_view(GPSIMD_PAIR), in_=late)
-        scale_x(LAST - 1)
-        scale_x(LAST)
-        make_h(LAST - 3)
-        make_out(LAST - 5)
-        make_out(LAST - 6)
-        make_h(LAST - 2)
-        quantise_quarter(h_place(LAST - 4))
-        quantise_quarter(x_place(LAST - 1))
-        finish(LAST - 6)
-        quantise_quarter(x_place(LAST))
-        quantise_quarter(h_place(LAST - 3))
-        make_h(LAST - 1)
-        make_out(LAST - 4)
-        make_h(LAST)
+        r = ROUNDS
+        quantise_quarters(r, 2, 1)
+        quantise_quarters(r, 0, 2)
+        quantise_quarters(r, 3, 1)
         finish(LAST - 5)
-        for i in range(LAST - 3, LAST - 1):
-            quantise_quarter(h_place(i + 1))
-            make_out(i)
-            finish(i - 1)
+        make_h(LAST - 1, 0)
+        make_h(LAST - 1, 1)
+        round_h(LAST - 1, 0)
+        round_h(LAST - 1, 1)
+        make_out(LAST - 4)
+        make_h(LAST, 0)
+        make_h(LAST, 1)
+        round_h(LAST, 0)
+        round_h(LAST, 1)
+        quantise_quarters(r + 1, 1, 1)
+        finish(LAST - 4)
+        make_out(LAST - 3)
+        make_out(LAST - 2)
+        finish(LAST - 3)
+        quantise_quarters(r + 1, 0, 1)
+        finish(LAST - 2)
         make_out(LAST - 1)
         last_result = result_tile()
         last_banks = []
-        r, quarter = h_place(LAST)
         for j in range(2):
-            quantise(r, slice(quarter * PAIR_WORDS + j * P, quarter * PAIR_WORDS + (j + 1) * P))
+            quantise(r + 2, PAIR_WORDS + j * P, P)
             last_banks.append(bank("h", [P, D_OUT]))
             out_tile(LAST, j, last_banks[j][:])
-            finish(LAST - 2 + j)
+            if j == 0:
+                finish(LAST - 1)
         for j in range(2):
             nc.vector.tensor_tensor(out=last_result[:, j, :], in0=last_banks[j][:], in1=bias_sb[:], op=ALU.add)
             nc.sync.dma_start(out=out_view(LAST)[:, j, :], in_=last_result[:, j, :])

@@ -31,12 +31,10 @@ ROUNDS = PAIRS // 2
 PAIR_COLS = 2 * D
 PAIR_WORDS = PAIR_COLS // PACK
 ROUND_TILES = 5
-RAW_TILES = 4
-SHARED_ROUNDS = range(3, ROUNDS)
-HANDED_ROUNDS = ()
-VECTOR_ROWS = 1
-HANDED = [2 * r - 6 + n for r in HANDED_ROUNDS for n in range(2)]
-FIRST_PAIRS = 5
+LONG_ROUNDS = (3, 9)
+SHARED_ROUNDS = [r for r in range(3, ROUNDS) if r not in LONG_ROUNDS]
+GPSIMD_CAST = {2: 8, 8: 18}
+SHORT_COLS, LONG_COLS = (512, 768), (2048, 1536)
 
 
 def tile_replaced_compose_lora_pa_t_w4_kernel(
@@ -61,7 +59,7 @@ def tile_replaced_compose_lora_pa_t_w4_kernel(
 
         xb = keep.tile([P, ROWS * D], U8, name="xb", align_bytes=64)
         scale_col = keep.tile([P, PACK], F32, name="scale_col")
-        first = keep.tile([P, FIRST_PAIRS * PAIR_COLS], BF16, name="first", align_bytes=64)
+        wide = keep.tile([P, ROWS * D], BF16, name="wide", align_bytes=64)
         a_sb = keep.tile([P, PACK * D], BF16, name="a_sb", align_bytes=64)
         b_sb = keep.tile([P, D_OUT, RANK], BF16, name="b_sb", align_bytes=64)
         w_sb = keep.tile([P, 2 * D_OUT], U8, name="w_sb", align_bytes=64)
@@ -114,7 +112,10 @@ def tile_replaced_compose_lora_pa_t_w4_kernel(
         b_values = keep.tile([P, PACK * D_OUT], BF16, name="b_values", align_bytes=64)
 
         scale_rows = keep.tile([P, D], F32, name="scale_rows", align_bytes=64)
-        cast, x_banks, h_banks, out_banks, sums = {}, {}, {}, {}, {}
+        moved, x_banks, h_banks, out_banks = {}, {}, {}, {}
+        aside = {}
+        cast_ends = [0]
+        left = [i for i in range(6, PAIRS) if i // 2 * 2 not in [GPSIMD_CAST[r] for r in GPSIMD_CAST]]
         round_values, round_codes = {}, {}
 
         def x_place(i):
@@ -138,40 +139,51 @@ def tile_replaced_compose_lora_pa_t_w4_kernel(
                 )
             return round_values[r][:, quarter * PAIR_COLS : (quarter + 1) * PAIR_COLS]
 
-        def cast_x(copy, i, dst, lo=0):
-            cols = dst.shape[1]
-            copy(out=dst[:, lo:], in_=xb[:, i * PAIR_COLS + lo : i * PAIR_COLS + cols].bitcast(FP8))
-            for n in range(cols // PAIR_COLS):
-                cast[i + n] = dst[:, n * PAIR_COLS : (n + 1) * PAIR_COLS]
+        def cast_cols(copy, lo, hi):
+            copy(out=wide[:, lo:hi], in_=xb[:, lo:hi].bitcast(FP8))
 
-        def cast_first(copy, i, pairs=1):
-            cast_x(copy, i, first[:, i * PAIR_COLS : (i + pairs) * PAIR_COLS])
+        def cast_pair(copy, i):
+            cast_cols(copy, i * PAIR_COLS, (i + 1) * PAIR_COLS)
 
-        def raw_tile():
-            return work.tile([P, PAIR_COLS], BF16, name="raw", tag="raw", bufs=RAW_TILES, align_bytes=64)
+        def cast_next(copy, cols):
+            lo = cast_ends[-1]
+            hi = min(lo + cols, len(left) * PAIR_COLS)
+            while lo < hi:
+                n = lo // PAIR_COLS
+                run = 1
+                while n + run < len(left) and left[n + run] == left[n] + run:
+                    run = run + 1
+                end = min(hi, (n + run) * PAIR_COLS)
+                shift = (left[n] - n) * PAIR_COLS
+                cast_cols(copy, lo + shift, end + shift)
+                lo = end
+            cast_ends.append(hi)
 
-        def cast_raw(i):
-            cast_x(nc.scalar.copy, i, raw_tile()[:])
+        def cast_aside(row, rows, dst):
+            nc.gpsimd.tensor_copy(out=dst, in_=xb[:, row * D : (row + rows) * D].bitcast(FP8))
+            for n in range(rows):
+                moved[row + n] = dst[:, n * D : (n + 1) * D]
 
-        def cast_row(copy, i, j):
-            if i not in cast:
-                cast[i] = raw_tile()[:]
-            copy(out=cast[i][:, j * D : (j + 1) * D], in_=xb[:, (2 * i + j) * D : (2 * i + j + 1) * D].bitcast(FP8))
+        def x_row(row):
+            i = row // 2
+            assert row in moved or i not in left or (left.index(i) + 1) * PAIR_COLS <= cast_ends[-1], row
+            return moved.get(row, wide[:, row * D : (row + 1) * D])
 
         def scale_before(i, dst):
             nc.gpsimd.tensor_tensor(
                 out=dst.rearrange("p (j d) -> p j d", j=2),
-                in0=cast[i].rearrange("p (j d) -> p j d", j=2),
+                in0=aside.get(i, wide[:, i * PAIR_COLS : (i + 1) * PAIR_COLS]).rearrange("p (j d) -> p j d", j=2),
                 in1=scale_rows[:].unsqueeze(1).to_broadcast([P, 2, D]),
                 op=ALU.mult,
             )
-            cast[i] = dst
+            x_row(2 * i)
+            moved[2 * i], moved[2 * i + 1] = dst[:, 0:D], dst[:, D:]
 
         def h_half(r):
             return round_values[r][:, 0 : 2 * PAIR_COLS]
 
         def turn_x(i, kind="turn"):
-            x_banks[i] = turn([cast[i][:, 0:D], cast[i][:, D:]], kind)
+            x_banks[i] = turn([x_row(2 * i), x_row(2 * i + 1)], kind)
 
         def copy_words(values, turned):
             nc.scalar.copy(
@@ -249,8 +261,8 @@ def tile_replaced_compose_lora_pa_t_w4_kernel(
             for j in range(2):
                 out_tile(i, j, out_banks[i][:, j, :])
 
-        def result_tile():
-            return work.tile([P, 2, D_OUT], F32, name="result", tag="result", bufs=PAIRS - len(HANDED), align_bytes=64)
+        def result_tile(i):
+            return wide[:, i * PAIR_COLS : (i + 1) * PAIR_COLS].bitcast(F32).rearrange("p (n o) -> p n o", o=D_OUT)
 
         def out_view(i):
             c, q = divmod(i, CHUNK_ROWS // 2)
@@ -260,21 +272,18 @@ def tile_replaced_compose_lora_pa_t_w4_kernel(
             return bias_sb[:].unsqueeze(1).to_broadcast([P, rows, D_OUT])
 
         def finish(i):
-            result = result_tile()
-            nc.vector.tensor_tensor(out=result[:], in0=out_banks.pop(i)[:], in1=bias_rows(2), op=ALU.add)
-            nc.sync.dma_start(out=out_view(i), in_=result[:])
+            nc.vector.tensor_tensor(out=result_tile(i), in0=out_banks.pop(i)[:], in1=bias_rows(2), op=ALU.add)
+            nc.sync.dma_start(out=out_view(i), in_=result_tile(i))
 
         def hand_over(i):
-            r, n = divmod(i + 6, 2)
-            if n == 0:
-                sums[r] = work.tile([P, 4, D_OUT], F32, name="sums", tag="sums", bufs=2, align_bytes=64)
-            nc.scalar.copy(out=sums[r][:, 2 * n : 2 * n + 2, :], in_=out_banks.pop(i)[:])
+            sums = keep.tile([P, 2, D_OUT], F32, name="sums%d" % i, align_bytes=64)
+            nc.scalar.copy(out=sums[:], in_=out_banks.pop(i)[:])
+            return sums
 
-        def finish_handed(r):
-            result = h_half(r + 1).bitcast(F32).rearrange("p (n o) -> p n o", o=D_OUT)
-            nc.gpsimd.tensor_tensor(out=result, in0=sums.pop(r)[:], in1=bias_rows(4), op=ALU.add)
-            for n in range(2):
-                nc.sync.dma_start(out=out_view(2 * r - 6 + n), in_=result[:, 2 * n : 2 * n + 2, :])
+        def finish_handed(i, sums, place):
+            result = values_at(place).bitcast(F32).rearrange("p (n o) -> p n o", o=D_OUT)
+            nc.gpsimd.tensor_tensor(out=result, in0=sums[:], in1=bias_rows(2), op=ALU.add)
+            nc.sync.dma_start(out=out_view(i), in_=result)
 
         def turn_a(half):
             rows = [a_sb[:, (2 * half + n) * D : (2 * half + n + 1) * D] for n in range(2)]
@@ -288,27 +297,34 @@ def tile_replaced_compose_lora_pa_t_w4_kernel(
                 in_=a_values[:, half * 2 * D : (half + 1) * 2 * D],
             )
 
-        nc.vector.tensor_copy(out=first[:, 0:D], in_=xb[:, 0:D].bitcast(FP8))
-        cast_x(nc.scalar.copy, 0, first[:, 0:PAIR_COLS], D)
-        cast_first(nc.vector.tensor_copy, 1)
-        cast_first(nc.gpsimd.tensor_copy, 2)
-        cast_first(nc.scalar.copy, 3)
-        first_tiles = [turn([cast[0][:, j * D : (j + 1) * D]], "out") for j in range(2)]
-        turn_x(1)
-        turn_a(0)
-        turn_a(1)
-        turn_x(2)
-        turn_x(3, "out")
+        def make_pair_h(i):
+            for j in range(2):
+                make_h(i, j)
+            for j in range(2):
+                round_h(i, j)
+
+        cast_cols(nc.vector.tensor_copy, 0, D)
+        cast_cols(nc.scalar.copy, D, 2 * D)
+        cast_pair(nc.vector.tensor_copy, 1)
+        cast_pair(nc.gpsimd.tensor_copy, 2)
+        cast_pair(nc.scalar.copy, 3)
         nc.scalar.activation(
             out=coef_row[0:1, :].rearrange("p (n q) -> p n q", q=PACK),
             in_=lw_row[:].unsqueeze(2).to_broadcast([1, ADAPTERS, PACK]),
             func=ACT.Copy,
             scale=ALPHA_OVER_RANK,
         )
+        first_tiles = [turn([wide[:, j * D : (j + 1) * D]], "out") for j in range(2)]
+        turn_x(1)
+        turn_a(0)
+        turn_a(1)
         coef_bank = bank("h", [P, P])
         nc.tensor.transpose(coef_bank[:], coef_row[:], ident[:])
+        turn_x(2)
+        turn_x(3, "out")
         nc.scalar.copy(out=coef[:], in_=coef_bank[:, 0:1])
-        cast_first(nc.scalar.copy, 4)
+        cast_cols(nc.scalar.copy, 8 * D, 9 * D)
+        cast_next(nc.scalar.copy, 2 * PAIR_COLS)
         for j in range(2):
             scale_into(values_at(x_place(0))[:, j * D : (j + 1) * D], first_tiles[j])
         scale_x(1)
@@ -316,37 +332,40 @@ def tile_replaced_compose_lora_pa_t_w4_kernel(
         quantise_quarters(1, 2, 2)
         quantise_a(1)
 
-        for r in range(1, ROUNDS):
-            even_h, odd_h = 2 * r - 2, 2 * r - 1
-            outs = [i for i in (2 * r - 5, 2 * r - 4) if i >= 0]
-            if r == 2:
-                quantise_quarters(r, 0, 1)
-            elif r > 2:
-                if r + 1 < ROUNDS:
-                    cast_row(nc.vector.tensor_copy, 2 * r + 2, 1)
-                quantise_quarters(r, 0, 2)
+        for r in range(1, ROUNDS - 1):
+            quota = LONG_COLS if r in LONG_ROUNDS else SHORT_COLS
+            if r == 3:
+                nc.vector.quantize_mx(out=b_codes[:].bitcast(FP8X4), scales=b_scales[:], in_=b_values[:])
             if r > 1:
+                quantise_quarters(r, 0, min(r - 1, 2))
                 quantise_quarters(r, 2, 2)
             if r == 1:
-                cast_x(nc.gpsimd.tensor_copy, 5, a_values[:])
-            elif r == 2:
-                nc.vector.quantize_mx(out=b_codes[:].bitcast(FP8X4), scales=b_scales[:], in_=b_values[:])
-                scale_before(2 * r + 3, b_values[:])
-            elif r + 1 < ROUNDS:
-                scale_before(2 * r + 3, h_half(r)[:, 0:PAIR_COLS])
-            scale_x(2 * r)
-            if r in SHARED_ROUNDS:
-                copy_words(values_at(x_place(2 * r + 1)), x_banks.pop(2 * r + 1))
+                cast_aside(9, 3, a_values[:, D:])
+            elif r + 1 in LONG_ROUNDS:
+                cast_aside(2 * GPSIMD_CAST[r], 4, h_half(r))
+                aside[GPSIMD_CAST[r]] = h_half(r)[:, 0:PAIR_COLS]
             else:
+                scale_before(2 * r + 2, h_half(r)[:, 0:PAIR_COLS])
+            if r in SHARED_ROUNDS:
                 scale_x(2 * r + 1)
-            if r > 2 and r + 1 < ROUNDS:
-                cast_row(nc.scalar.copy, 2 * r + 2, 0)
-            if len(outs) == 2:
-                make_out(outs[0])
-            make_h(even_h, 0)
-            make_h(even_h, 1)
-            round_h(even_h, 0)
-            round_h(even_h, 1)
+                copy_words(values_at(x_place(2 * r)), x_banks.pop(2 * r))
+            else:
+                scale_x(2 * r)
+                scale_x(2 * r + 1)
+            if r > 1:
+                cast_next(nc.scalar.copy, quota[0])
+            if r == 3:
+                make_out(0)
+            if r > 2:
+                make_out(2 * r - 5)
+            make_pair_h(2 * r - 2)
+            if r == 2:
+                spread = bank("out", [P, PACK, P])
+                for t in range(PACK):
+                    nc.tensor.transpose(spread[:, t, :], scale_col[:, t : t + 1].to_broadcast([P, P]), ident[:])
+                nc.scalar.copy(
+                    out=scale_rows[:].rearrange("p (m t) -> p m t", t=PACK), in_=spread[:].rearrange("p t m -> p m t")
+                )
             if r == 1:
                 nc.scalar.activation(
                     out=b_values[:].rearrange("p (o t) -> p o t", t=PACK),
@@ -354,58 +373,61 @@ def tile_replaced_compose_lora_pa_t_w4_kernel(
                     func=ACT.Copy,
                     scale=coef[:],
                 )
-            if outs:
-                make_out(outs[-1])
-            if r + 2 < ROUNDS:
-                cast_raw(2 * r + 5)
-            for i in (2 * r - 6, 2 * r - 5):
-                if i >= 0:
-                    (hand_over if i in HANDED else finish)(i)
-            make_h(odd_h, 0)
-            make_h(odd_h, 1)
-            if r == 1:
-                spread = bank("out", [P, PACK, P])
-                for t in range(PACK):
-                    nc.tensor.transpose(spread[:, t, :], scale_col[:, t : t + 1].to_broadcast([P, P]), ident[:])
-                nc.scalar.copy(
-                    out=scale_rows[:].rearrange("p (m t) -> p m t", t=PACK), in_=spread[:].rearrange("p t m -> p m t")
-                )
-            round_h(odd_h, 0)
-            round_h(odd_h, 1)
-            if r + 1 < ROUNDS:
-                turn_x(2 * r + 2)
-                turn_x(2 * r + 3)
+            if r > 2:
+                make_out(2 * r - 4)
+            if r > 1:
+                cast_next(nc.scalar.copy, quota[1])
+            if r > 2:
+                finish(2 * r - 6)
+                finish(2 * r - 5)
+            if r == ROUNDS - 2:
+                late_sums = hand_over(2 * r - 4)
+            make_pair_h(2 * r - 1)
+            for i in (2 * r + 3, 2 * r + 2) if r + 1 in SHARED_ROUNDS else (2 * r + 2, 2 * r + 3):
+                turn_x(i)
 
-        r = ROUNDS
-        quantise_quarters(r, 2, 1)
+        r = ROUNDS - 1
+        quantise_quarters(r, 2, 2)
         quantise_quarters(r, 0, 2)
-        quantise_quarters(r, 3, 1)
+        finish_handed(LAST - 7, late_sums, x_place(LAST - 3))
+        copy_words(values_at(x_place(LAST - 1)), x_banks.pop(LAST - 1))
+        scale_x(LAST)
+        make_h(LAST - 3, 0)
+        make_h(LAST - 3, 1)
+        make_h(LAST - 2, 0)
+        round_h(LAST - 3, 0)
+        make_out(LAST - 6)
+        make_h(LAST - 2, 1)
+        round_h(LAST - 3, 1)
+        round_h(LAST - 2, 0)
+        round_h(LAST - 2, 1)
+        make_out(LAST - 5)
+        quantise_quarters(*x_place(LAST - 1), 1)
+        quantise_quarters(*h_place(LAST - 4), 1)
+        quantise_quarters(*x_place(LAST), 1)
+        finish(LAST - 6)
+        make_pair_h(LAST - 1)
+        quantise_quarters(*h_place(LAST - 3), 1)
         finish(LAST - 5)
-        make_h(LAST - 1, 0)
-        make_h(LAST - 1, 1)
-        round_h(LAST - 1, 0)
-        round_h(LAST - 1, 1)
         make_out(LAST - 4)
-        make_h(LAST, 0)
-        make_h(LAST, 1)
-        round_h(LAST, 0)
-        round_h(LAST, 1)
-        quantise_quarters(r + 1, 1, 1)
-        finish(LAST - 4)
+        make_pair_h(LAST)
+        quantise_quarters(*h_place(LAST - 2), 1)
         make_out(LAST - 3)
+        finish(LAST - 4)
         make_out(LAST - 2)
+        quantise_quarters(*h_place(LAST - 1), 1)
         finish(LAST - 3)
-        quantise_quarters(r + 1, 0, 1)
-        finish(LAST - 2)
         make_out(LAST - 1)
-        last_result = result_tile()
+        finish(LAST - 2)
+        last_result = result_tile(LAST)
         last_banks = []
+        r, quarter = h_place(LAST)
         for j in range(2):
-            quantise(r + 2, PAIR_WORDS + j * P, P)
+            quantise(r, quarter * PAIR_WORDS + j * P, P)
+        for j in range(2):
             last_banks.append(bank("h", [P, D_OUT]))
             out_tile(LAST, j, last_banks[j][:])
-            if j == 0:
-                finish(LAST - 1)
+        finish(LAST - 1)
         for j in range(2):
             nc.vector.tensor_tensor(out=last_result[:, j, :], in0=last_banks[j][:], in1=bias_sb[:], op=ALU.add)
             nc.sync.dma_start(out=out_view(LAST)[:, j, :], in_=last_result[:, j, :])

@@ -31,10 +31,11 @@ ROUNDS = PAIRS // 2
 PAIR_COLS = 2 * D
 PAIR_WORDS = PAIR_COLS // PACK
 ROUND_TILES = 5
-LONG_ROUNDS = (3, 9)
+LONG_ROUNDS = (3, 8, 12)
 SHARED_ROUNDS = [r for r in range(3, ROUNDS) if r not in LONG_ROUNDS]
-GPSIMD_CAST = {2: 8, 8: 18}
-SHORT_COLS, LONG_COLS = (512, 768), (2048, 1536)
+GPSIMD_ROWS = dict([(1, (10, 3)), (2, (18, 4))] + [(r - 1, (4 * r, 4)) for r in LONG_ROUNDS[1:]] + [(r, (4 * r + 10, 1)) for r in LONG_ROUNDS])
+HEAD_ROWS = 10
+SHORT_COLS, LONG_COLS = (512, 512), (1536, 1024)
 
 
 def tile_replaced_compose_lora_pa_t_w4_kernel(
@@ -79,12 +80,13 @@ def tile_replaced_compose_lora_pa_t_w4_kernel(
         load_x(0, 2)
         load_x(2, 2)
         nc.sync.dma_start(out=scale_col[:], in_=x_scale.rearrange("a b (p t) -> p (a b t)", t=PACK))
-        nc.sync.dma_start(out=a_sb[:, 0 : 2 * D], in_=a_rows[:, 0 : 2 * D])
         load_x(4, 4)
+        nc.sync.dma_start(out=a_sb[:, 0 : 2 * D], in_=a_rows[:, 0 : 2 * D])
+        load_x(8, 2)
         nc.sync.dma_start(out=a_sb[:, 2 * D :], in_=a_rows[:, 2 * D :])
-        load_x(8, 4)
         nc.sync.dma_start(out=lw_row[:], in_=lora_weights.unsqueeze(0))
-        load_x(12, 4)
+        load_x(10, 6)
+        load_x(16, 6)
         b_rows = lora_B.rearrange("n o r -> n (o r)")
         b_run = RANK * D_OUT - (RANK - PACK)
         for q in range(PACK):
@@ -92,13 +94,12 @@ def tile_replaced_compose_lora_pa_t_w4_kernel(
                 out=b_sb[:].rearrange("p o r -> p (o r)")[q:P:PACK, 0:b_run],
                 in_=b_rows[:, PACK * q : PACK * q + b_run],
             )
-        load_x(16, 4)
+        load_x(22, 2)
         nc.sync.dma_start(out=w_sb[:], in_=W_words[0])
         for q in range(4):
             nc.sync.dma_start(
                 out=w_sc[32 * q : 32 * q + 4, :].bitcast(I32), in_=W_scales[0, 4 * q : 4 * q + 4, :].bitcast(I32)
             )
-        load_x(20, 4)
         nc.sync.dma_start(out=bias_sb[:], in_=bias.partition_broadcast(P))
         load_x(3 * CHUNK_ROWS, CHUNK_ROWS)
         for c in range(4, CHUNKS):
@@ -113,9 +114,9 @@ def tile_replaced_compose_lora_pa_t_w4_kernel(
 
         scale_rows = keep.tile([P, D], F32, name="scale_rows", align_bytes=64)
         moved, x_banks, h_banks, out_banks = {}, {}, {}, {}
-        aside = {}
         cast_ends = [0]
-        left = [i for i in range(6, PAIRS) if i // 2 * 2 not in [GPSIMD_CAST[r] for r in GPSIMD_CAST]]
+        aside = [row + n for row, rows in [GPSIMD_ROWS[r] for r in GPSIMD_ROWS] for n in range(rows)]
+        left = [row for row in range(HEAD_ROWS, ROWS) if row not in aside]
         round_values, round_codes = {}, {}
 
         def x_place(i):
@@ -145,39 +146,40 @@ def tile_replaced_compose_lora_pa_t_w4_kernel(
         def cast_pair(copy, i):
             cast_cols(copy, i * PAIR_COLS, (i + 1) * PAIR_COLS)
 
-        def cast_next(copy, cols):
+        def cast_next(cols):
             lo = cast_ends[-1]
-            hi = min(lo + cols, len(left) * PAIR_COLS)
+            hi = min(lo + cols, len(left) * D)
             while lo < hi:
-                n = lo // PAIR_COLS
+                n = lo // D
                 run = 1
                 while n + run < len(left) and left[n + run] == left[n] + run:
                     run = run + 1
-                end = min(hi, (n + run) * PAIR_COLS)
-                shift = (left[n] - n) * PAIR_COLS
-                cast_cols(copy, lo + shift, end + shift)
+                end = min(hi, (n + run) * D)
+                shift = (left[n] - n) * D
+                cast_cols(nc.scalar.copy, lo + shift, end + shift)
                 lo = end
             cast_ends.append(hi)
 
         def cast_aside(row, rows, dst):
             nc.gpsimd.tensor_copy(out=dst, in_=xb[:, row * D : (row + rows) * D].bitcast(FP8))
             for n in range(rows):
-                moved[row + n] = dst[:, n * D : (n + 1) * D]
+                moved[row + n] = dst, n
 
-        def x_row(row):
-            i = row // 2
-            assert row in moved or i not in left or (left.index(i) + 1) * PAIR_COLS <= cast_ends[-1], row
-            return moved.get(row, wide[:, row * D : (row + 1) * D])
+        def x_row(row, rows=1):
+            assert row in moved or row not in left or (left.index(row) + rows) * D <= cast_ends[-1], row
+            if row in moved:
+                dst, n = moved[row]
+                return dst[:, n * D : (n + rows) * D]
+            return wide[:, row * D : (row + rows) * D]
 
         def scale_before(i, dst):
             nc.gpsimd.tensor_tensor(
                 out=dst.rearrange("p (j d) -> p j d", j=2),
-                in0=aside.get(i, wide[:, i * PAIR_COLS : (i + 1) * PAIR_COLS]).rearrange("p (j d) -> p j d", j=2),
+                in0=x_row(2 * i, 2).rearrange("p (j d) -> p j d", j=2),
                 in1=scale_rows[:].unsqueeze(1).to_broadcast([P, 2, D]),
                 op=ALU.mult,
             )
-            x_row(2 * i)
-            moved[2 * i], moved[2 * i + 1] = dst[:, 0:D], dst[:, D:]
+            moved[2 * i], moved[2 * i + 1] = (dst, 0), (dst, 1)
 
         def h_half(r):
             return round_values[r][:, 0 : 2 * PAIR_COLS]
@@ -303,28 +305,31 @@ def tile_replaced_compose_lora_pa_t_w4_kernel(
             for j in range(2):
                 round_h(i, j)
 
-        cast_cols(nc.vector.tensor_copy, 0, D)
-        cast_cols(nc.scalar.copy, D, 2 * D)
+        cast_cols(nc.vector.tensor_copy, 0, D // 2)
+        cast_cols(nc.scalar.copy, D // 2, D)
+        cast_cols(nc.vector.tensor_copy, D, D + D // 2)
+        cast_cols(nc.scalar.copy, D + D // 2, 2 * D)
         cast_pair(nc.vector.tensor_copy, 1)
-        cast_pair(nc.gpsimd.tensor_copy, 2)
-        cast_pair(nc.scalar.copy, 3)
+        cast_cols(nc.gpsimd.tensor_copy, 4 * D, 7 * D)
+        cast_cols(nc.scalar.copy, 7 * D, 8 * D)
+        cast_pair(nc.scalar.copy, 4)
+        first_tiles = [turn([wide[:, j * D : (j + 1) * D]], "out") for j in range(2)]
+        turn_x(1)
+        turn_a(0)
+        turn_a(1)
         nc.scalar.activation(
             out=coef_row[0:1, :].rearrange("p (n q) -> p n q", q=PACK),
             in_=lw_row[:].unsqueeze(2).to_broadcast([1, ADAPTERS, PACK]),
             func=ACT.Copy,
             scale=ALPHA_OVER_RANK,
         )
-        first_tiles = [turn([wide[:, j * D : (j + 1) * D]], "out") for j in range(2)]
-        turn_x(1)
-        turn_a(0)
-        turn_a(1)
-        coef_bank = bank("h", [P, P])
-        nc.tensor.transpose(coef_bank[:], coef_row[:], ident[:])
         turn_x(2)
         turn_x(3, "out")
+        coef_bank = bank("h", [P, P])
+        nc.tensor.transpose(coef_bank[:], coef_row[:], ident[:])
+        cast_next(3 * D)
         nc.scalar.copy(out=coef[:], in_=coef_bank[:, 0:1])
-        cast_cols(nc.scalar.copy, 8 * D, 9 * D)
-        cast_next(nc.scalar.copy, 2 * PAIR_COLS)
+        cast_next(1 * D)
         for j in range(2):
             scale_into(values_at(x_place(0))[:, j * D : (j + 1) * D], first_tiles[j])
         scale_x(1)
@@ -339,21 +344,26 @@ def tile_replaced_compose_lora_pa_t_w4_kernel(
             if r > 1:
                 quantise_quarters(r, 0, min(r - 1, 2))
                 quantise_quarters(r, 2, 2)
-            if r == 1:
-                cast_aside(9, 3, a_values[:, D:])
-            elif r + 1 in LONG_ROUNDS:
-                cast_aside(2 * GPSIMD_CAST[r], 4, h_half(r))
-                aside[GPSIMD_CAST[r]] = h_half(r)[:, 0:PAIR_COLS]
-            else:
+            if r + 1 in SHARED_ROUNDS:
                 scale_before(2 * r + 2, h_half(r)[:, 0:PAIR_COLS])
+            if r in GPSIMD_ROWS:
+                row, rows = GPSIMD_ROWS[r]
+                cast_aside(row, rows, (a_values[:] if r == 1 else h_half(r))[:, (4 - rows) * D :])
             if r in SHARED_ROUNDS:
                 scale_x(2 * r + 1)
                 copy_words(values_at(x_place(2 * r)), x_banks.pop(2 * r))
             else:
                 scale_x(2 * r)
                 scale_x(2 * r + 1)
-            if r > 1:
-                cast_next(nc.scalar.copy, quota[0])
+            if r == 2:
+                nc.scalar.activation(
+                    out=b_values[:].rearrange("p (o t) -> p o t", t=PACK),
+                    in_=b_sb[:, :, 0:PACK],
+                    func=ACT.Copy,
+                    scale=coef[:],
+                )
+            if r > 2:
+                cast_next(quota[0])
             if r == 3:
                 make_out(0)
             if r > 2:
@@ -366,17 +376,9 @@ def tile_replaced_compose_lora_pa_t_w4_kernel(
                 nc.scalar.copy(
                     out=scale_rows[:].rearrange("p (m t) -> p m t", t=PACK), in_=spread[:].rearrange("p t m -> p m t")
                 )
-            if r == 1:
-                nc.scalar.activation(
-                    out=b_values[:].rearrange("p (o t) -> p o t", t=PACK),
-                    in_=b_sb[:, :, 0:PACK],
-                    func=ACT.Copy,
-                    scale=coef[:],
-                )
             if r > 2:
                 make_out(2 * r - 4)
-            if r > 1:
-                cast_next(nc.scalar.copy, quota[1])
+            cast_next(quota[1])
             if r > 2:
                 finish(2 * r - 6)
                 finish(2 * r - 5)

@@ -376,7 +376,7 @@ def tile_replaced_compose_lora_pa_t_w4_kernel(
                 nc.scalar.copy(
                     out=scale_rows[:].rearrange("p (m t) -> p m t", t=PACK), in_=spread[:].rearrange("p t m -> p m t")
                 )
-            if r > 2:
+            if r in SHARED_ROUNDS:
                 make_out(2 * r - 4)
             cast_next(quota[1])
             if r > 2:
@@ -387,6 +387,8 @@ def tile_replaced_compose_lora_pa_t_w4_kernel(
             make_pair_h(2 * r - 1)
             for i in (2 * r + 3, 2 * r + 2) if r + 1 in SHARED_ROUNDS else (2 * r + 2, 2 * r + 3):
                 turn_x(i)
+            if r in LONG_ROUNDS:
+                make_out(2 * r - 4)
 
         r = ROUNDS - 1
         quantise_quarters(r, 2, 2)

@@ -65,7 +65,11 @@ def tile_replaced_compose_lora_pa_t_w4_kernel(
         b_sb = keep.tile([P, D_OUT, RANK], BF16, name="b_sb", align_bytes=64)
         w_sb = keep.tile([P, 2 * D_OUT], U8, name="w_sb", align_bytes=64)
         w_sc = keep.tile([P, D_OUT], U8, name="w_sc", align_bytes=64)
-        bias_sb = keep.tile([P, D_OUT], BF16, name="bias_sb", align_bytes=64)
+        bias_sb = keep.tile([P, D_OUT], F32, name="bias_sb", align_bytes=64)
+        bias_row = keep.tile([P, D_OUT], BF16, name="bias_row", align_bytes=64)
+        nc.vector.memset(bias_row[:], 0.0)
+        ones = keep.tile([P, P], BF16, name="ones", align_bytes=64)
+        nc.vector.memset(ones[:], 1.0)
         lw_row = keep.tile([1, ADAPTERS], BF16, name="lw_row")
         coef_row = keep.tile([P, P], F32, name="coef_row")
         nc.vector.memset(coef_row[:], 0.0)
@@ -87,6 +91,7 @@ def tile_replaced_compose_lora_pa_t_w4_kernel(
         nc.sync.dma_start(out=lw_row[:], in_=lora_weights.unsqueeze(0))
         load_x(10, 6)
         load_x(16, 6)
+        nc.sync.dma_start(out=bias_row[0:1, :], in_=bias.unsqueeze(0))
         b_rows = lora_B.rearrange("n o r -> n (o r)")
         b_run = RANK * D_OUT - (RANK - PACK)
         for q in range(PACK):
@@ -100,7 +105,6 @@ def tile_replaced_compose_lora_pa_t_w4_kernel(
             nc.sync.dma_start(
                 out=w_sc[32 * q : 32 * q + 4, :].bitcast(I32), in_=W_scales[0, 4 * q : 4 * q + 4, :].bitcast(I32)
             )
-        nc.sync.dma_start(out=bias_sb[:], in_=bias.partition_broadcast(P))
         load_x(3 * CHUNK_ROWS, CHUNK_ROWS)
         for c in range(4, CHUNKS):
             load_x(c * CHUNK_ROWS, CHUNK_ROWS)
@@ -120,10 +124,10 @@ def tile_replaced_compose_lora_pa_t_w4_kernel(
         round_values, round_codes = {}, {}
 
         def x_place(i):
-            return i // 2 + 1, 2 + i % 2
+            return i // 2 + 1, 1 + i % 2
 
         def h_place(i):
-            return i // 2 + 2 + i % 2, i % 2
+            return i // 2 + 2 + i % 2, 3 * (i % 2)
 
         def turn(rows, kind):
             turned = bank(kind, [P, 2, len(rows), P])
@@ -334,7 +338,7 @@ def tile_replaced_compose_lora_pa_t_w4_kernel(
             scale_into(values_at(x_place(0))[:, j * D : (j + 1) * D], first_tiles[j])
         scale_x(1)
         quantise_a(0)
-        quantise_quarters(1, 2, 2)
+        quantise_quarters(1, 1, 2)
         quantise_a(1)
 
         for r in range(1, ROUNDS - 1):
@@ -342,8 +346,8 @@ def tile_replaced_compose_lora_pa_t_w4_kernel(
             if r == 3:
                 nc.vector.quantize_mx(out=b_codes[:].bitcast(FP8X4), scales=b_scales[:], in_=b_values[:])
             if r > 1:
-                quantise_quarters(r, 0, min(r - 1, 2))
-                quantise_quarters(r, 2, 2)
+                quantise_quarters(r, 0, 2)
+                quantise_quarters(r, 2, min(r - 1, 2))
             if r + 1 in SHARED_ROUNDS:
                 scale_before(2 * r + 2, h_half(r)[:, 0:PAIR_COLS])
             if r in GPSIMD_ROWS:
@@ -364,18 +368,21 @@ def tile_replaced_compose_lora_pa_t_w4_kernel(
                 )
             if r > 2:
                 cast_next(quota[0])
+            make_pair_h(2 * r - 2)
             if r == 3:
                 make_out(0)
             if r > 2:
                 make_out(2 * r - 5)
-            make_pair_h(2 * r - 2)
             if r == 2:
+                bias_bank = bank("out", [P, D_OUT])
+                nc.tensor.matmul(bias_bank[:], lhsT=ones[:], rhs=bias_row[:], start=True, stop=True)
                 spread = bank("out", [P, PACK, P])
                 for t in range(PACK):
                     nc.tensor.transpose(spread[:, t, :], scale_col[:, t : t + 1].to_broadcast([P, P]), ident[:])
                 nc.scalar.copy(
                     out=scale_rows[:].rearrange("p (m t) -> p m t", t=PACK), in_=spread[:].rearrange("p t m -> p m t")
                 )
+                nc.scalar.copy(out=bias_sb[:], in_=bias_bank[:])
             if r in SHARED_ROUNDS:
                 make_out(2 * r - 4)
             cast_next(quota[1])
@@ -391,8 +398,8 @@ def tile_replaced_compose_lora_pa_t_w4_kernel(
                 make_out(2 * r - 4)
 
         r = ROUNDS - 1
-        quantise_quarters(r, 2, 2)
         quantise_quarters(r, 0, 2)
+        quantise_quarters(r, 2, 2)
         finish_handed(LAST - 7, late_sums, x_place(LAST - 3))
         copy_words(values_at(x_place(LAST - 1)), x_banks.pop(LAST - 1))
         scale_x(LAST)

@@ -31,11 +31,11 @@ ROUNDS = PAIRS // 2
 PAIR_COLS = 2 * D
 PAIR_WORDS = PAIR_COLS // PACK
 ROUND_TILES = 5
-LONG_ROUNDS = (3, 8, 12)
+LONG_ROUNDS = (3, 9)
 SHARED_ROUNDS = [r for r in range(3, ROUNDS) if r not in LONG_ROUNDS]
 GPSIMD_ROWS = dict([(1, (10, 3)), (2, (18, 4))] + [(r - 1, (4 * r, 4)) for r in LONG_ROUNDS[1:]] + [(r, (4 * r + 10, 1)) for r in LONG_ROUNDS])
 HEAD_ROWS = 10
-SHORT_COLS, LONG_COLS = (512, 512), (1536, 1024)
+SHORT_COLS, LONG_COLS = (640, 576), (1536, 1536)
 
 
 def tile_replaced_compose_lora_pa_t_w4_kernel(
@@ -81,16 +81,16 @@ def tile_replaced_compose_lora_pa_t_w4_kernel(
             c, n = divmod(row, CHUNK_ROWS)
             nc.sync.dma_start(out=xb[:, row * D : (row + rows) * D], in_=x_rows[c][:, n * D : (n + rows) * D])
 
+        nc.sync.dma_start(out=scale_col[:], in_=x_scale.rearrange("a b (p t) -> p (a b t)", t=PACK))
         load_x(0, 2)
         load_x(2, 2)
-        nc.sync.dma_start(out=scale_col[:], in_=x_scale.rearrange("a b (p t) -> p (a b t)", t=PACK))
         load_x(4, 4)
         nc.sync.dma_start(out=a_sb[:, 0 : 2 * D], in_=a_rows[:, 0 : 2 * D])
         load_x(8, 2)
         nc.sync.dma_start(out=a_sb[:, 2 * D :], in_=a_rows[:, 2 * D :])
         nc.sync.dma_start(out=lw_row[:], in_=lora_weights.unsqueeze(0))
         load_x(10, 6)
-        load_x(16, 6)
+        load_x(16, 8)
         nc.sync.dma_start(out=bias_row[0:1, :], in_=bias.unsqueeze(0))
         b_rows = lora_B.rearrange("n o r -> n (o r)")
         b_run = RANK * D_OUT - (RANK - PACK)
@@ -99,7 +99,6 @@ def tile_replaced_compose_lora_pa_t_w4_kernel(
                 out=b_sb[:].rearrange("p o r -> p (o r)")[q:P:PACK, 0:b_run],
                 in_=b_rows[:, PACK * q : PACK * q + b_run],
             )
-        load_x(22, 2)
         nc.sync.dma_start(out=w_sb[:], in_=W_words[0])
         for q in range(4):
             nc.sync.dma_start(
@@ -342,14 +341,22 @@ def tile_replaced_compose_lora_pa_t_w4_kernel(
         quantise_a(1)
 
         for r in range(1, ROUNDS - 1):
-            quota = LONG_COLS if r in LONG_ROUNDS else SHORT_COLS
+            quota = LONG_COLS if r in LONG_ROUNDS else SHORT_COLS if r > 2 else (D, D)
             if r == 3:
-                nc.vector.quantize_mx(out=b_codes[:].bitcast(FP8X4), scales=b_scales[:], in_=b_values[:])
+                nc.vector.tensor_scalar(
+                    out=b_values[:].rearrange("p (o t) -> p o t", t=PACK),
+                    in0=b_sb[:, :, 0:PACK],
+                    scalar1=coef[:],
+                    scalar2=None,
+                    op0=ALU.mult,
+                )
             if r > 1:
                 quantise_quarters(r, 0, 2)
+                if r == 3:
+                    nc.vector.quantize_mx(out=b_codes[:].bitcast(FP8X4), scales=b_scales[:], in_=b_values[:])
                 quantise_quarters(r, 2, min(r - 1, 2))
             if r + 1 in SHARED_ROUNDS:
-                scale_before(2 * r + 2, h_half(r)[:, 0:PAIR_COLS])
+                scale_before(2 * r + 2, b_values[:] if r == 3 else h_half(r)[:, 0:PAIR_COLS])
             if r in GPSIMD_ROWS:
                 row, rows = GPSIMD_ROWS[r]
                 cast_aside(row, rows, (a_values[:] if r == 1 else h_half(r))[:, (4 - rows) * D :])
@@ -359,14 +366,7 @@ def tile_replaced_compose_lora_pa_t_w4_kernel(
             else:
                 scale_x(2 * r)
                 scale_x(2 * r + 1)
-            if r == 2:
-                nc.scalar.activation(
-                    out=b_values[:].rearrange("p (o t) -> p o t", t=PACK),
-                    in_=b_sb[:, :, 0:PACK],
-                    func=ACT.Copy,
-                    scale=coef[:],
-                )
-            if r > 2:
+            if r > 1:
                 cast_next(quota[0])
             make_pair_h(2 * r - 2)
             if r == 3:

@@ -115,8 +115,9 @@ def tile_replaced_compose_lora_pa_t_w4_kernel(
         a_values = keep.tile([P, PACK * NR], BF16, name="a_values", align_bytes=64)
         b_values = keep.tile([P, PACK * D_OUT], BF16, name="b_values", align_bytes=64)
 
-        scale_rows = keep.tile([P, D], F32, name="scale_rows", align_bytes=64)
+        scale_rows = keep.tile([P, 2, 2, D // 2], F32, name="scale_rows", align_bytes=64)
         moved, x_banks, h_banks, out_banks = {}, {}, {}, {}
+        sorted_words = {}
         cast_ends = [0]
         aside = [row + n for row, rows in [GPSIMD_ROWS[r] for r in GPSIMD_ROWS] for n in range(rows)]
         left = [row for row in range(HEAD_ROWS, ROWS) if row not in aside]
@@ -177,17 +178,23 @@ def tile_replaced_compose_lora_pa_t_w4_kernel(
 
         def scale_before(i, dst):
             nc.gpsimd.tensor_tensor(
-                out=dst.rearrange("p (j d) -> p j d", j=2),
-                in0=x_row(2 * i, 2).rearrange("p (j d) -> p j d", j=2),
-                in1=scale_rows[:].unsqueeze(1).to_broadcast([P, 2, D]),
+                out=dst.rearrange("p (u n e) -> p u n e", u=2, e=2),
+                in0=x_row(2 * i, 2).rearrange("p (n u e) -> p u n e", u=2, e=2),
+                in1=scale_rows[:].rearrange("p u j (m e) -> p u (j m) e", e=2),
                 op=ALU.mult,
             )
-            moved[2 * i], moved[2 * i + 1] = (dst, 0), (dst, 1)
+            sorted_words[i] = dst.bitcast(F32).rearrange("p (u j m) -> p u j m", u=2, j=2)
 
         def h_half(r):
             return round_values[r][:, 0 : 2 * PAIR_COLS]
 
         def turn_x(i, kind="turn"):
+            if i in sorted_words:
+                x_banks[i] = bank(kind, [P, 2, 2, P])
+                for j in range(2):
+                    for u in range(2):
+                        nc.tensor.transpose(x_banks[i][:, u, j, :], sorted_words[i][:, u, j, :], ident[:])
+                return
             x_banks[i] = turn([x_row(2 * i), x_row(2 * i + 1)], kind)
 
         def copy_words(values, turned):
@@ -353,6 +360,7 @@ def tile_replaced_compose_lora_pa_t_w4_kernel(
             if r > 1:
                 quantise_quarters(r, 0, 2)
                 if r == 3:
+                    nc.vector.tensor_copy(out=scale_rows[:, :, 1, :], in_=scale_rows[:, :, 0, :])
                     nc.vector.quantize_mx(out=b_codes[:].bitcast(FP8X4), scales=b_scales[:], in_=b_values[:])
                 quantise_quarters(r, 2, min(r - 1, 2))
             if r + 1 in SHARED_ROUNDS:
@@ -380,7 +388,8 @@ def tile_replaced_compose_lora_pa_t_w4_kernel(
                 for t in range(PACK):
                     nc.tensor.transpose(spread[:, t, :], scale_col[:, t : t + 1].to_broadcast([P, P]), ident[:])
                 nc.scalar.copy(
-                    out=scale_rows[:].rearrange("p (m t) -> p m t", t=PACK), in_=spread[:].rearrange("p t m -> p m t")
+                    out=scale_rows[:, :, 0, :].rearrange("p u (m e) -> p u m e", e=2),
+                    in_=spread[:].rearrange("p (u e) m -> p u m e", e=2),
                 )
                 nc.scalar.copy(out=bias_sb[:], in_=bias_bank[:])
             if r in SHARED_ROUNDS:

@@ -35,7 +35,7 @@ LONG_ROUNDS = (3, 9)
 SHARED_ROUNDS = [r for r in range(3, ROUNDS) if r not in LONG_ROUNDS]
 GPSIMD_ROWS = dict([(1, (10, 3)), (2, (18, 4))] + [(r - 1, (4 * r, 4)) for r in LONG_ROUNDS[1:]] + [(r, (4 * r + 10, 1)) for r in LONG_ROUNDS])
 HEAD_ROWS = 10
-SHORT_COLS, LONG_COLS = (640, 576), (1536, 1536)
+SHORT_COLS, LONG_COLS = (0, 1280), (1536, 1536)
 
 
 def tile_replaced_compose_lora_pa_t_w4_kernel(
@@ -127,7 +127,7 @@ def tile_replaced_compose_lora_pa_t_w4_kernel(
             return i // 2 + 1, 1 + i % 2
 
         def h_place(i):
-            return i // 2 + 2 + i % 2, 3 * (i % 2)
+            return (2, 3) if i == 0 else (i // 2 + 2 + i % 2, 3 * (i % 2))
 
         def turn(rows, kind):
             turned = bank(kind, [P, 2, len(rows), P])
@@ -348,7 +348,7 @@ def tile_replaced_compose_lora_pa_t_w4_kernel(
         quantise_a(1)
 
         for r in range(1, ROUNDS - 1):
-            quota = LONG_COLS if r in LONG_ROUNDS else SHORT_COLS if r > 2 else (D, D)
+            quota = LONG_COLS if r in LONG_ROUNDS else SHORT_COLS if r > 2 else (D, D * (2 - r))
             if r == 3:
                 nc.vector.tensor_scalar(
                     out=b_values[:].rearrange("p (o t) -> p o t", t=PACK),
@@ -357,11 +357,15 @@ def tile_replaced_compose_lora_pa_t_w4_kernel(
                     scalar2=None,
                     op0=ALU.mult,
                 )
-            if r > 1:
+            if r == 2:
+                quantise_quarters(r, 1, 1)
+            if r == 3:
+                quantise_quarters(*h_place(0), 1)
+            if r > 2:
                 quantise_quarters(r, 0, 2)
                 if r == 3:
-                    nc.vector.tensor_copy(out=scale_rows[:, :, 1, :], in_=scale_rows[:, :, 0, :])
                     nc.vector.quantize_mx(out=b_codes[:].bitcast(FP8X4), scales=b_scales[:], in_=b_values[:])
+            if r > 1:
                 quantise_quarters(r, 2, min(r - 1, 2))
             if r + 1 in SHARED_ROUNDS:
                 scale_before(2 * r + 2, b_values[:] if r == 3 else h_half(r)[:, 0:PAIR_COLS])
@@ -392,6 +396,7 @@ def tile_replaced_compose_lora_pa_t_w4_kernel(
                     in_=spread[:].rearrange("p (u e) m -> p u m e", e=2),
                 )
                 nc.scalar.copy(out=bias_sb[:], in_=bias_bank[:])
+                nc.scalar.copy(out=scale_rows[:, :, 1, :], in_=scale_rows[:, :, 0, :])
             if r in SHARED_ROUNDS:
                 make_out(2 * r - 4)
             cast_next(quota[1])
@@ -423,8 +428,7 @@ def tile_replaced_compose_lora_pa_t_w4_kernel(
         round_h(LAST - 2, 1)
         make_out(LAST - 5)
         quantise_quarters(*x_place(LAST - 1), 1)
-        quantise_quarters(*h_place(LAST - 4), 1)
-        quantise_quarters(*x_place(LAST), 1)
+        quantise_quarters(*x_place(LAST), 2)
         finish(LAST - 6)
         make_pair_h(LAST - 1)
         quantise_quarters(*h_place(LAST - 3), 1)

from contextlib import ExitStack

import concourse.mybir as mybir
from concourse.masks import make_identity

TOKENS, D, NR, D_OUT, RANK = 8192, 512, 512, 256, 16
ADAPTERS = NR // RANK
ALPHA_OVER_RANK = 2.0
FLOPS = 2 * TOKENS * (D * NR + D * D_OUT + NR * D_OUT)

F32 = mybir.dt.float32
BF16 = mybir.dt.bfloat16
U32 = mybir.dt.uint32
I32 = mybir.dt.int32
U8 = mybir.dt.uint8
FP8 = mybir.dt.float8_e4m3fn
FP8X4 = mybir.dt.float8_e4m3fn_x4
FP4X4 = mybir.dt.float4_e2m1fn_x4
ALU = mybir.AluOpType
ACT = mybir.ActivationFunctionType

P = 128
PACK = 4
CHUNK_ROWS = 8
ROWS = TOKENS // P
CHUNKS = ROWS // CHUNK_ROWS
PAIRS = ROWS // 2
LAST = PAIRS - 1
ROUNDS = PAIRS // 2

PAIR_COLS = 2 * D
PAIR_WORDS = PAIR_COLS // PACK
ROUND_TILES = 5
LONG_ROUNDS = (3, 9)
SHARED_ROUNDS = [r for r in range(3, ROUNDS) if r not in LONG_ROUNDS]
GPSIMD_ROWS = dict([(1, (10, 3)), (2, (18, 4))] + [(r - 1, (4 * r, 4)) for r in LONG_ROUNDS[1:]] + [(r, (4 * r + 10, 1)) for r in LONG_ROUNDS])
HEAD_ROWS = 10
SHORT_COLS, LONG_COLS = (0, 1280), (1536, 1536)


def tile_replaced_compose_lora_pa_t_w4_kernel(
    tc, x_bytes, x_scale, lora_A, lora_B, W_words, W_scales, bias, lora_weights, out
):
    nc = tc.nc
    x_rows = x_bytes.rearrange("b s d -> (b s) d").rearrange("(c p n) d -> c p (n d)", p=P, n=CHUNK_ROWS)
    out_rows = out.rearrange("b s o -> (b s) o").rearrange("(c p n) o -> c p n o", p=P, n=CHUNK_ROWS)

    with ExitStack() as ctx:
        keep = ctx.enter_context(tc.tile_pool(name="keep", bufs=1))
        work = ctx.enter_context(tc.tile_pool(name="work", bufs=1))
        psum = ctx.enter_context(tc.psum_pool(name="psum", bufs=1))
        ctx.enter_context(tc.manual_schedule())

        def bank(kind, shape):
            return psum.tile(shape, F32, name=kind, tag=kind, bufs={"turn": 2, "h": 3, "out": 3}[kind])

        ident = keep.tile([P, P], F32, name="ident")
        nc.vector.memset(ident[:], 0.0)
        make_identity(nc, ident[:], nomemset=True)

        xb = keep.tile([P, ROWS * D], U8, name="xb", align_bytes=64)
        scale_col = keep.tile([P, PACK], F32, name="scale_col")
        wide = keep.tile([P, ROWS * D], BF16, name="wide", align_bytes=64)
        a_sb = keep.tile([P, PACK * D], BF16, name="a_sb", align_bytes=64)
        b_sb = keep.tile([P, D_OUT, RANK], BF16, name="b_sb", align_bytes=64)
        w_sb = keep.tile([P, 2 * D_OUT], U8, name="w_sb", align_bytes=64)
        w_sc = keep.tile([P, D_OUT], U8, name="w_sc", align_bytes=64)
        bias_sb = keep.tile([P, D_OUT], F32, name="bias_sb", align_bytes=64)
        bias_row = keep.tile([P, D_OUT], BF16, name="bias_row", align_bytes=64)
        nc.vector.memset(bias_row[:], 0.0)
        ones = keep.tile([P, P], BF16, name="ones", align_bytes=64)
        nc.vector.memset(ones[:], 1.0)
        lw_row = keep.tile([1, ADAPTERS], BF16, name="lw_row")
        coef_row = keep.tile([P, P], F32, name="coef_row")
        nc.vector.memset(coef_row[:], 0.0)
        coef = keep.tile([P, 1], F32, name="coef")
        nc.vector.memset(w_sc[:].bitcast(I32), 0)
        a_rows = lora_A.rearrange("n r d -> (n r) d").rearrange("(m t) d -> m (t d)", t=PACK)

        def load_x(row, rows):
            c, n = divmod(row, CHUNK_ROWS)
            nc.sync.dma_start(out=xb[:, row * D : (row + rows) * D], in_=x_rows[c][:, n * D : (n + rows) * D])

        nc.sync.dma_start(out=scale_col[:], in_=x_scale.rearrange("a b (p t) -> p (a b t)", t=PACK))
        load_x(0, 2)
        load_x(2, 2)
        load_x(4, 4)
        nc.sync.dma_start(out=a_sb[:, 0 : 2 * D], in_=a_rows[:, 0 : 2 * D])
        load_x(8, 2)
        nc.sync.dma_start(out=a_sb[:, 2 * D :], in_=a_rows[:, 2 * D :])
        nc.sync.dma_start(out=lw_row[:], in_=lora_weights.unsqueeze(0))
        load_x(10, 6)
        load_x(16, 8)
        nc.sync.dma_start(out=bias_row[0:1, :], in_=bias.unsqueeze(0))
        b_rows = lora_B.rearrange("n o r -> n (o r)")
        b_run = RANK * D_OUT - (RANK - PACK)
        for q in range(PACK):
            nc.sync.dma_start(
                out=b_sb[:].rearrange("p o r -> p (o r)")[q:P:PACK, 0:b_run],
                in_=b_rows[:, PACK * q : PACK * q + b_run],
            )
        nc.sync.dma_start(out=w_sb[:], in_=W_words[0])
        for q in range(4):
            nc.sync.dma_start(
                out=w_sc[32 * q : 32 * q + 4, :].bitcast(I32), in_=W_scales[0, 4 * q : 4 * q + 4, :].bitcast(I32)
            )
        load_x(3 * CHUNK_ROWS, CHUNK_ROWS)
        for c in range(4, CHUNKS):
            load_x(c * CHUNK_ROWS, CHUNK_ROWS)

        a_codes = keep.tile([P, NR], U32, name="a_codes", align_bytes=64)
        a_scales = keep.tile([P, NR], U8, name="a_scales", align_bytes=64)
        b_codes = keep.tile([P, D_OUT], U32, name="b_codes", align_bytes=64)
        b_scales = keep.tile([P, D_OUT], U8, name="b_scales", align_bytes=64)
        a_values = keep.tile([P, PACK * NR], BF16, name="a_values", align_bytes=64)
        b_values = keep.tile([P, PACK * D_OUT], BF16, name="b_values", align_bytes=64)

        scale_rows = keep.tile([P, 2, 2, D // 2], F32, name="scale_rows", align_bytes=64)
        moved, x_banks, h_banks, out_banks = {}, {}, {}, {}
        sorted_words = {}
        cast_ends = [0]
        aside = [row + n for row, rows in [GPSIMD_ROWS[r] for r in GPSIMD_ROWS] for n in range(rows)]
        left = [row for row in range(HEAD_ROWS, ROWS) if row not in aside]
        round_values, round_codes = {}, {}

        def x_place(i):
            return i // 2 + 1, 1 + i % 2

        def h_place(i):
            return (2, 3) if i == 0 else (i // 2 + 2 + i % 2, 3 * (i % 2))

        def turn(rows, kind):
            turned = bank(kind, [P, 2, len(rows), P])
            for j, row in enumerate(rows):
                for u in range(2):
                    nc.tensor.transpose(turned[:, u, j, :], row.bitcast(F32)[:, u::2], ident[:])
            return turned

        def values_at(place):
            r, quarter = place
            if r not in round_values:
                round_values[r] = work.tile(
                    [P, 4 * PAIR_COLS], BF16, name="values", tag="values", bufs=ROUND_TILES, align_bytes=64
                )
            return round_values[r][:, quarter * PAIR_COLS : (quarter + 1) * PAIR_COLS]

        def cast_cols(copy, lo, hi):
            copy(out=wide[:, lo:hi], in_=xb[:, lo:hi].bitcast(FP8))

        def cast_pair(copy, i):
            cast_cols(copy, i * PAIR_COLS, (i + 1) * PAIR_COLS)

        def cast_next(cols):
            lo = cast_ends[-1]
            hi = min(lo + cols, len(left) * D)
            while lo < hi:
                n = lo // D
                run = 1
                while n + run < len(left) and left[n + run] == left[n] + run:
                    run = run + 1
                end = min(hi, (n + run) * D)
                shift = (left[n] - n) * D
                cast_cols(nc.scalar.copy, lo + shift, end + shift)
                lo = end
            cast_ends.append(hi)

        def cast_aside(row, rows, dst):
            nc.gpsimd.tensor_copy(out=dst, in_=xb[:, row * D : (row + rows) * D].bitcast(FP8))
            for n in range(rows):
                moved[row + n] = dst, n

        def x_row(row, rows=1):
            assert row in moved or row not in left or (left.index(row) + rows) * D <= cast_ends[-1], row
            if row in moved:
                dst, n = moved[row]
                return dst[:, n * D : (n + rows) * D]
            return wide[:, row * D : (row + rows) * D]

        def scale_before(i, dst):
            nc.gpsimd.tensor_tensor(
                out=dst.rearrange("p (u n e) -> p u n e", u=2, e=2),
                in0=x_row(2 * i, 2).rearrange("p (n u e) -> p u n e", u=2, e=2),
                in1=scale_rows[:].rearrange("p u j (m e) -> p u (j m) e", e=2),
                op=ALU.mult,
            )
            sorted_words[i] = dst.bitcast(F32).rearrange("p (u j m) -> p u j m", u=2, j=2)

        def h_half(r):
            return round_values[r][:, 0 : 2 * PAIR_COLS]

        def turn_x(i, kind="turn"):
            if i in sorted_words:
                x_banks[i] = bank(kind, [P, 2, 2, P])
                for j in range(2):
                    for u in range(2):
                        nc.tensor.transpose(x_banks[i][:, u, j, :], sorted_words[i][:, u, j, :], ident[:])
                return
            x_banks[i] = turn([x_row(2 * i), x_row(2 * i + 1)], kind)

        def copy_words(values, turned):
            nc.scalar.copy(
                out=values.bitcast(F32).rearrange("p (n u) -> p n u", u=2),
                in_=turned[:].rearrange("p u j r -> p (j r) u"),
            )

        def scale_into(values, turned):
            tokens = values.shape[1] // PACK
            nc.vector.tensor_tensor(
                out=values.rearrange("p (n u e) -> p n u e", u=2, e=2),
                in0=turned[:].bitcast(BF16).rearrange("p u j (r e) -> p (j r) u e", e=2),
                in1=scale_col[:].rearrange("p (u e) -> p u e", e=2).unsqueeze(1).to_broadcast([P, tokens, 2, 2]),
                op=ALU.mult,
            )

        def scale_x(i):
            scale_into(values_at(x_place(i)), x_banks.pop(i))

        def quantise(r, lo, width):
            if r not in round_codes:
                round_codes[r] = (
                    work.tile([P, 4 * PAIR_WORDS], U32, name="codes", tag="codes", bufs=ROUND_TILES, align_bytes=64),
                    work.tile([P, 4 * PAIR_WORDS], U8, name="scales", tag="scales", bufs=ROUND_TILES, align_bytes=64),
                )
            codes, scales = round_codes[r]
            nc.vector.quantize_mx(
                out=codes[:, lo : lo + width].bitcast(FP8X4),
                scales=scales[:, lo : lo + width],
                in_=round_values[r][:, PACK * lo : PACK * (lo + width)],
            )

        def quantise_quarters(r, quarter, count):
            quantise(r, quarter * PAIR_WORDS, count * PAIR_WORDS)

        def mx(acc, stationary, moving, start, stop):
            nc.tensor.matmul_mx(
                out=acc,
                lhsT=stationary[0],
                lhsT_scale=stationary[1],
                rhs=moving[0],
                rhs_scale=moving[1],
                start=start,
                stop=stop,
            )

        def e4m3(codes, scales, lo, width):
            return codes[:, lo : lo + width].bitcast(FP8X4), scales[:, lo : lo + width]

        def x_cols(i, j, tiles):
            r, quarter = x_place(i)
            return e4m3(*round_codes[r], quarter * PAIR_WORDS + j * P, tiles * P)

        def h_cols(i, j, tiles):
            r, quarter = h_place(i)
            return e4m3(*round_codes[r], quarter * PAIR_WORDS + j * P, tiles * P)

        def make_h(i, j):
            h_banks[i, j] = bank("h", [P, PACK, P])
            for t in range(PACK):
                mx(h_banks[i, j][:, t, :], e4m3(a_codes, a_scales, t * P, P), x_cols(i, j, 1), True, True)

        def round_h(i, j):
            nc.scalar.copy(
                out=values_at(h_place(i))[:, j * NR : (j + 1) * NR].rearrange("p (r t) -> p r t", t=PACK),
                in_=h_banks.pop((i, j))[:].rearrange("p t r -> p r t"),
            )

        def out_tile(i, j, acc):
            mx(acc, h_cols(i, j, 1), e4m3(b_codes, b_scales, 0, D_OUT), True, False)
            mx(acc, x_cols(i, j, 1), (w_sb[:].bitcast(FP4X4), w_sc[:]), False, True)

        def make_out(i):
            out_banks[i] = bank("out", [P, 2, D_OUT])
            for j in range(2):
                out_tile(i, j, out_banks[i][:, j, :])

        def result_tile(i):
            return wide[:, i * PAIR_COLS : (i + 1) * PAIR_COLS].bitcast(F32).rearrange("p (n o) -> p n o", o=D_OUT)

        def out_view(i):
            c, q = divmod(i, CHUNK_ROWS // 2)
            return out_rows[c][:, 2 * q : 2 * q + 2, :]

        def bias_rows(rows):
            return bias_sb[:].unsqueeze(1).to_broadcast([P, rows, D_OUT])

        def finish(i):
            nc.vector.tensor_tensor(out=result_tile(i), in0=out_banks.pop(i)[:], in1=bias_rows(2), op=ALU.add)
            nc.sync.dma_start(out=out_view(i), in_=result_tile(i))

        def hand_over(i):
            sums = keep.tile([P, 2, D_OUT], F32, name="sums%d" % i, align_bytes=64)
            nc.scalar.copy(out=sums[:], in_=out_banks.pop(i)[:])
            return sums

        def finish_handed(i, sums, place):
            result = values_at(place).bitcast(F32).rearrange("p (n o) -> p n o", o=D_OUT)
            nc.gpsimd.tensor_tensor(out=result, in0=sums[:], in1=bias_rows(2), op=ALU.add)
            nc.sync.dma_start(out=out_view(i), in_=result)

        def turn_a(half):
            rows = [a_sb[:, (2 * half + n) * D : (2 * half + n + 1) * D] for n in range(2)]
            copy_words(a_values[:, half * 2 * D : (half + 1) * 2 * D], turn(rows, "h"))

        def quantise_a(half):
            words = slice(half * 2 * P, (half + 1) * 2 * P)
            nc.vector.quantize_mx(
                out=a_codes[:, words].bitcast(FP8X4),
                scales=a_scales[:, words],
                in_=a_values[:, half * 2 * D : (half + 1) * 2 * D],
            )

        def make_pair_h(i):
            for j in range(2):
                make_h(i, j)
            for j in range(2):
                round_h(i, j)

        cast_cols(nc.vector.tensor_copy, 0, D // 2)
        cast_cols(nc.scalar.copy, D // 2, D)
        cast_cols(nc.vector.tensor_copy, D, D + D // 2)
        cast_cols(nc.scalar.copy, D + D // 2, 2 * D)
        cast_pair(nc.vector.tensor_copy, 1)
        cast_cols(nc.gpsimd.tensor_copy, 4 * D, 7 * D)
        cast_cols(nc.scalar.copy, 7 * D, 8 * D)
        cast_pair(nc.scalar.copy, 4)
        first_tiles = [turn([wide[:, j * D : (j + 1) * D]], "out") for j in range(2)]
        turn_x(1)
        turn_a(0)
        turn_a(1)
        nc.scalar.activation(
            out=coef_row[0:1, :].rearrange("p (n q) -> p n q", q=PACK),
            in_=lw_row[:].unsqueeze(2).to_broadcast([1, ADAPTERS, PACK]),
            func=ACT.Copy,
            scale=ALPHA_OVER_RANK,
        )
        turn_x(2)
        turn_x(3, "out")
        coef_bank = bank("h", [P, P])
        nc.tensor.transpose(coef_bank[:], coef_row[:], ident[:])
        cast_next(3 * D)
        nc.scalar.copy(out=coef[:], in_=coef_bank[:, 0:1])
        cast_next(1 * D)
        for j in range(2):
            scale_into(values_at(x_place(0))[:, j * D : (j + 1) * D], first_tiles[j])
        scale_x(1)
        quantise_a(0)
        quantise_quarters(1, 1, 2)
        quantise_a(1)

        for r in range(1, ROUNDS - 1):
            quota = LONG_COLS if r in LONG_ROUNDS else SHORT_COLS if r > 2 else (D, D * (2 - r))
            if r == 3:
                nc.vector.tensor_scalar(
                    out=b_values[:].rearrange("p (o t) -> p o t", t=PACK),
                    in0=b_sb[:, :, 0:PACK],
                    scalar1=coef[:],
                    scalar2=None,
                    op0=ALU.mult,
                )
            if r == 2:
                quantise_quarters(r, 1, 1)
            if r == 3:
                quantise_quarters(*h_place(0), 1)
            if r > 2:
                quantise_quarters(r, 0, 2)
                if r == 3:
                    nc.vector.quantize_mx(out=b_codes[:].bitcast(FP8X4), scales=b_scales[:], in_=b_values[:])
            if r > 1:
                quantise_quarters(r, 2, min(r - 1, 2))
            if r + 1 in SHARED_ROUNDS:
                scale_before(2 * r + 2, b_values[:] if r == 3 else h_half(r)[:, 0:PAIR_COLS])
            if r in GPSIMD_ROWS:
                row, rows = GPSIMD_ROWS[r]
                cast_aside(row, rows, (a_values[:] if r == 1 else h_half(r))[:, (4 - rows) * D :])
            if r in SHARED_ROUNDS:
                scale_x(2 * r + 1)
                copy_words(values_at(x_place(2 * r)), x_banks.pop(2 * r))
            else:
                scale_x(2 * r)
                scale_x(2 * r + 1)
            if r > 1:
                cast_next(quota[0])
            make_pair_h(2 * r - 2)
            if r == 3:
                make_out(0)
            if r > 2:
                make_out(2 * r - 5)
            if r == 2:
                bias_bank = bank("out", [P, D_OUT])
                nc.tensor.matmul(bias_bank[:], lhsT=ones[:], rhs=bias_row[:], start=True, stop=True)
                spread = bank("out", [P, PACK, P])
                for t in range(PACK):
                    nc.tensor.transpose(spread[:, t, :], scale_col[:, t : t + 1].to_broadcast([P, P]), ident[:])
                nc.scalar.copy(
                    out=scale_rows[:, :, 0, :].rearrange("p u (m e) -> p u m e", e=2),
                    in_=spread[:].rearrange("p (u e) m -> p u m e", e=2),
                )
                nc.scalar.copy(out=bias_sb[:], in_=bias_bank[:])
                nc.scalar.copy(out=scale_rows[:, :, 1, :], in_=scale_rows[:, :, 0, :])
            if r in SHARED_ROUNDS:
                make_out(2 * r - 4)
            cast_next(quota[1])
            if r > 2:
                finish(2 * r - 6)
                finish(2 * r - 5)
            if r == ROUNDS - 2:
                late_sums = hand_over(2 * r - 4)
            make_pair_h(2 * r - 1)
            for i in (2 * r + 3, 2 * r + 2) if r + 1 in SHARED_ROUNDS else (2 * r + 2, 2 * r + 3):
                turn_x(i)
            if r in LONG_ROUNDS:
                make_out(2 * r - 4)

        r = ROUNDS - 1
        quantise_quarters(r, 0, 2)
        quantise_quarters(r, 2, 2)
        finish_handed(LAST - 7, late_sums, x_place(LAST - 3))
        copy_words(values_at(x_place(LAST - 1)), x_banks.pop(LAST - 1))
        scale_x(LAST)
        make_h(LAST - 3, 0)
        make_h(LAST - 3, 1)
        make_h(LAST - 2, 0)
        round_h(LAST - 3, 0)
        make_out(LAST - 6)
        make_h(LAST - 2, 1)
        round_h(LAST - 3, 1)
        round_h(LAST - 2, 0)
        round_h(LAST - 2, 1)
        make_out(LAST - 5)
        quantise_quarters(*x_place(LAST - 1), 1)
        quantise_quarters(*x_place(LAST), 2)
        finish(LAST - 6)
        make_pair_h(LAST - 1)
        quantise_quarters(*h_place(LAST - 3), 1)
        finish(LAST - 5)
        make_out(LAST - 4)
        make_pair_h(LAST)
        quantise_quarters(*h_place(LAST - 2), 1)
        make_out(LAST - 3)
        finish(LAST - 4)
        make_out(LAST - 2)
        quantise_quarters(*h_place(LAST - 1), 1)
        finish(LAST - 3)
        make_out(LAST - 1)
        finish(LAST - 2)
        last_result = result_tile(LAST)
        last_banks = []
        r, quarter = h_place(LAST)
        for j in range(2):
            quantise(r, quarter * PAIR_WORDS + j * P, P)
        for j in range(2):
            last_banks.append(bank("h", [P, D_OUT]))
            out_tile(LAST, j, last_banks[j][:])
        finish(LAST - 1)
        for j in range(2):
            nc.vector.tensor_tensor(out=last_result[:, j, :], in0=last_banks[j][:], in1=bias_sb[:], op=ALU.add)
            nc.sync.dma_start(out=out_view(LAST)[:, j, :], in_=last_result[:, j, :])
